import numpy as np
import ml_dtypes


def mxq(x, axis, fmt="e4m3"):
    dtype, down = {"e4m3": (ml_dtypes.float8_e4m3fn, 7), "e5m2": (ml_dtypes.float8_e5m2, 14)}[fmt]
    v = np.moveaxis(np.asarray(x, np.float32).astype(ml_dtypes.bfloat16).astype(np.float64), axis, -1)
    blocks = v.reshape(v.shape[:-1] + (-1, 32))
    amax = np.abs(blocks).max(-1, keepdims=True)
    byte = np.maximum(np.where(amax > 0, np.frexp(amax)[1] - 1 + 127, 0) - down, 1)
    scale = np.exp2(byte - 127.0)
    codes = (blocks / scale).astype(np.float32).astype(dtype).astype(np.float64)
    return np.moveaxis((codes * scale).reshape(v.shape), -1, axis)


WIDE = False


def mx_kscale(k):
    if not WIDE:
        return np.ones(k)
    levels = np.array([10, -10, 5, -5, 0])
    a = np.random.permutation(np.resize(levels, k // 512 * 4)).reshape(k // 512, 4)
    idx = np.arange(k)
    return np.exp2(a[idx // 512, idx % 128 // 32])


BF16 = ml_dtypes.bfloat16


def bf(x):
    return np.asarray(x, np.float32).astype(BF16)


def f64(x):
    return np.asarray(x).astype(np.float64)


E2M1 = np.array([0.0, 0.5, 1.0, 1.5, 2.0, 3.0, 4.0, 6.0, -0.0, -0.5, -1.0, -1.5, -2.0, -3.0, -4.0, -6.0])


def pack_weight(w, fmt):
    k, n = w.shape
    w = f64(bf(w)).reshape(k // 32, 32, n)
    amax = np.abs(w).max(1)
    if fmt == "e4m3":
        byte = np.frexp(amax)[1] - 1 + 127 - 7
    else:
        mant, ex = np.frexp(amax / 6.0)
        byte = np.where(mant > 0.5, ex, ex - 1) + 127
    byte = np.clip(np.where(amax > 0, byte, 1), 1, 254)
    scaled = (w * np.exp2(127.0 - byte)[:, None, :]).reshape(k, n).astype(np.float32)
    by_word = np.ascontiguousarray(scaled.reshape(k // 512, 128, 4, n).transpose(0, 1, 3, 2))
    if fmt == "e4m3":
        words = by_word.astype(ml_dtypes.float8_e4m3fn).view(np.uint8)
    else:
        c = by_word.astype(ml_dtypes.float4_e2m1fn).view(np.uint8) & 0xF
        words = c[..., 0::2] | (c[..., 1::2] << 4)
    return np.ascontiguousarray(words), np.ascontiguousarray(byte.astype(np.uint8).reshape(k // 512, 16, n))


def unpack_weight(words, scales, fmt):
    g, p, n, _ = words.shape
    if fmt == "e4m3":
        vals = np.ascontiguousarray(words).view(ml_dtypes.float8_e4m3fn).astype(np.float64)
    else:
        nib = np.empty((g, p, n, 4), np.uint8)
        nib[..., 0::2] = words & 0xF
        nib[..., 1::2] = words >> 4
        vals = E2M1[nib]
    vals = vals * np.repeat(np.exp2(scales.astype(np.float64) - 127.0), 8, axis=1)[..., None]
    return vals.transpose(0, 1, 3, 2).reshape(g * 512, n)


BS, BLOCK, HID, GAP, G = 4096, 512, 512, 64, 2


def elu(v):
    return np.where(v > 0.0, v, np.exp(np.minimum(v, 0.0)) - 1.0)


def setup_inputs():
    s = mx_kscale(BLOCK)
    s = s / s.max()
    x_blocks = bf((np.random.standard_normal((BS, G, BLOCK)) * s[None, None, :]).reshape(BS, G * BLOCK))
    w1 = np.random.standard_normal((G, BLOCK, HID)) / np.sqrt(BLOCK) / s[None, :, None]
    w1_words, w1_scales = pack_weight(w1.reshape(-1, HID), "e4m3")
    b1 = bf(np.random.standard_normal((G, 1, HID)) * 0.2)
    w2 = np.random.standard_normal((G, HID, BLOCK)) / np.sqrt(HID)
    w2_words, w2_scales = pack_weight(w2.reshape(-1, BLOCK), "e4m3")
    b2 = bf(np.random.standard_normal((G, 1, BLOCK)) * 0.2)
    return {"x_blocks": x_blocks,
            "w1_words": w1_words,
            "w1_scales": w1_scales,
            "b1": b1,
            "w2_words": w2_words,
            "w2_scales": w2_scales,
            "b2": b2}


def reference(x_blocks, w1_words, w1_scales, b1, w2_words, w2_scales, b2):
    y = f64(x_blocks)
    bs = y.shape[0]
    z = y.reshape(bs, -1, BLOCK).transpose(1, 0, 2)
    h = elu((mxq(z, 2, "e4m3") @ unpack_weight(w1_words, w1_scales, "e4m3").reshape(G, BLOCK, HID)) + f64(b1))
    h = (mxq(h, 2, "e4m3") @ unpack_weight(w2_words, w2_scales, "e4m3").reshape(G, HID, BLOCK)) + f64(b2)
    z = h + z
    return z.transpose(1, 0, 2).reshape(bs, -1)

@@ -1,0 +1,165 @@
+from contextlib import ExitStack
+
+import concourse.mybir as mybir
+from concourse.masks import make_identity
+
+F32 = mybir.dt.float32
+BF16 = mybir.dt.bfloat16
+I32 = mybir.dt.int32
+U32 = mybir.dt.uint32
+U8 = mybir.dt.uint8
+FP8X4 = mybir.dt.float8_e4m3fn_x4
+ALU = mybir.AluOpType
+ACT = mybir.ActivationFunctionType
+
+P = 128
+PACK = 4
+BATCH = 4096
+BLOCKS = 2
+WIDTH = 512
+TILES = BATCH // P
+GROUP = 4
+CHUNKS = TILES // GROUP
+COLS = GROUP * P
+
+FLOPS = 2 * BATCH * WIDTH * WIDTH * BLOCKS * 2
+
+
+def load_weight(nc, pool, words, scales, label):
+    codes = pool.tile([P, BLOCKS, WIDTH], U32, name=label + "_codes", align_bytes=64)
+    plane = pool.tile([P, BLOCKS, WIDTH], U8, name=label + "_plane", align_bytes=64)
+    nc.vector.memset(plane[:].rearrange("p g n -> p (g n)").bitcast(I32), 0)
+    nc.sync.dma_start(
+        out=codes[:].bitcast(I32),
+        in_=words.rearrange("g p n t -> p g (n t)").bitcast(I32),
+    )
+    for quadrant in range(4):
+        nc.sync.dma_start(
+            out=plane[32 * quadrant : 32 * quadrant + 4].bitcast(I32),
+            in_=scales[:, 4 * quadrant : 4 * quadrant + 4, :].rearrange("g r n -> r g n").bitcast(I32),
+        )
+    return codes, plane
+
+
+def tile_blockresmlp_mixerblock_pb_t_e_kernel(
+    tc, x_blocks, w1_words, w1_scales, b1, w2_words, w2_scales, b2, out
+):
+    nc = tc.nc
+    with ExitStack() as ctx:
+        const = ctx.enter_context(tc.tile_pool(name="const", bufs=1))
+        rows = ctx.enter_context(tc.tile_pool(name="rows", bufs=3))
+        work = ctx.enter_context(tc.tile_pool(name="work", bufs=2))
+        psum = ctx.enter_context(tc.psum_pool(name="psum", bufs=2))
+
+        x_view = x_blocks.rearrange("(p i) c -> p i c", i=TILES)
+        out_view = out.rearrange("(p i) c -> p i c", i=TILES)
+
+        def load_rows(chunk):
+            x_sb = rows.tile([P, GROUP, BLOCKS * WIDTH], BF16, name="x_sb")
+            nc.sync.dma_start(out=x_sb[:], in_=x_view[:, GROUP * chunk : GROUP * (chunk + 1), :])
+            return x_sb
+
+        x_first = load_rows(0)
+        w1_codes, w1_plane = load_weight(nc, const, w1_words, w1_scales, "w1")
+        w2_codes, w2_plane = load_weight(nc, const, w2_words, w2_scales, "w2")
+
+        ident = const.tile([P, P], F32, name="ident")
+        make_identity(nc, ident[:])
+
+        b1_raw = const.tile([P, BLOCKS, PACK], BF16, name="b1_raw")
+        nc.scalar.dma_start(out=b1_raw[:], in_=b1.rearrange("g o (p t) -> p (g o) t", t=PACK))
+        b1_col = const.tile([P, BLOCKS * PACK], F32, name="b1_col")
+        nc.vector.tensor_copy(out=b1_col[:], in_=b1_raw[:].rearrange("p g t -> p (g t)"))
+        b2_all = const.tile([P, BLOCKS * WIDTH], BF16, name="b2_all")
+        nc.scalar.dma_start(out=b2_all[:], in_=b2.rearrange("g o d -> (g o d)").partition_broadcast(P))
+
+        for chunk in range(CHUNKS):
+            x_sb = x_first if chunk == 0 else load_rows(chunk)
+
+            result = rows.tile([P, GROUP, BLOCKS * WIDTH], F32, name="result")
+            for a in range(GROUP):
+                nc.gpsimd.tensor_tensor(out=result[:, a, :], in0=x_sb[:, a, :], in1=b2_all[:], op=ALU.add)
+
+            for g in range(BLOCKS):
+                z_grouped = work.tile([P, GROUP, P, PACK], BF16, name="z_grouped", align_bytes=64)
+                z_words = (
+                    z_grouped[:]
+                    .rearrange("p a r k -> p (a r k)")
+                    .bitcast(F32)
+                    .rearrange("p (a r u) -> p a r u", a=GROUP, u=2)
+                )
+                for half in range(GROUP // 2):
+                    x_t = psum.tile([P, 2, 2, P], F32, name="x_t")
+                    for a in range(2):
+                        x_words = x_sb[:, 2 * half + a, :].bitcast(F32)
+                        for u in range(2):
+                            nc.tensor.transpose(
+                                x_t[:, a, u, :], x_words[:, 256 * g + u : 256 * (g + 1) : 2], ident[:]
+                            )
+                    nc.vector.tensor_copy(
+                        out=z_words[:, 2 * half : 2 * half + 2, :, :],
+                        in_=x_t[:].rearrange("p a u r -> p a r u"),
+                    )
+
+                z_codes = work.tile([P, COLS], U32, name="z_codes", align_bytes=64)
+                z_plane = work.tile([P, COLS], U8, name="z_plane", align_bytes=64)
+                nc.vector.quantize_mx(
+                    out=z_codes[:].bitcast(FP8X4),
+                    scales=z_plane[:],
+                    in_=z_grouped[:].rearrange("p a r k -> p (a r k)"),
+                )
+                v_sorted = work.tile([P, GROUP, PACK, P], F32, name="v_sorted")
+                for a in range(GROUP):
+                    v_ps = psum.tile([P, WIDTH], F32, name="v_ps")
+                    nc.tensor.matmul_mx(
+                        out=v_ps[:],
+                        lhsT=z_codes[:, P * a : P * (a + 1)].bitcast(FP8X4),
+                        lhsT_scale=z_plane[:, P * a : P * (a + 1)],
+                        rhs=w1_codes[:, g, :].bitcast(FP8X4),
+                        rhs_scale=w1_plane[:, g, :],
+                        start=True,
+                        stop=True,
+                    )
+                    nc.scalar.copy(out=v_sorted[:, a, :, :], in_=v_ps[:].rearrange("b (p t) -> b t p", t=PACK))
+
+                grown = work.tile([P, PACK, COLS], F32, name="grown")
+                kept = work.tile([P, PACK, COLS], F32, name="kept")
+                for t in range(PACK):
+                    v_t = psum.tile([P, COLS], F32, name="v_t")
+                    for a in range(GROUP):
+                        nc.tensor.transpose(v_t[:, P * a : P * (a + 1)], v_sorted[:, a, t, :], ident[:])
+                    bias = b1_col[:, PACK * g + t : PACK * g + t + 1]
+                    nc.scalar.activation(out=grown[:, t, :], in_=v_t[:], func=ACT.Exp, bias=bias, scale=1.0)
+                    nc.scalar.activation(out=kept[:, t, :], in_=v_t[:], func=ACT.Relu, bias=bias, scale=1.0)
+                h_grouped = work.tile([P, COLS, PACK], BF16, name="h_grouped", align_bytes=64)
+                nc.vector.scalar_tensor_tensor(
+                    out=h_grouped[:],
+                    in0=grown[:].rearrange("p t w -> p w t"),
+                    scalar=-1.0,
+                    in1=kept[:].rearrange("p t w -> p w t"),
+                    op0=ALU.add,
+                    op1=ALU.min,
+                )
+
+                h_codes = work.tile([P, COLS], U32, name="h_codes", align_bytes=64)
+                h_plane = work.tile([P, COLS], U8, name="h_plane", align_bytes=64)
+                nc.vector.quantize_mx(
+                    out=h_codes[:].bitcast(FP8X4),
+                    scales=h_plane[:],
+                    in_=h_grouped[:].rearrange("p w t -> p (w t)"),
+                )
+                for a in range(GROUP):
+                    r_ps = psum.tile([P, WIDTH], F32, name="r_ps")
+                    nc.tensor.matmul_mx(
+                        out=r_ps[:],
+                        lhsT=h_codes[:, P * a : P * (a + 1)].bitcast(FP8X4),
+                        lhsT_scale=h_plane[:, P * a : P * (a + 1)],
+                        rhs=w2_codes[:, g, :].bitcast(FP8X4),
+                        rhs_scale=w2_plane[:, g, :],
+                        start=True,
+                        stop=True,
+                    )
+                    block = result[:, a, WIDTH * g : WIDTH * (g + 1)]
+                    nc.vector.tensor_tensor(out=block, in0=r_ps[:], in1=block, op=ALU.add)
+
+            nc.sync.dma_start(out=out_view[:, GROUP * chunk : GROUP * (chunk + 1), :], in_=result[:])

@@ -131,14 +131,19 @@ def tile_blockresmlp_mixerblock_pb_t_e_kernel(
                     bias = b1_col[:, PACK * g + t : PACK * g + t + 1]
                     nc.scalar.activation(out=grown[:, t, :], in_=v_t[:], func=ACT.Exp, bias=bias, scale=1.0)
                     nc.scalar.activation(out=kept[:, t, :], in_=v_t[:], func=ACT.Relu, bias=bias, scale=1.0)
-                h_grouped = work.tile([P, COLS, PACK], BF16, name="h_grouped", align_bytes=64)
+                h_planes = work.tile([P, PACK, COLS], BF16, name="h_planes")
                 nc.vector.scalar_tensor_tensor(
-                    out=h_grouped[:],
-                    in0=grown[:].rearrange("p t w -> p w t"),
+                    out=h_planes[:].rearrange("p t w -> p (t w)"),
+                    in0=grown[:].rearrange("p t w -> p (t w)"),
                     scalar=-1.0,
-                    in1=kept[:].rearrange("p t w -> p w t"),
+                    in1=kept[:].rearrange("p t w -> p (t w)"),
                     op0=ALU.add,
                     op1=ALU.min,
+                )
+                h_grouped = work.tile([P, COLS, PACK], BF16, name="h_grouped", align_bytes=64)
+                nc.vector.tensor_copy(
+                    out=h_grouped[:].rearrange("p (c i) t -> p c t i", i=4),
+                    in_=h_planes[:].rearrange("p t (c i) -> p c t i", i=4),
                 )
 
                 h_codes = work.tile([P, COLS], U32, name="h_codes", align_bytes=64)

@@ -19,8 +19,20 @@ BLOCKS = 2
 WIDTH = 512
 TILES = BATCH // P
 GROUP = 4
-CHUNKS = TILES // GROUP
 COLS = GROUP * P
+CHUNKS = TILES // GROUP
+ITEMS = TILES * BLOCKS
+UNITS = ITEMS // GROUP
+PAIRS = ITEMS // 2
+
+X_LEAD = 14
+Z_LEAD = 12
+V_LEAD = 6
+SORT_LEAD = 5
+TURN_LEAD = 1
+JOIN_LAG = 1
+R_LAG = 6
+END_LAG = 7
 
 FLOPS = 2 * BATCH * WIDTH * WIDTH * BLOCKS * 2
 
@@ -46,22 +58,27 @@ def tile_blockresmlp_mixerblock_pb_t_e_kernel(
 ):
     nc = tc.nc
     with ExitStack() as ctx:
+        ctx.enter_context(tc.manual_schedule())
         const = ctx.enter_context(tc.tile_pool(name="const", bufs=1))
-        rows = ctx.enter_context(tc.tile_pool(name="rows", bufs=3))
+        results = ctx.enter_context(tc.tile_pool(name="results", bufs=3))
         work = ctx.enter_context(tc.tile_pool(name="work", bufs=2))
         psum = ctx.enter_context(tc.psum_pool(name="psum", bufs=2))
 
         x_view = x_blocks.rearrange("(p i) c -> p i c", i=TILES)
         out_view = out.rearrange("(p i) c -> p i c", i=TILES)
 
-        def load_rows(chunk):
-            x_sb = rows.tile([P, GROUP, BLOCKS * WIDTH], BF16, name="x_sb")
-            nc.sync.dma_start(out=x_sb[:], in_=x_view[:, GROUP * chunk : GROUP * (chunk + 1), :])
-            return x_sb
+        x_sb = {}
 
-        x_first = load_rows(0)
+        def load_rows(chunk):
+            x_sb[chunk] = const.tile([P, GROUP, BLOCKS * WIDTH], BF16, name="x_sb%d" % chunk)
+            nc.sync.dma_start(out=x_sb[chunk][:], in_=x_view[:, GROUP * chunk : GROUP * (chunk + 1), :])
+
+        load_rows(0)
         w1_codes, w1_plane = load_weight(nc, const, w1_words, w1_scales, "w1")
+        load_rows(1)
         w2_codes, w2_plane = load_weight(nc, const, w2_words, w2_scales, "w2")
+        for chunk in range(2, CHUNKS):
+            load_rows(chunk)
 
         ident = const.tile([P, P], F32, name="ident")
         make_identity(nc, ident[:])
@@ -73,98 +90,191 @@ def tile_blockresmlp_mixerblock_pb_t_e_kernel(
         b2_all = const.tile([P, BLOCKS * WIDTH], BF16, name="b2_all")
         nc.scalar.dma_start(out=b2_all[:], in_=b2.rearrange("g o d -> (g o d)").partition_broadcast(P))
 
-        for chunk in range(CHUNKS):
-            x_sb = x_first if chunk == 0 else load_rows(chunk)
+        x_t, z_grouped, z_codes, z_plane = {}, {}, {}, {}
+        v_ps, v_sorted, v_t, grown, kept = {}, {}, {}, {}, {}
+        h_planes, h_grouped, h_codes, h_plane = {}, {}, {}, {}
+        r_ps, result = {}, {}
 
-            result = rows.tile([P, GROUP, BLOCKS * WIDTH], F32, name="result")
+        def transpose_x(pair):
+            if not 0 <= pair < PAIRS:
+                return
+            unit, half = divmod(pair, 2)
+            chunk, g = divmod(unit, BLOCKS)
+            x_t[pair] = psum.tile([P, 2, 2, P], F32, name="x_t")
+            for a in range(2):
+                x_words = x_sb[chunk][:, 2 * half + a, :].bitcast(F32)
+                for u in range(2):
+                    nc.tensor.transpose(
+                        x_t[pair][:, a, u, :], x_words[:, 256 * g + u : 256 * (g + 1) : 2], ident[:]
+                    )
+
+        def gather_z(pair):
+            if not 0 <= pair < PAIRS:
+                return
+            unit, half = divmod(pair, 2)
+            if half == 0:
+                z_grouped[unit] = work.tile([P, GROUP, P, PACK], BF16, name="z_grouped", align_bytes=64)
+            z_words = (
+                z_grouped[unit][:]
+                .rearrange("p a r k -> p (a r k)")
+                .bitcast(F32)
+                .rearrange("p (a r u) -> p a r u", a=GROUP, u=2)
+            )
+            target = z_words[:, 2 * half : 2 * half + 2, :, :]
+            source = x_t[pair][:].rearrange("p a u r -> p a r u")
+            if half == 0:
+                nc.scalar.copy(out=target, in_=source)
+            else:
+                nc.vector.tensor_copy(out=target, in_=source)
+
+        def quantise_z(unit):
+            if not 0 <= unit < UNITS:
+                return
+            z_codes[unit] = work.tile([P, COLS], U32, name="z_codes", align_bytes=64)
+            z_plane[unit] = work.tile([P, COLS], U8, name="z_plane", align_bytes=64)
+            nc.vector.quantize_mx(
+                out=z_codes[unit][:].bitcast(FP8X4),
+                scales=z_plane[unit][:],
+                in_=z_grouped[unit][:].rearrange("p a r k -> p (a r k)"),
+            )
+
+        def first_product(item):
+            if not 0 <= item < ITEMS:
+                return
+            unit, a = divmod(item, GROUP)
+            v_ps[item] = psum.tile([P, WIDTH], F32, name="v_ps")
+            nc.tensor.matmul_mx(
+                out=v_ps[item][:],
+                lhsT=z_codes[unit][:, P * a : P * (a + 1)].bitcast(FP8X4),
+                lhsT_scale=z_plane[unit][:, P * a : P * (a + 1)],
+                rhs=w1_codes[:, unit % BLOCKS, :].bitcast(FP8X4),
+                rhs_scale=w1_plane[:, unit % BLOCKS, :],
+                start=True,
+                stop=True,
+            )
+
+        def sort_v(item):
+            if not 0 <= item < ITEMS:
+                return
+            unit, a = divmod(item, GROUP)
+            if a == 0:
+                v_sorted[unit] = work.tile([P, GROUP, PACK, P], F32, name="v_sorted")
+            nc.scalar.copy(
+                out=v_sorted[unit][:, a, :, :], in_=v_ps[item][:].rearrange("b (p t) -> b t p", t=PACK)
+            )
+
+        def transpose_v(bank):
+            if not 0 <= bank < ITEMS:
+                return
+            unit, t = divmod(bank, PACK)
+            v_t[bank] = psum.tile([P, COLS], F32, name="v_t")
             for a in range(GROUP):
-                nc.gpsimd.tensor_tensor(out=result[:, a, :], in0=x_sb[:, a, :], in1=b2_all[:], op=ALU.add)
+                nc.tensor.transpose(v_t[bank][:, P * a : P * (a + 1)], v_sorted[unit][:, a, t, :], ident[:])
 
-            for g in range(BLOCKS):
-                z_grouped = work.tile([P, GROUP, P, PACK], BF16, name="z_grouped", align_bytes=64)
-                z_words = (
-                    z_grouped[:]
-                    .rearrange("p a r k -> p (a r k)")
-                    .bitcast(F32)
-                    .rearrange("p (a r u) -> p a r u", a=GROUP, u=2)
-                )
-                for half in range(GROUP // 2):
-                    x_t = psum.tile([P, 2, 2, P], F32, name="x_t")
-                    for a in range(2):
-                        x_words = x_sb[:, 2 * half + a, :].bitcast(F32)
-                        for u in range(2):
-                            nc.tensor.transpose(
-                                x_t[:, a, u, :], x_words[:, 256 * g + u : 256 * (g + 1) : 2], ident[:]
-                            )
-                    nc.vector.tensor_copy(
-                        out=z_words[:, 2 * half : 2 * half + 2, :, :],
-                        in_=x_t[:].rearrange("p a u r -> p a r u"),
-                    )
+        def exp_and_relu(bank):
+            if not 0 <= bank < ITEMS:
+                return
+            unit, t = divmod(bank, PACK)
+            if t == 0:
+                grown[unit] = work.tile([P, PACK, COLS], F32, name="grown")
+                kept[unit] = work.tile([P, PACK, COLS], F32, name="kept")
+            column = PACK * (unit % BLOCKS) + t
+            bias = b1_col[:, column : column + 1]
+            nc.scalar.activation(out=grown[unit][:, t, :], in_=v_t[bank][:], func=ACT.Exp, bias=bias, scale=1.0)
+            nc.scalar.activation(out=kept[unit][:, t, :], in_=v_t[bank][:], func=ACT.Relu, bias=bias, scale=1.0)
 
-                z_codes = work.tile([P, COLS], U32, name="z_codes", align_bytes=64)
-                z_plane = work.tile([P, COLS], U8, name="z_plane", align_bytes=64)
-                nc.vector.quantize_mx(
-                    out=z_codes[:].bitcast(FP8X4),
-                    scales=z_plane[:],
-                    in_=z_grouped[:].rearrange("p a r k -> p (a r k)"),
-                )
-                v_sorted = work.tile([P, GROUP, PACK, P], F32, name="v_sorted")
-                for a in range(GROUP):
-                    v_ps = psum.tile([P, WIDTH], F32, name="v_ps")
-                    nc.tensor.matmul_mx(
-                        out=v_ps[:],
-                        lhsT=z_codes[:, P * a : P * (a + 1)].bitcast(FP8X4),
-                        lhsT_scale=z_plane[:, P * a : P * (a + 1)],
-                        rhs=w1_codes[:, g, :].bitcast(FP8X4),
-                        rhs_scale=w1_plane[:, g, :],
-                        start=True,
-                        stop=True,
-                    )
-                    nc.scalar.copy(out=v_sorted[:, a, :, :], in_=v_ps[:].rearrange("b (p t) -> b t p", t=PACK))
+        def join(bank):
+            if not 0 <= bank < ITEMS:
+                return
+            unit, t = divmod(bank, PACK)
+            if t == 0:
+                h_planes[unit] = work.tile([P, PACK, COLS], BF16, name="h_planes")
+            nc.vector.scalar_tensor_tensor(
+                out=h_planes[unit][:, t, :],
+                in0=grown[unit][:, t, :],
+                scalar=-1.0,
+                in1=kept[unit][:, t, :],
+                op0=ALU.add,
+                op1=ALU.min,
+            )
 
-                grown = work.tile([P, PACK, COLS], F32, name="grown")
-                kept = work.tile([P, PACK, COLS], F32, name="kept")
-                for t in range(PACK):
-                    v_t = psum.tile([P, COLS], F32, name="v_t")
-                    for a in range(GROUP):
-                        nc.tensor.transpose(v_t[:, P * a : P * (a + 1)], v_sorted[:, a, t, :], ident[:])
-                    bias = b1_col[:, PACK * g + t : PACK * g + t + 1]
-                    nc.scalar.activation(out=grown[:, t, :], in_=v_t[:], func=ACT.Exp, bias=bias, scale=1.0)
-                    nc.scalar.activation(out=kept[:, t, :], in_=v_t[:], func=ACT.Relu, bias=bias, scale=1.0)
-                h_planes = work.tile([P, PACK, COLS], BF16, name="h_planes")
-                nc.vector.scalar_tensor_tensor(
-                    out=h_planes[:].rearrange("p t w -> p (t w)"),
-                    in0=grown[:].rearrange("p t w -> p (t w)"),
-                    scalar=-1.0,
-                    in1=kept[:].rearrange("p t w -> p (t w)"),
-                    op0=ALU.add,
-                    op1=ALU.min,
-                )
-                h_grouped = work.tile([P, COLS, PACK], BF16, name="h_grouped", align_bytes=64)
-                nc.vector.tensor_copy(
-                    out=h_grouped[:].rearrange("p (c i) t -> p c t i", i=4),
-                    in_=h_planes[:].rearrange("p t (c i) -> p c t i", i=4),
+        def regroup(unit):
+            if not 0 <= unit < UNITS:
+                return
+            h_grouped[unit] = work.tile([P, COLS, PACK], BF16, name="h_grouped", align_bytes=64)
+            nc.vector.tensor_copy(
+                out=h_grouped[unit][:].rearrange("p (c i) t -> p c t i", i=4),
+                in_=h_planes[unit][:].rearrange("p t (c i) -> p c t i", i=4),
+            )
+
+        def quantise_h(unit):
+            if not 0 <= unit < UNITS:
+                return
+            h_codes[unit] = work.tile([P, COLS], U32, name="h_codes", align_bytes=64)
+            h_plane[unit] = work.tile([P, COLS], U8, name="h_plane", align_bytes=64)
+            nc.vector.quantize_mx(
+                out=h_codes[unit][:].bitcast(FP8X4),
+                scales=h_plane[unit][:],
+                in_=h_grouped[unit][:].rearrange("p w t -> p (w t)"),
+            )
+
+        def second_product(item):
+            if not 0 <= item < ITEMS:
+                return
+            unit, a = divmod(item, GROUP)
+            r_ps[item] = psum.tile([P, WIDTH], F32, name="r_ps")
+            nc.tensor.matmul_mx(
+                out=r_ps[item][:],
+                lhsT=h_codes[unit][:, P * a : P * (a + 1)].bitcast(FP8X4),
+                lhsT_scale=h_plane[unit][:, P * a : P * (a + 1)],
+                rhs=w2_codes[:, unit % BLOCKS, :].bitcast(FP8X4),
+                rhs_scale=w2_plane[:, unit % BLOCKS, :],
+                start=True,
+                stop=True,
+            )
+
+        def add_b2(tile):
+            if not 0 <= tile < TILES:
+                return
+            chunk, a = divmod(tile, GROUP)
+            if a == 0:
+                result[chunk] = results.tile([P, GROUP, BLOCKS * WIDTH], F32, name="result")
+            nc.gpsimd.tensor_tensor(out=result[chunk][:, a, :], in0=x_sb[chunk][:, a, :], in1=b2_all[:], op=ALU.add)
+
+        def finish(item):
+            if not 0 <= item < ITEMS:
+                return
+            unit, a = divmod(item, GROUP)
+            chunk, g = divmod(unit, BLOCKS)
+            columns = slice(WIDTH * g, WIDTH * (g + 1))
+            block = result[chunk][:, a, columns]
+            nc.vector.tensor_tensor(out=block, in0=r_ps[item][:], in1=block, op=ALU.add)
+            if a == GROUP - 1:
+                nc.sync.dma_start(
+                    out=out_view[:, GROUP * chunk : GROUP * (chunk + 1), columns],
+                    in_=result[chunk][:, :, columns],
                 )
 
-                h_codes = work.tile([P, COLS], U32, name="h_codes", align_bytes=64)
-                h_plane = work.tile([P, COLS], U8, name="h_plane", align_bytes=64)
-                nc.vector.quantize_mx(
-                    out=h_codes[:].bitcast(FP8X4),
-                    scales=h_plane[:],
-                    in_=h_grouped[:].rearrange("p w t -> p (w t)"),
-                )
-                for a in range(GROUP):
-                    r_ps = psum.tile([P, WIDTH], F32, name="r_ps")
-                    nc.tensor.matmul_mx(
-                        out=r_ps[:],
-                        lhsT=h_codes[:, P * a : P * (a + 1)].bitcast(FP8X4),
-                        lhsT_scale=h_plane[:, P * a : P * (a + 1)],
-                        rhs=w2_codes[:, g, :].bitcast(FP8X4),
-                        rhs_scale=w2_plane[:, g, :],
-                        start=True,
-                        stop=True,
-                    )
-                    block = result[:, a, WIDTH * g : WIDTH * (g + 1)]
-                    nc.vector.tensor_tensor(out=block, in0=r_ps[:], in1=block, op=ALU.add)
-
-            nc.sync.dma_start(out=out_view[:, GROUP * chunk : GROUP * (chunk + 1), :], in_=result[:])
+        for slot in range(-X_LEAD, ITEMS + END_LAG):
+            phase = slot % GROUP
+            transpose_v(slot + TURN_LEAD)
+            first_product(slot + V_LEAD)
+            second_product(slot - R_LAG)
+            if slot % 2 == 0:
+                transpose_x((slot + X_LEAD) // 2)
+            if slot % 2 == 0:
+                add_b2(slot // 2)
+            sort_v(slot + SORT_LEAD)
+            exp_and_relu(slot)
+            if phase == 0:
+                gather_z((slot + Z_LEAD) // 2)
+            join(slot - JOIN_LAG)
+            if phase == 0:
+                regroup((slot - JOIN_LAG) // GROUP)
+            finish(slot - END_LAG)
+            if phase == 1:
+                quantise_h((slot - JOIN_LAG - 1) // GROUP)
+            if phase == 2:
+                gather_z((slot + Z_LEAD) // 2)
+            if phase == 3:
+                quantise_z((slot + Z_LEAD - 3) // GROUP)

@@ -33,6 +33,7 @@ TURN_LEAD = 1
 JOIN_LAG = 1
 R_LAG = 6
 END_LAG = 7
+B2_LEAD = 16
 
 FLOPS = 2 * BATCH * WIDTH * WIDTH * BLOCKS * 2
 
@@ -60,7 +61,7 @@ def tile_blockresmlp_mixerblock_pb_t_e_kernel(
     with ExitStack() as ctx:
         ctx.enter_context(tc.manual_schedule())
         const = ctx.enter_context(tc.tile_pool(name="const", bufs=1))
-        results = ctx.enter_context(tc.tile_pool(name="results", bufs=3))
+        results = ctx.enter_context(tc.tile_pool(name="results", bufs=4))
         work = ctx.enter_context(tc.tile_pool(name="work", bufs=2))
         psum = ctx.enter_context(tc.psum_pool(name="psum", bufs=2))
 
@@ -120,12 +121,9 @@ def tile_blockresmlp_mixerblock_pb_t_e_kernel(
                 .bitcast(F32)
                 .rearrange("p (a r u) -> p a r u", a=GROUP, u=2)
             )
-            target = z_words[:, 2 * half : 2 * half + 2, :, :]
-            source = x_t[pair][:].rearrange("p a u r -> p a r u")
-            if half == 0:
-                nc.scalar.copy(out=target, in_=source)
-            else:
-                nc.vector.tensor_copy(out=target, in_=source)
+            nc.scalar.copy(
+                out=z_words[:, 2 * half : 2 * half + 2, :, :], in_=x_t[pair][:].rearrange("p a u r -> p a r u")
+            )
 
         def quantise_z(unit):
             if not 0 <= unit < UNITS:
@@ -239,7 +237,7 @@ def tile_blockresmlp_mixerblock_pb_t_e_kernel(
             chunk, a = divmod(tile, GROUP)
             if a == 0:
                 result[chunk] = results.tile([P, GROUP, BLOCKS * WIDTH], F32, name="result")
-            nc.gpsimd.tensor_tensor(out=result[chunk][:, a, :], in0=x_sb[chunk][:, a, :], in1=b2_all[:], op=ALU.add)
+            nc.vector.tensor_tensor(out=result[chunk][:, a, :], in0=x_sb[chunk][:, a, :], in1=b2_all[:], op=ALU.add)
 
         def finish(item):
             if not 0 <= item < ITEMS:
@@ -262,11 +260,9 @@ def tile_blockresmlp_mixerblock_pb_t_e_kernel(
             second_product(slot - R_LAG)
             if slot % 2 == 0:
                 transpose_x((slot + X_LEAD) // 2)
-            if slot % 2 == 0:
-                add_b2(slot // 2)
             sort_v(slot + SORT_LEAD)
             exp_and_relu(slot)
-            if phase == 0:
+            if slot % 2 == 0:
                 gather_z((slot + Z_LEAD) // 2)
             join(slot - JOIN_LAG)
             if phase == 0:
@@ -274,7 +270,7 @@ def tile_blockresmlp_mixerblock_pb_t_e_kernel(
             finish(slot - END_LAG)
             if phase == 1:
                 quantise_h((slot - JOIN_LAG - 1) // GROUP)
-            if phase == 2:
-                gather_z((slot + Z_LEAD) // 2)
             if phase == 3:
                 quantise_z((slot + Z_LEAD - 3) // GROUP)
+            if phase >= 2:
+                add_b2(2 * ((slot + B2_LEAD) // GROUP) + phase - 2)

@@ -31,8 +31,7 @@ V_LEAD = 6
 SORT_LEAD = 5
 TURN_LEAD = 1
 JOIN_LAG = 1
-R_LAG = 6
-END_LAG = 7
+END_UNITS = 2
 B2_LEAD = 16
 
 FLOPS = 2 * BATCH * WIDTH * WIDTH * BLOCKS * 2
@@ -200,9 +199,13 @@ def tile_blockresmlp_mixerblock_pb_t_e_kernel(
             if not 0 <= unit < UNITS:
                 return
             h_grouped[unit] = work.tile([P, COLS, PACK], BF16, name="h_grouped", align_bytes=64)
-            nc.vector.tensor_copy(
-                out=h_grouped[unit][:].rearrange("p (c i) t -> p c t i", i=4),
-                in_=h_planes[unit][:].rearrange("p t (c i) -> p c t i", i=4),
+            nc.gpsimd.tensor_scalar(
+                out=h_grouped[unit][:],
+                in0=h_planes[unit][:].rearrange("p t w -> p w t"),
+                scalar1=1.0,
+                scalar2=0.0,
+                op0=ALU.mult,
+                op1=ALU.add,
             )
 
         def quantise_h(unit):
@@ -253,13 +256,13 @@ def tile_blockresmlp_mixerblock_pb_t_e_kernel(
                     in_=result[chunk][:, :, columns],
                 )
 
-        for slot in range(-X_LEAD, ITEMS + END_LAG):
+        for slot in range(-X_LEAD, ITEMS + GROUP * END_UNITS + 1):
             phase = slot % GROUP
+            ending = GROUP * (slot // GROUP - END_UNITS)
             transpose_v(slot + TURN_LEAD)
-            first_product(slot + V_LEAD)
-            second_product(slot - R_LAG)
             if slot % 2 == 0:
                 transpose_x((slot + X_LEAD) // 2)
+            first_product(slot + V_LEAD)
             sort_v(slot + SORT_LEAD)
             exp_and_relu(slot)
             if slot % 2 == 0:
@@ -267,9 +270,17 @@ def tile_blockresmlp_mixerblock_pb_t_e_kernel(
             join(slot - JOIN_LAG)
             if phase == 0:
                 regroup((slot - JOIN_LAG) // GROUP)
-            finish(slot - END_LAG)
+                finish(ending)
+                finish(ending + 1)
+                second_product(ending + 2)
+                second_product(ending + 3)
+                finish(ending + 2)
+                finish(ending + 3)
             if phase == 1:
                 quantise_h((slot - JOIN_LAG - 1) // GROUP)
+            if phase == 2:
+                second_product(ending + GROUP)
+                second_product(ending + GROUP + 1)
             if phase == 3:
                 quantise_z((slot + Z_LEAD - 3) // GROUP)
             if phase >= 2:

@@ -13,10 +13,12 @@ ALU = mybir.AluOpType
 ACT = mybir.ActivationFunctionType
 
 P = 128
+QUADRANT = 32
 PACK = 4
 BATCH = 4096
 BLOCKS = 2
 WIDTH = 512
+WORDS = WIDTH // 2
 TILES = BATCH // P
 GROUP = 4
 COLS = GROUP * P
@@ -30,27 +32,28 @@ Z_LEAD = 12
 V_LEAD = 6
 SORT_LEAD = 5
 TURN_LEAD = 1
+B2_LEAD = 16
 JOIN_LAG = 1
 END_UNITS = 2
-B2_LEAD = 16
+LAST_SLOT = GROUP * (UNITS - 1 + END_UNITS)
 
 FLOPS = 2 * BATCH * WIDTH * WIDTH * BLOCKS * 2
 
 
 def load_weight(nc, pool, words, scales, label):
     codes = pool.tile([P, BLOCKS, WIDTH], U32, name=label + "_codes", align_bytes=64)
-    plane = pool.tile([P, BLOCKS, WIDTH], U8, name=label + "_plane", align_bytes=64)
-    nc.vector.memset(plane[:].rearrange("p g n -> p (g n)").bitcast(I32), 0)
+    scale_sb = pool.tile([P, BLOCKS, WIDTH], U8, name=label + "_scale_sb", align_bytes=64)
+    nc.vector.memset(scale_sb[:].rearrange("p g n -> p (g n)").bitcast(I32), 0)
     nc.sync.dma_start(
         out=codes[:].bitcast(I32),
         in_=words.rearrange("g p n t -> p g (n t)").bitcast(I32),
     )
-    for quadrant in range(4):
+    for quadrant in range(P // QUADRANT):
         nc.sync.dma_start(
-            out=plane[32 * quadrant : 32 * quadrant + 4].bitcast(I32),
-            in_=scales[:, 4 * quadrant : 4 * quadrant + 4, :].rearrange("g r n -> r g n").bitcast(I32),
+            out=scale_sb[QUADRANT * quadrant : QUADRANT * quadrant + PACK].bitcast(I32),
+            in_=scales[:, PACK * quadrant : PACK * (quadrant + 1), :].rearrange("g r n -> r g n").bitcast(I32),
         )
-    return codes, plane
+    return codes, scale_sb
 
 
 def tile_blockresmlp_mixerblock_pb_t_e_kernel(
@@ -74,9 +77,9 @@ def tile_blockresmlp_mixerblock_pb_t_e_kernel(
             nc.sync.dma_start(out=x_sb[chunk][:], in_=x_view[:, GROUP * chunk : GROUP * (chunk + 1), :])
 
         load_rows(0)
-        w1_codes, w1_plane = load_weight(nc, const, w1_words, w1_scales, "w1")
+        w1_codes, w1_scale_sb = load_weight(nc, const, w1_words, w1_scales, "w1")
         load_rows(1)
-        w2_codes, w2_plane = load_weight(nc, const, w2_words, w2_scales, "w2")
+        w2_codes, w2_scale_sb = load_weight(nc, const, w2_words, w2_scales, "w2")
         for chunk in range(2, CHUNKS):
             load_rows(chunk)
 
@@ -90,9 +93,9 @@ def tile_blockresmlp_mixerblock_pb_t_e_kernel(
         b2_all = const.tile([P, BLOCKS * WIDTH], BF16, name="b2_all")
         nc.scalar.dma_start(out=b2_all[:], in_=b2.rearrange("g o d -> (g o d)").partition_broadcast(P))
 
-        x_t, z_grouped, z_codes, z_plane = {}, {}, {}, {}
-        v_ps, v_sorted, v_t, grown, kept = {}, {}, {}, {}, {}
-        h_planes, h_grouped, h_codes, h_plane = {}, {}, {}, {}
+        x_turned, z_grouped, z_codes, z_scales = {}, {}, {}, {}
+        v_ps, v_sorted, v_turned, grown, kept = {}, {}, {}, {}, {}
+        h_quarters, h_grouped, h_codes, h_scales = {}, {}, {}, {}
         r_ps, result = {}, {}
 
         def transpose_x(pair):
@@ -100,12 +103,12 @@ def tile_blockresmlp_mixerblock_pb_t_e_kernel(
                 return
             unit, half = divmod(pair, 2)
             chunk, g = divmod(unit, BLOCKS)
-            x_t[pair] = psum.tile([P, 2, 2, P], F32, name="x_t")
+            x_turned[pair] = psum.tile([P, 2, 2, P], F32, name="x_turned")
             for a in range(2):
                 x_words = x_sb[chunk][:, 2 * half + a, :].bitcast(F32)
                 for u in range(2):
                     nc.tensor.transpose(
-                        x_t[pair][:, a, u, :], x_words[:, 256 * g + u : 256 * (g + 1) : 2], ident[:]
+                        x_turned[pair][:, a, u, :], x_words[:, WORDS * g + u : WORDS * (g + 1) : 2], ident[:]
                     )
 
         def gather_z(pair):
@@ -121,17 +124,18 @@ def tile_blockresmlp_mixerblock_pb_t_e_kernel(
                 .rearrange("p (a r u) -> p a r u", a=GROUP, u=2)
             )
             nc.scalar.copy(
-                out=z_words[:, 2 * half : 2 * half + 2, :, :], in_=x_t[pair][:].rearrange("p a u r -> p a r u")
+                out=z_words[:, 2 * half : 2 * half + 2, :, :],
+                in_=x_turned[pair][:].rearrange("p a u r -> p a r u"),
             )
 
         def quantise_z(unit):
             if not 0 <= unit < UNITS:
                 return
             z_codes[unit] = work.tile([P, COLS], U32, name="z_codes", align_bytes=64)
-            z_plane[unit] = work.tile([P, COLS], U8, name="z_plane", align_bytes=64)
+            z_scales[unit] = work.tile([P, COLS], U8, name="z_scales", align_bytes=64)
             nc.vector.quantize_mx(
                 out=z_codes[unit][:].bitcast(FP8X4),
-                scales=z_plane[unit][:],
+                scales=z_scales[unit][:],
                 in_=z_grouped[unit][:].rearrange("p a r k -> p (a r k)"),
             )
 
@@ -143,9 +147,9 @@ def tile_blockresmlp_mixerblock_pb_t_e_kernel(
             nc.tensor.matmul_mx(
                 out=v_ps[item][:],
                 lhsT=z_codes[unit][:, P * a : P * (a + 1)].bitcast(FP8X4),
-                lhsT_scale=z_plane[unit][:, P * a : P * (a + 1)],
+                lhsT_scale=z_scales[unit][:, P * a : P * (a + 1)],
                 rhs=w1_codes[:, unit % BLOCKS, :].bitcast(FP8X4),
-                rhs_scale=w1_plane[:, unit % BLOCKS, :],
+                rhs_scale=w1_scale_sb[:, unit % BLOCKS, :],
                 start=True,
                 stop=True,
             )
@@ -160,34 +164,37 @@ def tile_blockresmlp_mixerblock_pb_t_e_kernel(
                 out=v_sorted[unit][:, a, :, :], in_=v_ps[item][:].rearrange("b (p t) -> b t p", t=PACK)
             )
 
-        def transpose_v(bank):
-            if not 0 <= bank < ITEMS:
+        def transpose_v(quarter):
+            if not 0 <= quarter < ITEMS:
                 return
-            unit, t = divmod(bank, PACK)
-            v_t[bank] = psum.tile([P, COLS], F32, name="v_t")
+            unit, t = divmod(quarter, PACK)
+            v_turned[quarter] = psum.tile([P, COLS], F32, name="v_turned")
             for a in range(GROUP):
-                nc.tensor.transpose(v_t[bank][:, P * a : P * (a + 1)], v_sorted[unit][:, a, t, :], ident[:])
+                nc.tensor.transpose(
+                    v_turned[quarter][:, P * a : P * (a + 1)], v_sorted[unit][:, a, t, :], ident[:]
+                )
 
-        def exp_and_relu(bank):
-            if not 0 <= bank < ITEMS:
+        def exp_and_relu(quarter):
+            if not 0 <= quarter < ITEMS:
                 return
-            unit, t = divmod(bank, PACK)
+            unit, t = divmod(quarter, PACK)
             if t == 0:
                 grown[unit] = work.tile([P, PACK, COLS], F32, name="grown")
                 kept[unit] = work.tile([P, PACK, COLS], F32, name="kept")
             column = PACK * (unit % BLOCKS) + t
             bias = b1_col[:, column : column + 1]
-            nc.scalar.activation(out=grown[unit][:, t, :], in_=v_t[bank][:], func=ACT.Exp, bias=bias, scale=1.0)
-            nc.scalar.activation(out=kept[unit][:, t, :], in_=v_t[bank][:], func=ACT.Relu, bias=bias, scale=1.0)
+            source = v_turned[quarter][:]
+            nc.scalar.activation(out=grown[unit][:, t, :], in_=source, func=ACT.Exp, bias=bias, scale=1.0)
+            nc.scalar.activation(out=kept[unit][:, t, :], in_=source, func=ACT.Relu, bias=bias, scale=1.0)
 
-        def join(bank):
-            if not 0 <= bank < ITEMS:
+        def join(quarter):
+            if not 0 <= quarter < ITEMS:
                 return
-            unit, t = divmod(bank, PACK)
+            unit, t = divmod(quarter, PACK)
             if t == 0:
-                h_planes[unit] = work.tile([P, PACK, COLS], BF16, name="h_planes")
+                h_quarters[unit] = work.tile([P, PACK, COLS], BF16, name="h_quarters")
             nc.vector.scalar_tensor_tensor(
-                out=h_planes[unit][:, t, :],
+                out=h_quarters[unit][:, t, :],
                 in0=grown[unit][:, t, :],
                 scalar=-1.0,
                 in1=kept[unit][:, t, :],
@@ -201,7 +208,7 @@ def tile_blockresmlp_mixerblock_pb_t_e_kernel(
             h_grouped[unit] = work.tile([P, COLS, PACK], BF16, name="h_grouped", align_bytes=64)
             nc.gpsimd.tensor_scalar(
                 out=h_grouped[unit][:],
-                in0=h_planes[unit][:].rearrange("p t w -> p w t"),
+                in0=h_quarters[unit][:].rearrange("p t w -> p w t"),
                 scalar1=1.0,
                 scalar2=0.0,
                 op0=ALU.mult,
@@ -212,10 +219,10 @@ def tile_blockresmlp_mixerblock_pb_t_e_kernel(
             if not 0 <= unit < UNITS:
                 return
             h_codes[unit] = work.tile([P, COLS], U32, name="h_codes", align_bytes=64)
-            h_plane[unit] = work.tile([P, COLS], U8, name="h_plane", align_bytes=64)
+            h_scales[unit] = work.tile([P, COLS], U8, name="h_scales", align_bytes=64)
             nc.vector.quantize_mx(
                 out=h_codes[unit][:].bitcast(FP8X4),
-                scales=h_plane[unit][:],
+                scales=h_scales[unit][:],
                 in_=h_grouped[unit][:].rearrange("p w t -> p (w t)"),
             )
 
@@ -227,17 +234,17 @@ def tile_blockresmlp_mixerblock_pb_t_e_kernel(
             nc.tensor.matmul_mx(
                 out=r_ps[item][:],
                 lhsT=h_codes[unit][:, P * a : P * (a + 1)].bitcast(FP8X4),
-                lhsT_scale=h_plane[unit][:, P * a : P * (a + 1)],
+                lhsT_scale=h_scales[unit][:, P * a : P * (a + 1)],
                 rhs=w2_codes[:, unit % BLOCKS, :].bitcast(FP8X4),
-                rhs_scale=w2_plane[:, unit % BLOCKS, :],
+                rhs_scale=w2_scale_sb[:, unit % BLOCKS, :],
                 start=True,
                 stop=True,
             )
 
-        def add_b2(tile):
-            if not 0 <= tile < TILES:
+        def add_b2(batch_tile):
+            if not 0 <= batch_tile < TILES:
                 return
-            chunk, a = divmod(tile, GROUP)
+            chunk, a = divmod(batch_tile, GROUP)
             if a == 0:
                 result[chunk] = results.tile([P, GROUP, BLOCKS * WIDTH], F32, name="result")
             nc.vector.tensor_tensor(out=result[chunk][:, a, :], in0=x_sb[chunk][:, a, :], in1=b2_all[:], op=ALU.add)
@@ -250,15 +257,12 @@ def tile_blockresmlp_mixerblock_pb_t_e_kernel(
             columns = slice(WIDTH * g, WIDTH * (g + 1))
             block = result[chunk][:, a, columns]
             nc.vector.tensor_tensor(out=block, in0=r_ps[item][:], in1=block, op=ALU.add)
-            if a == GROUP - 1:
-                nc.sync.dma_start(
-                    out=out_view[:, GROUP * chunk : GROUP * (chunk + 1), columns],
-                    in_=result[chunk][:, :, columns],
-                )
+            nc.sync.dma_start(out=out_view[:, GROUP * chunk + a, columns], in_=block)
 
-        for slot in range(-X_LEAD, ITEMS + GROUP * END_UNITS + 1):
+        for slot in range(-X_LEAD, LAST_SLOT + 1):
             phase = slot % GROUP
-            ending = GROUP * (slot // GROUP - END_UNITS)
+            unit_now = slot // GROUP
+            ending = GROUP * (unit_now - END_UNITS)
             transpose_v(slot + TURN_LEAD)
             if slot % 2 == 0:
                 transpose_x((slot + X_LEAD) // 2)
@@ -269,7 +273,7 @@ def tile_blockresmlp_mixerblock_pb_t_e_kernel(
                 gather_z((slot + Z_LEAD) // 2)
             join(slot - JOIN_LAG)
             if phase == 0:
-                regroup((slot - JOIN_LAG) // GROUP)
+                regroup(unit_now - 1)
                 finish(ending)
                 finish(ending + 1)
                 second_product(ending + 2)
@@ -277,11 +281,11 @@ def tile_blockresmlp_mixerblock_pb_t_e_kernel(
                 finish(ending + 2)
                 finish(ending + 3)
             if phase == 1:
-                quantise_h((slot - JOIN_LAG - 1) // GROUP)
+                quantise_h(unit_now - 1)
             if phase == 2:
                 second_product(ending + GROUP)
                 second_product(ending + GROUP + 1)
             if phase == 3:
-                quantise_z((slot + Z_LEAD - 3) // GROUP)
+                quantise_z(unit_now + Z_LEAD // GROUP)
             if phase >= 2:
-                add_b2(2 * ((slot + B2_LEAD) // GROUP) + phase - 2)
+                add_b2(2 * (unit_now + B2_LEAD // GROUP) + phase - 2)

@@ -20,52 +20,28 @@ BLOCKS = 2
 WIDTH = 512
 WORDS = WIDTH // 2
 TILES = BATCH // P
-GROUP = 4
-COLS = GROUP * P
-CHUNKS = TILES // GROUP
-ITEMS = TILES * BLOCKS
-UNITS = ITEMS // GROUP
-PAIRS = ITEMS // 2
-
-X_LEAD = 14
-Z_LEAD = 12
-V_LEAD = 6
-SORT_LEAD = 5
-TURN_LEAD = 1
-B2_LEAD = 16
-JOIN_LAG = 1
-END_UNITS = 2
-LAST_SLOT = GROUP * (UNITS - 1 + END_UNITS)
+MOST = 4
+CHUNK_TILES = [2, 2, 4, 4, 4, 4, 4, 4, 2, 2]
+RESULT_BUFS = 16
+ADD_LEAD = 4
 
 FLOPS = 2 * BATCH * WIDTH * WIDTH * BLOCKS * 2
-
-
-def load_weight(nc, pool, words, scales, label):
-    codes = pool.tile([P, BLOCKS, WIDTH], U32, name=label + "_codes", align_bytes=64)
-    scale_sb = pool.tile([P, BLOCKS, WIDTH], U8, name=label + "_scale_sb", align_bytes=64)
-    nc.vector.memset(scale_sb[:].rearrange("p g n -> p (g n)").bitcast(I32), 0)
-    nc.sync.dma_start(
-        out=codes[:].bitcast(I32),
-        in_=words.rearrange("g p n t -> p g (n t)").bitcast(I32),
-    )
-    for quadrant in range(P // QUADRANT):
-        nc.sync.dma_start(
-            out=scale_sb[QUADRANT * quadrant : QUADRANT * quadrant + PACK].bitcast(I32),
-            in_=scales[:, PACK * quadrant : PACK * (quadrant + 1), :].rearrange("g r n -> r g n").bitcast(I32),
-        )
-    return codes, scale_sb
 
 
 def tile_blockresmlp_mixerblock_pb_t_e_kernel(
     tc, x_blocks, w1_words, w1_scales, b1, w2_words, w2_scales, b2, out
 ):
     nc = tc.nc
+    firsts = [sum(CHUNK_TILES[:c]) for c in range(len(CHUNK_TILES))]
+    units = [(c, g, n) for c, n in enumerate(CHUNK_TILES) for g in range(BLOCKS)]
     with ExitStack() as ctx:
         ctx.enter_context(tc.manual_schedule())
         const = ctx.enter_context(tc.tile_pool(name="const", bufs=1))
-        results = ctx.enter_context(tc.tile_pool(name="results", bufs=4))
+        results = ctx.enter_context(tc.tile_pool(name="results", bufs=RESULT_BUFS))
+        ahead = ctx.enter_context(tc.tile_pool(name="ahead", bufs=3))
         work = ctx.enter_context(tc.tile_pool(name="work", bufs=2))
-        psum = ctx.enter_context(tc.psum_pool(name="psum", bufs=2))
+        psum_two = ctx.enter_context(tc.psum_pool(name="psum_two", bufs=2))
+        psum_four = ctx.enter_context(tc.psum_pool(name="psum_four", bufs=4))
 
         x_view = x_blocks.rearrange("(p i) c -> p i c", i=TILES)
         out_view = out.rearrange("(p i) c -> p i c", i=TILES)
@@ -73,219 +49,230 @@ def tile_blockresmlp_mixerblock_pb_t_e_kernel(
         x_sb = {}
 
         def load_rows(chunk):
-            x_sb[chunk] = const.tile([P, GROUP, BLOCKS * WIDTH], BF16, name="x_sb%d" % chunk)
-            nc.sync.dma_start(out=x_sb[chunk][:], in_=x_view[:, GROUP * chunk : GROUP * (chunk + 1), :])
+            n = CHUNK_TILES[chunk]
+            first = firsts[chunk]
+            x_sb[chunk] = const.tile([P, n, BLOCKS * WIDTH], BF16, name="x_sb%d" % chunk)
+            nc.sync.dma_start(out=x_sb[chunk][:], in_=x_view[:, first : first + n, :])
+
+        def load_scales(scale_sb, scales):
+            nc.vector.memset(scale_sb[:].rearrange("p g n -> p (g n)").bitcast(I32), 0)
+            for quadrant in range(P // QUADRANT):
+                nc.sync.dma_start(
+                    out=scale_sb[QUADRANT * quadrant : QUADRANT * quadrant + PACK].bitcast(I32),
+                    in_=scales[:, PACK * quadrant : PACK * (quadrant + 1), :].rearrange("g r n -> r g n").bitcast(I32),
+                )
+
+        def load_codes(codes, words):
+            for g in range(BLOCKS):
+                nc.sync.dma_start(
+                    out=codes[:, g, :].bitcast(I32), in_=words[g].rearrange("p n t -> p (n t)").bitcast(I32)
+                )
+
+        w1_raw = const.tile([P, BLOCKS, WIDTH], U32, name="w1_raw", align_bytes=64)
+        w1_scale_raw = const.tile([P, BLOCKS, WIDTH], U8, name="w1_scale_raw", align_bytes=64)
+        w1_codes = const.tile([P, BLOCKS, WIDTH], U32, name="w1_codes", align_bytes=64)
+        w1_scale_sb = const.tile([P, BLOCKS, WIDTH], U8, name="w1_scale_sb", align_bytes=64)
+        w2_codes = const.tile([P, BLOCKS, WIDTH], U32, name="w2_codes", align_bytes=64)
+        w2_scale_sb = const.tile([P, BLOCKS, WIDTH], U8, name="w2_scale_sb", align_bytes=64)
 
         load_rows(0)
-        w1_codes, w1_scale_sb = load_weight(nc, const, w1_words, w1_scales, "w1")
+        load_codes(w1_raw, w1_words)
+        load_scales(w1_scale_raw, w1_scales)
         load_rows(1)
-        w2_codes, w2_scale_sb = load_weight(nc, const, w2_words, w2_scales, "w2")
-        for chunk in range(2, CHUNKS):
+        load_codes(w2_codes, w2_words)
+        load_scales(w2_scale_sb, w2_scales)
+        for chunk in range(2, len(CHUNK_TILES)):
             load_rows(chunk)
 
+        warm = const.tile([P, 1], F32, name="warm")
+        nc.gpsimd.memset(warm[:], 0.0)
+        warmed = const.tile([P, 1], F32, name="warmed")
+        nc.scalar.activation(out=warmed[:], in_=warm[:], func=ACT.Exp)
         ident = const.tile([P, P], F32, name="ident")
         make_identity(nc, ident[:])
 
         b1_raw = const.tile([P, BLOCKS, PACK], BF16, name="b1_raw")
         nc.scalar.dma_start(out=b1_raw[:], in_=b1.rearrange("g o (p t) -> p (g o) t", t=PACK))
         b1_col = const.tile([P, BLOCKS * PACK], F32, name="b1_col")
-        nc.vector.tensor_copy(out=b1_col[:], in_=b1_raw[:].rearrange("p g t -> p (g t)"))
         b2_all = const.tile([P, BLOCKS * WIDTH], BF16, name="b2_all")
         nc.scalar.dma_start(out=b2_all[:], in_=b2.rearrange("g o d -> (g o d)").partition_broadcast(P))
 
         x_turned, z_grouped, z_codes, z_scales = {}, {}, {}, {}
-        v_ps, v_sorted, v_turned, grown, kept = {}, {}, {}, {}, {}
-        h_quarters, h_grouped, h_codes, h_scales = {}, {}, {}, {}
+        v_ps, grown, kept = {}, {}, {}
+        h_grouped, h_codes, h_scales = {}, {}, {}
         r_ps, result = {}, {}
 
-        def transpose_x(pair):
-            if not 0 <= pair < PAIRS:
-                return
-            unit, half = divmod(pair, 2)
-            chunk, g = divmod(unit, BLOCKS)
-            x_turned[pair] = psum.tile([P, 2, 2, P], F32, name="x_turned")
-            for a in range(2):
-                x_words = x_sb[chunk][:, 2 * half + a, :].bitcast(F32)
-                for u in range(2):
-                    nc.tensor.transpose(
-                        x_turned[pair][:, a, u, :], x_words[:, WORDS * g + u : WORDS * (g + 1) : 2], ident[:]
-                    )
+        def reorder_w1():
+            for g in range(BLOCKS):
+                nc.vector.tensor_copy(
+                    out=w1_codes[:, g, :].bitcast(I32).rearrange("p (t m) -> p t m", t=PACK),
+                    in_=w1_raw[:, g, :].bitcast(I32).rearrange("p (m t) -> p t m", t=PACK),
+                )
+                nc.vector.tensor_copy(
+                    out=w1_scale_sb[:, g, :].rearrange("p (t m) -> p t m", t=PACK),
+                    in_=w1_scale_raw[:, g, :].rearrange("p (m t) -> p t m", t=PACK),
+                )
 
-        def gather_z(pair):
-            if not 0 <= pair < PAIRS:
+        def halves(unit):
+            return (units[unit][2] + 1) // 2
+
+        def transpose_x(unit):
+            if not 0 <= unit < len(units):
                 return
-            unit, half = divmod(pair, 2)
+            chunk, g, n = units[unit]
+            for half in range(halves(unit)):
+                x_turned[unit, half] = psum_two.tile([P, 2, 2, P], F32, name="x_turned")
+                for a in range(2 * half, min(2 * half + 2, n)):
+                    x_words = x_sb[chunk][:, a, :].bitcast(F32)
+                    for u in range(2):
+                        nc.tensor.transpose(
+                            x_turned[unit, half][:, a % 2, u, :], x_words[:, WORDS * g + u : WORDS * (g + 1) : 2], ident[:]
+                        )
+
+        def gather_z(unit, half):
+            if not 0 <= unit < len(units) or half >= halves(unit):
+                return
+            n = units[unit][2]
             if half == 0:
-                z_grouped[unit] = work.tile([P, GROUP, P, PACK], BF16, name="z_grouped", align_bytes=64)
+                z_grouped[unit] = ahead.tile([P, MOST, P, PACK], BF16, name="z_grouped", align_bytes=64)
             z_words = (
                 z_grouped[unit][:]
                 .rearrange("p a r k -> p (a r k)")
                 .bitcast(F32)
-                .rearrange("p (a r u) -> p a r u", a=GROUP, u=2)
+                .rearrange("p (a r u) -> p a r u", a=MOST, u=2)
             )
+            low, high = 2 * half, min(2 * half + 2, n)
             nc.scalar.copy(
-                out=z_words[:, 2 * half : 2 * half + 2, :, :],
-                in_=x_turned[pair][:].rearrange("p a u r -> p a r u"),
+                out=z_words[:, low:high, :, :],
+                in_=x_turned[unit, half][:, : high - low].rearrange("p a u r -> p a r u"),
             )
 
         def quantise_z(unit):
-            if not 0 <= unit < UNITS:
+            if not 0 <= unit < len(units):
                 return
-            z_codes[unit] = work.tile([P, COLS], U32, name="z_codes", align_bytes=64)
-            z_scales[unit] = work.tile([P, COLS], U8, name="z_scales", align_bytes=64)
+            n = units[unit][2]
+            z_codes[unit] = work.tile([P, MOST * P], U32, name="z_codes", align_bytes=64)
+            z_scales[unit] = work.tile([P, MOST * P], U8, name="z_scales", align_bytes=64)
             nc.vector.quantize_mx(
-                out=z_codes[unit][:].bitcast(FP8X4),
-                scales=z_scales[unit][:],
-                in_=z_grouped[unit][:].rearrange("p a r k -> p (a r k)"),
+                out=z_codes[unit][:, : n * P].bitcast(FP8X4),
+                scales=z_scales[unit][:, : n * P],
+                in_=z_grouped[unit][:, :n].rearrange("p a r k -> p (a r k)"),
             )
 
-        def first_product(item):
-            if not 0 <= item < ITEMS:
+        def first_product(unit, t):
+            if not 0 <= unit < len(units):
                 return
-            unit, a = divmod(item, GROUP)
-            v_ps[item] = psum.tile([P, WIDTH], F32, name="v_ps")
+            chunk, g, n = units[unit]
+            v_ps[unit, t] = psum_two.tile([P, MOST * P], F32, name="v_ps")
             nc.tensor.matmul_mx(
-                out=v_ps[item][:],
-                lhsT=z_codes[unit][:, P * a : P * (a + 1)].bitcast(FP8X4),
-                lhsT_scale=z_scales[unit][:, P * a : P * (a + 1)],
-                rhs=w1_codes[:, unit % BLOCKS, :].bitcast(FP8X4),
-                rhs_scale=w1_scale_sb[:, unit % BLOCKS, :],
+                out=v_ps[unit, t][:, : n * P],
+                lhsT=w1_codes[:, g, P * t : P * (t + 1)].bitcast(FP8X4),
+                lhsT_scale=w1_scale_sb[:, g, P * t : P * (t + 1)],
+                rhs=z_codes[unit][:, : n * P].bitcast(FP8X4),
+                rhs_scale=z_scales[unit][:, : n * P],
                 start=True,
                 stop=True,
             )
 
-        def sort_v(item):
-            if not 0 <= item < ITEMS:
+        def exp_and_relu(unit, t):
+            if not 0 <= unit < len(units):
                 return
-            unit, a = divmod(item, GROUP)
-            if a == 0:
-                v_sorted[unit] = work.tile([P, GROUP, PACK, P], F32, name="v_sorted")
-            nc.scalar.copy(
-                out=v_sorted[unit][:, a, :, :], in_=v_ps[item][:].rearrange("b (p t) -> b t p", t=PACK)
-            )
-
-        def transpose_v(quarter):
-            if not 0 <= quarter < ITEMS:
-                return
-            unit, t = divmod(quarter, PACK)
-            v_turned[quarter] = psum.tile([P, COLS], F32, name="v_turned")
-            for a in range(GROUP):
-                nc.tensor.transpose(
-                    v_turned[quarter][:, P * a : P * (a + 1)], v_sorted[unit][:, a, t, :], ident[:]
-                )
-
-        def exp_and_relu(quarter):
-            if not 0 <= quarter < ITEMS:
-                return
-            unit, t = divmod(quarter, PACK)
+            chunk, g, n = units[unit]
             if t == 0:
-                grown[unit] = work.tile([P, PACK, COLS], F32, name="grown")
-                kept[unit] = work.tile([P, PACK, COLS], F32, name="kept")
-            column = PACK * (unit % BLOCKS) + t
-            bias = b1_col[:, column : column + 1]
-            source = v_turned[quarter][:]
-            nc.scalar.activation(out=grown[unit][:, t, :], in_=source, func=ACT.Exp, bias=bias, scale=1.0)
-            nc.scalar.activation(out=kept[unit][:, t, :], in_=source, func=ACT.Relu, bias=bias, scale=1.0)
+                grown[unit] = work.tile([P, PACK, MOST * P], F32, name="grown")
+                kept[unit] = work.tile([P, PACK, MOST * P], BF16, name="kept")
+            bias = b1_col[:, PACK * g + t : PACK * g + t + 1]
+            source = v_ps[unit, t][:, : n * P]
+            nc.scalar.activation(out=grown[unit][:, t, : n * P], in_=source, func=ACT.Exp, bias=bias, scale=1.0)
+            nc.scalar.activation(out=kept[unit][:, t, : n * P], in_=source, func=ACT.Relu, bias=bias, scale=1.0)
 
-        def join(quarter):
-            if not 0 <= quarter < ITEMS:
+        def join(unit):
+            if not 0 <= unit < len(units):
                 return
-            unit, t = divmod(quarter, PACK)
-            if t == 0:
-                h_quarters[unit] = work.tile([P, PACK, COLS], BF16, name="h_quarters")
+            n = units[unit][2]
+            h_grouped[unit] = work.tile([P, MOST * P, PACK], BF16, name="h_grouped", align_bytes=64)
             nc.vector.scalar_tensor_tensor(
-                out=h_quarters[unit][:, t, :],
-                in0=grown[unit][:, t, :],
+                out=h_grouped[unit][:, : n * P, :],
+                in0=grown[unit][:, :, : n * P].rearrange("p t w -> p w t"),
                 scalar=-1.0,
-                in1=kept[unit][:, t, :],
+                in1=kept[unit][:, :, : n * P].rearrange("p t w -> p w t"),
                 op0=ALU.add,
                 op1=ALU.min,
             )
 
-        def regroup(unit):
-            if not 0 <= unit < UNITS:
-                return
-            h_grouped[unit] = work.tile([P, COLS, PACK], BF16, name="h_grouped", align_bytes=64)
-            nc.gpsimd.tensor_scalar(
-                out=h_grouped[unit][:],
-                in0=h_quarters[unit][:].rearrange("p t w -> p w t"),
-                scalar1=1.0,
-                scalar2=0.0,
-                op0=ALU.mult,
-                op1=ALU.add,
-            )
-
         def quantise_h(unit):
-            if not 0 <= unit < UNITS:
+            if not 0 <= unit < len(units):
                 return
-            h_codes[unit] = work.tile([P, COLS], U32, name="h_codes", align_bytes=64)
-            h_scales[unit] = work.tile([P, COLS], U8, name="h_scales", align_bytes=64)
+            n = units[unit][2]
+            h_codes[unit] = work.tile([P, MOST * P], U32, name="h_codes", align_bytes=64)
+            h_scales[unit] = work.tile([P, MOST * P], U8, name="h_scales", align_bytes=64)
             nc.vector.quantize_mx(
-                out=h_codes[unit][:].bitcast(FP8X4),
-                scales=h_scales[unit][:],
-                in_=h_grouped[unit][:].rearrange("p w t -> p (w t)"),
+                out=h_codes[unit][:, : n * P].bitcast(FP8X4),
+                scales=h_scales[unit][:, : n * P],
+                in_=h_grouped[unit][:, : n * P, :].rearrange("p w t -> p (w t)"),
             )
 
-        def second_product(item):
-            if not 0 <= item < ITEMS:
+        def second_product(unit):
+            if not 0 <= unit < len(units):
                 return
-            unit, a = divmod(item, GROUP)
-            r_ps[item] = psum.tile([P, WIDTH], F32, name="r_ps")
-            nc.tensor.matmul_mx(
-                out=r_ps[item][:],
-                lhsT=h_codes[unit][:, P * a : P * (a + 1)].bitcast(FP8X4),
-                lhsT_scale=h_scales[unit][:, P * a : P * (a + 1)],
-                rhs=w2_codes[:, unit % BLOCKS, :].bitcast(FP8X4),
-                rhs_scale=w2_scale_sb[:, unit % BLOCKS, :],
-                start=True,
-                stop=True,
+            chunk, g, n = units[unit]
+            for a in range(n):
+                r_ps[unit, a] = psum_four.tile([P, WIDTH], F32, name="r_ps")
+                nc.tensor.matmul_mx(
+                    out=r_ps[unit, a][:],
+                    lhsT=h_codes[unit][:, P * a : P * (a + 1)].bitcast(FP8X4),
+                    lhsT_scale=h_scales[unit][:, P * a : P * (a + 1)],
+                    rhs=w2_codes[:, g, :].bitcast(FP8X4),
+                    rhs_scale=w2_scale_sb[:, g, :],
+                    start=True,
+                    stop=True,
+                )
+
+        def add_b2(tile_index):
+            chunk = max(c for c in range(len(CHUNK_TILES)) if firsts[c] <= tile_index)
+            result[tile_index] = results.tile([P, BLOCKS * WIDTH], F32, name="result")
+            nc.vector.tensor_tensor(
+                out=result[tile_index][:], in0=x_sb[chunk][:, tile_index - firsts[chunk], :], in1=b2_all[:], op=ALU.add
             )
 
-        def add_b2(batch_tile):
-            if not 0 <= batch_tile < TILES:
+        def finish(unit):
+            if not 0 <= unit < len(units):
                 return
-            chunk, a = divmod(batch_tile, GROUP)
-            if a == 0:
-                result[chunk] = results.tile([P, GROUP, BLOCKS * WIDTH], F32, name="result")
-            nc.vector.tensor_tensor(out=result[chunk][:, a, :], in0=x_sb[chunk][:, a, :], in1=b2_all[:], op=ALU.add)
-
-        def finish(item):
-            if not 0 <= item < ITEMS:
-                return
-            unit, a = divmod(item, GROUP)
-            chunk, g = divmod(unit, BLOCKS)
+            chunk, g, n = units[unit]
             columns = slice(WIDTH * g, WIDTH * (g + 1))
-            block = result[chunk][:, a, columns]
-            nc.vector.tensor_tensor(out=block, in0=r_ps[item][:], in1=block, op=ALU.add)
-            nc.sync.dma_start(out=out_view[:, GROUP * chunk + a, columns], in_=block)
+            for a in range(n):
+                block = result[firsts[chunk] + a][:, columns]
+                nc.vector.tensor_tensor(out=block, in0=r_ps[unit, a][:], in1=block, op=ALU.add)
+                nc.sync.dma_start(out=out_view[:, firsts[chunk] + a, columns], in_=block)
 
-        for slot in range(-X_LEAD, LAST_SLOT + 1):
-            phase = slot % GROUP
-            unit_now = slot // GROUP
-            ending = GROUP * (unit_now - END_UNITS)
-            transpose_v(slot + TURN_LEAD)
-            if slot % 2 == 0:
-                transpose_x((slot + X_LEAD) // 2)
-            first_product(slot + V_LEAD)
-            sort_v(slot + SORT_LEAD)
-            exp_and_relu(slot)
-            if slot % 2 == 0:
-                gather_z((slot + Z_LEAD) // 2)
-            join(slot - JOIN_LAG)
-            if phase == 0:
-                regroup(unit_now - 1)
-                finish(ending)
-                finish(ending + 1)
-                second_product(ending + 2)
-                second_product(ending + 3)
-                finish(ending + 2)
-                finish(ending + 3)
-            if phase == 1:
-                quantise_h(unit_now - 1)
-            if phase == 2:
-                second_product(ending + GROUP)
-                second_product(ending + GROUP + 1)
-            if phase == 3:
-                quantise_z(unit_now + Z_LEAD // GROUP)
-            if phase >= 2:
-                add_b2(2 * (unit_now + B2_LEAD // GROUP) + phase - 2)
+        def tiles_due(unit):
+            if unit >= len(units):
+                return TILES
+            chunk, g, n = units[unit]
+            return firsts[chunk] + (g + 1) * n // BLOCKS
+
+        added = 0
+        for k in range(-3, len(units)):
+            transpose_x(k + 3)
+            exp_and_relu(k + 1, 0)
+            first_product(k + 1, 2)
+            exp_and_relu(k + 1, 1)
+            first_product(k + 1, 3)
+            gather_z(k + 3, 0)
+            join(k)
+            if k == -2:
+                nc.vector.tensor_copy(out=b1_col[:], in_=b1_raw[:].rearrange("p g t -> p (g t)"))
+                reorder_w1()
+            quantise_z(k + 2)
+            quantise_h(k)
+            if k >= -1:
+                while added < tiles_due(k + ADD_LEAD):
+                    add_b2(added)
+                    added += 1
+            second_product(k)
+            exp_and_relu(k + 1, 2)
+            first_product(k + 2, 0)
+            gather_z(k + 3, 1)
+            exp_and_relu(k + 1, 3)
+            first_product(k + 2, 1)
+            finish(k)

@@ -21,9 +21,13 @@ WIDTH = 512
 WORDS = WIDTH // 2
 TILES = BATCH // P
 MOST = 4
-CHUNK_TILES = [2, 2, 4, 4, 4, 4, 4, 4, 2, 2]
+CHUNK_TILES = [2, 4, 4, 4, 4, 4, 4, 4, 2]
+TURNED = 1
 RESULT_BUFS = 16
-ADD_LEAD = 4
+VECTOR_HEAD = 4
+PER_WINDOW = 2
+VG_MOD = 1
+VG_SET = ()
 
 FLOPS = 2 * BATCH * WIDTH * WIDTH * BLOCKS * 2
 
@@ -34,11 +38,17 @@ def tile_blockresmlp_mixerblock_pb_t_e_kernel(
     nc = tc.nc
     firsts = [sum(CHUNK_TILES[:c]) for c in range(len(CHUNK_TILES))]
     units = [(c, g, n) for c, n in enumerate(CHUNK_TILES) for g in range(BLOCKS)]
+
+    def turned(unit):
+        chunk, g, n = units[unit]
+        return g == TURNED and n == MOST
+
     with ExitStack() as ctx:
         ctx.enter_context(tc.manual_schedule())
         const = ctx.enter_context(tc.tile_pool(name="const", bufs=1))
         results = ctx.enter_context(tc.tile_pool(name="results", bufs=RESULT_BUFS))
-        ahead = ctx.enter_context(tc.tile_pool(name="ahead", bufs=3))
+        ahead = ctx.enter_context(tc.tile_pool(name="ahead", bufs=5))
+        stage = ctx.enter_context(tc.tile_pool(name="stage", bufs=8))
         work = ctx.enter_context(tc.tile_pool(name="work", bufs=2))
         psum_two = ctx.enter_context(tc.psum_pool(name="psum_two", bufs=2))
         psum_four = ctx.enter_context(tc.psum_pool(name="psum_four", bufs=4))
@@ -74,6 +84,8 @@ def tile_blockresmlp_mixerblock_pb_t_e_kernel(
         w1_scale_sb = const.tile([P, BLOCKS, WIDTH], U8, name="w1_scale_sb", align_bytes=64)
         w2_codes = const.tile([P, BLOCKS, WIDTH], U32, name="w2_codes", align_bytes=64)
         w2_scale_sb = const.tile([P, BLOCKS, WIDTH], U8, name="w2_scale_sb", align_bytes=64)
+        w2_turned = const.tile([P, WIDTH], U32, name="w2_turned", align_bytes=64)
+        w2_turned_scale = const.tile([P, WIDTH], U8, name="w2_turned_scale", align_bytes=64)
 
         load_rows(0)
         load_codes(w1_raw, w1_words)
@@ -88,6 +100,7 @@ def tile_blockresmlp_mixerblock_pb_t_e_kernel(
         nc.gpsimd.memset(warm[:], 0.0)
         warmed = const.tile([P, 1], F32, name="warmed")
         nc.scalar.activation(out=warmed[:], in_=warm[:], func=ACT.Exp)
+        cue_sb = const.tile([P, 32], BF16, name="cue_sb")
         ident = const.tile([P, P], F32, name="ident")
         make_identity(nc, ident[:])
 
@@ -96,22 +109,24 @@ def tile_blockresmlp_mixerblock_pb_t_e_kernel(
         b1_col = const.tile([P, BLOCKS * PACK], F32, name="b1_col")
         b2_all = const.tile([P, BLOCKS * WIDTH], BF16, name="b2_all")
         nc.scalar.dma_start(out=b2_all[:], in_=b2.rearrange("g o d -> (g o d)").partition_broadcast(P))
+        b2_raw = const.tile([P, PACK], BF16, name="b2_raw")
+        nc.scalar.dma_start(out=b2_raw[:], in_=b2[1].rearrange("o (p t) -> p (o t)", t=PACK))
+        b2_col = const.tile([P, PACK], F32, name="b2_col")
 
         x_turned, z_grouped, z_codes, z_scales = {}, {}, {}, {}
         v_ps, grown, kept = {}, {}, {}
         h_grouped, h_codes, h_scales = {}, {}, {}
-        r_ps, result = {}, {}
+        r_ps, result, r_turned = {}, {}, {}
 
-        def reorder_w1():
-            for g in range(BLOCKS):
-                nc.vector.tensor_copy(
-                    out=w1_codes[:, g, :].bitcast(I32).rearrange("p (t m) -> p t m", t=PACK),
-                    in_=w1_raw[:, g, :].bitcast(I32).rearrange("p (m t) -> p t m", t=PACK),
-                )
-                nc.vector.tensor_copy(
-                    out=w1_scale_sb[:, g, :].rearrange("p (t m) -> p t m", t=PACK),
-                    in_=w1_scale_raw[:, g, :].rearrange("p (m t) -> p t m", t=PACK),
-                )
+        def reorder(codes_to, scale_to, codes_from, scale_from):
+            nc.vector.tensor_copy(
+                out=codes_to.bitcast(I32).rearrange("p (t m) -> p t m", t=PACK),
+                in_=codes_from.bitcast(I32).rearrange("p (m t) -> p t m", t=PACK),
+            )
+            nc.vector.tensor_copy(
+                out=scale_to.rearrange("p (t m) -> p t m", t=PACK),
+                in_=scale_from.rearrange("p (m t) -> p t m", t=PACK),
+            )
 
         def halves(unit):
             return (units[unit][2] + 1) // 2
@@ -129,6 +144,9 @@ def tile_blockresmlp_mixerblock_pb_t_e_kernel(
                             x_turned[unit, half][:, a % 2, u, :], x_words[:, WORDS * g + u : WORDS * (g + 1) : 2], ident[:]
                         )
 
+        def on_vector(unit, half):
+            return half == 1 and unit % VG_MOD in VG_SET
+
         def gather_z(unit, half):
             if not 0 <= unit < len(units) or half >= halves(unit):
                 return
@@ -142,7 +160,8 @@ def tile_blockresmlp_mixerblock_pb_t_e_kernel(
                 .rearrange("p (a r u) -> p a r u", a=MOST, u=2)
             )
             low, high = 2 * half, min(2 * half + 2, n)
-            nc.scalar.copy(
+            copy = nc.vector.tensor_copy if on_vector(unit, half) else nc.scalar.copy
+            copy(
                 out=z_words[:, low:high, :, :],
                 in_=x_turned[unit, half][:, : high - low].rearrange("p a u r -> p a r u"),
             )
@@ -216,6 +235,19 @@ def tile_blockresmlp_mixerblock_pb_t_e_kernel(
             if not 0 <= unit < len(units):
                 return
             chunk, g, n = units[unit]
+            if turned(unit):
+                for t in range(PACK):
+                    r_ps[unit, t] = psum_four.tile([P, WIDTH], F32, name="r_ps")
+                    nc.tensor.matmul_mx(
+                        out=r_ps[unit, t][:, : n * P],
+                        lhsT=w2_turned[:, P * t : P * (t + 1)].bitcast(FP8X4),
+                        lhsT_scale=w2_turned_scale[:, P * t : P * (t + 1)],
+                        rhs=h_codes[unit][:, : n * P].bitcast(FP8X4),
+                        rhs_scale=h_scales[unit][:, : n * P],
+                        start=True,
+                        stop=True,
+                    )
+                return
             for a in range(n):
                 r_ps[unit, a] = psum_four.tile([P, WIDTH], F32, name="r_ps")
                 nc.tensor.matmul_mx(
@@ -228,51 +260,108 @@ def tile_blockresmlp_mixerblock_pb_t_e_kernel(
                     stop=True,
                 )
 
-        def add_b2(tile_index):
-            chunk = max(c for c in range(len(CHUNK_TILES)) if firsts[c] <= tile_index)
-            result[tile_index] = results.tile([P, BLOCKS * WIDTH], F32, name="result")
-            nc.vector.tensor_tensor(
-                out=result[tile_index][:], in0=x_sb[chunk][:, tile_index - firsts[chunk], :], in1=b2_all[:], op=ALU.add
+        def cue(unit):
+            if not 0 <= unit < len(units):
+                return
+            nc.gpsimd.tensor_copy(out=cue_sb[:, unit : unit + 1], in_=h_grouped[unit][:, 0, :1])
+
+        def add_b2(unit, a):
+            chunk, g, n = units[unit]
+            columns = slice(WIDTH * g, WIDTH * (g + 1))
+            result[unit, a] = results.tile([P, WIDTH], F32, name="result")
+            engine = nc.vector if len(added) < VECTOR_HEAD else nc.gpsimd
+            engine.tensor_tensor(
+                out=result[unit, a][:], in0=x_sb[chunk][:, a, columns], in1=b2_all[:, columns], op=ALU.add
             )
 
         def finish(unit):
             if not 0 <= unit < len(units):
                 return
             chunk, g, n = units[unit]
-            columns = slice(WIDTH * g, WIDTH * (g + 1))
+            if turned(unit):
+                r_turned[unit] = work.tile([P, PACK, MOST * P], F32, name="r_turned")
+                z_rows = z_grouped[unit][:].rearrange("p a r k -> p (a r) k")
+                for t in range(PACK):
+                    nc.vector.scalar_tensor_tensor(
+                        out=r_turned[unit][:, t, : n * P],
+                        in0=r_ps[unit, t][:, : n * P],
+                        scalar=b2_col[:, t : t + 1],
+                        in1=z_rows[:, : n * P, t],
+                        op0=ALU.add,
+                        op1=ALU.add,
+                    )
+                return
             for a in range(n):
-                block = result[firsts[chunk] + a][:, columns]
+                block = result[unit, a][:]
                 nc.vector.tensor_tensor(out=block, in0=r_ps[unit, a][:], in1=block, op=ALU.add)
-                nc.sync.dma_start(out=out_view[:, firsts[chunk] + a, columns], in_=block)
+                nc.sync.dma_start(out=out_view[:, firsts[chunk] + a, WIDTH * g : WIDTH * (g + 1)], in_=block)
 
-        def tiles_due(unit):
-            if unit >= len(units):
-                return TILES
+        def turn_back(unit):
+            if not 0 <= unit < len(units) or not turned(unit):
+                return
+            for a in range(units[unit][2]):
+                r_ps[unit, PACK + a] = psum_four.tile([P, PACK, P], F32, name="r_ps")
+                for t in range(PACK):
+                    nc.tensor.transpose(
+                        r_ps[unit, PACK + a][:, t, :], r_turned[unit][:, t, P * a : P * (a + 1)], ident[:]
+                    )
+
+        def copy_and_store(unit, low=0, high=MOST):
+            if not 0 <= unit < len(units) or not turned(unit):
+                return
             chunk, g, n = units[unit]
-            return firsts[chunk] + (g + 1) * n // BLOCKS
+            for a in range(low, min(high, n)):
+                rows = stage.tile([P, P, PACK], F32, name="rows")
+                nc.scalar.copy(out=rows[:], in_=r_ps[unit, PACK + a][:].rearrange("b t p -> b p t"))
+                nc.sync.dma_start(
+                    out=out_view[:, firsts[chunk] + a, WIDTH * g : WIDTH * (g + 1)], in_=rows[:].rearrange("b p t -> b (p t)")
+                )
 
-        added = 0
-        for k in range(-3, len(units)):
+        to_add = [(u, a) for u in range(len(units)) if not turned(u) for a in range(units[u][2])]
+        added = []
+
+        def adds_due(unit):
+            done = sum(units[u][2] for u in range(min(unit + 1, len(units))))
+            return min(len(to_add), VECTOR_HEAD + max(0, (unit + 1) * PER_WINDOW))
+
+        for k in range(-3, len(units) + 2):
+            copy_and_store(k - 2)
+            second_product(k - 1)
             transpose_x(k + 3)
+            if k == -2:
+                nc.vector.tensor_copy(out=b1_col[:], in_=b1_raw[:].rearrange("p g t -> p (g t)"))
+                nc.vector.tensor_copy(out=b2_col[:], in_=b2_raw[:])
+                reorder(w1_codes[:, 0, :], w1_scale_sb[:, 0, :], w1_raw[:, 0, :], w1_scale_raw[:, 0, :])
+            quantise_z(k + 2)
+            if k == -2:
+                reorder(w1_codes[:, 1, :], w1_scale_sb[:, 1, :], w1_raw[:, 1, :], w1_scale_raw[:, 1, :])
             exp_and_relu(k + 1, 0)
             first_product(k + 1, 2)
             exp_and_relu(k + 1, 1)
             first_product(k + 1, 3)
             gather_z(k + 3, 0)
+            if k == -1:
+                while len(added) < VECTOR_HEAD:
+                    pair = to_add[len(added)]
+                    add_b2(pair[0], pair[1])
+                    added.append(pair)
             join(k)
-            if k == -2:
-                nc.vector.tensor_copy(out=b1_col[:], in_=b1_raw[:].rearrange("p g t -> p (g t)"))
-                reorder_w1()
-            quantise_z(k + 2)
+            if k == 0:
+                reorder(w2_turned[:], w2_turned_scale[:], w2_codes[:, TURNED, :], w2_scale_sb[:, TURNED, :])
+            finish(k - 1)
+            if k >= 0:
+                cue(k)
+                while len(added) < adds_due(k):
+                    pair = to_add[len(added)]
+                    add_b2(pair[0], pair[1])
+                    added.append(pair)
+            if on_vector(k + 3, 1):
+                gather_z(k + 3, 1)
             quantise_h(k)
-            if k >= -1:
-                while added < tiles_due(k + ADD_LEAD):
-                    add_b2(added)
-                    added += 1
-            second_product(k)
             exp_and_relu(k + 1, 2)
             first_product(k + 2, 0)
-            gather_z(k + 3, 1)
+            if not on_vector(k + 3, 1):
+                gather_z(k + 3, 1)
             exp_and_relu(k + 1, 3)
+            turn_back(k - 1)
             first_product(k + 2, 1)
-            finish(k)

@@ -24,10 +24,11 @@ MOST = 4
 CHUNK_TILES = [2, 4, 4, 4, 4, 4, 4, 4, 2]
 TURNED = 1
 RESULT_BUFS = 16
-VECTOR_HEAD = 4
+W2_AT = 0
+VECTOR_HEAD = 8
 PER_WINDOW = 2
-VG_MOD = 1
-VG_SET = ()
+VG_MOD = 3
+VG_SET = (1,)
 
 FLOPS = 2 * BATCH * WIDTH * WIDTH * BLOCKS * 2
 
@@ -88,8 +89,8 @@ def tile_blockresmlp_mixerblock_pb_t_e_kernel(
         w2_turned_scale = const.tile([P, WIDTH], U8, name="w2_turned_scale", align_bytes=64)
 
         load_rows(0)
-        load_codes(w1_raw, w1_words)
         load_scales(w1_scale_raw, w1_scales)
+        load_codes(w1_raw, w1_words)
         load_rows(1)
         load_codes(w2_codes, w2_words)
         load_scales(w2_scale_sb, w2_scales)
@@ -152,19 +153,18 @@ def tile_blockresmlp_mixerblock_pb_t_e_kernel(
                 return
             n = units[unit][2]
             if half == 0:
-                z_grouped[unit] = ahead.tile([P, MOST, P, PACK], BF16, name="z_grouped", align_bytes=64)
-            z_words = (
-                z_grouped[unit][:]
-                .rearrange("p a r k -> p (a r k)")
-                .bitcast(F32)
-                .rearrange("p (a r u) -> p a r u", a=MOST, u=2)
-            )
+                z_grouped[unit] = ahead.tile([P, MOST * P * PACK], BF16, name="z_grouped", align_bytes=64)
+            z_words = z_grouped[unit][:].bitcast(F32)
             low, high = 2 * half, min(2 * half + 2, n)
+            turned_words = x_turned[unit, half][:, : high - low]
+            if n == MOST:
+                out_words = z_words.rearrange("p (r a u) -> p r a u", a=MOST, u=2)[:, :, low:high, :]
+                in_words = turned_words.rearrange("p a u r -> p r a u")
+            else:
+                out_words = z_words.rearrange("p (a r u) -> p a r u", r=P, u=2)[:, low:high]
+                in_words = turned_words.rearrange("p a u r -> p a r u")
             copy = nc.vector.tensor_copy if on_vector(unit, half) else nc.scalar.copy
-            copy(
-                out=z_words[:, low:high, :, :],
-                in_=x_turned[unit, half][:, : high - low].rearrange("p a u r -> p a r u"),
-            )
+            copy(out=out_words, in_=in_words)
 
         def quantise_z(unit):
             if not 0 <= unit < len(units):
@@ -175,7 +175,7 @@ def tile_blockresmlp_mixerblock_pb_t_e_kernel(
             nc.vector.quantize_mx(
                 out=z_codes[unit][:, : n * P].bitcast(FP8X4),
                 scales=z_scales[unit][:, : n * P],
-                in_=z_grouped[unit][:, :n].rearrange("p a r k -> p (a r k)"),
+                in_=z_grouped[unit][:, : n * P * PACK],
             )
 
         def first_product(unit, t):
@@ -193,30 +193,38 @@ def tile_blockresmlp_mixerblock_pb_t_e_kernel(
                 stop=True,
             )
 
+        def quarter(values, n, t):
+            if n == MOST:
+                return values[:].rearrange("p (r t a) -> p r t a", t=PACK, a=MOST)[:, :, t, :]
+            return values[:, n * P * t : n * P * (t + 1)]
+
         def exp_and_relu(unit, t):
             if not 0 <= unit < len(units):
                 return
             chunk, g, n = units[unit]
             if t == 0:
-                grown[unit] = work.tile([P, PACK, MOST * P], F32, name="grown")
-                kept[unit] = work.tile([P, PACK, MOST * P], BF16, name="kept")
+                grown[unit] = work.tile([P, PACK * MOST * P], F32, name="grown")
+                kept[unit] = work.tile([P, PACK * MOST * P], F32, name="kept")
             bias = b1_col[:, PACK * g + t : PACK * g + t + 1]
             source = v_ps[unit, t][:, : n * P]
-            nc.scalar.activation(out=grown[unit][:, t, : n * P], in_=source, func=ACT.Exp, bias=bias, scale=1.0)
-            nc.scalar.activation(out=kept[unit][:, t, : n * P], in_=source, func=ACT.Relu, bias=bias, scale=1.0)
+            if n == MOST:
+                source = source.rearrange("p (r a) -> p r a", a=MOST)
+            nc.scalar.activation(out=quarter(grown[unit], n, t), in_=source, func=ACT.Exp, bias=bias, scale=1.0)
+            nc.scalar.activation(out=quarter(kept[unit], n, t), in_=source, func=ACT.Relu, bias=bias, scale=1.0)
 
         def join(unit):
             if not 0 <= unit < len(units):
                 return
             n = units[unit][2]
             h_grouped[unit] = work.tile([P, MOST * P, PACK], BF16, name="h_grouped", align_bytes=64)
+            if n == MOST:
+                out_view_h = h_grouped[unit][:].rearrange("p (a r) t -> p (r t) a", a=MOST)
+                sides = [values[:].rearrange("p (r t a) -> p (r t) a", t=PACK, a=MOST) for values in (grown[unit], kept[unit])]
+            else:
+                out_view_h = h_grouped[unit][:, : n * P, :]
+                sides = [values[:, : n * P * PACK].rearrange("p (t w) -> p w t", t=PACK) for values in (grown[unit], kept[unit])]
             nc.vector.scalar_tensor_tensor(
-                out=h_grouped[unit][:, : n * P, :],
-                in0=grown[unit][:, :, : n * P].rearrange("p t w -> p w t"),
-                scalar=-1.0,
-                in1=kept[unit][:, :, : n * P].rearrange("p t w -> p w t"),
-                op0=ALU.add,
-                op1=ALU.min,
+                out=out_view_h, in0=sides[0], scalar=-1.0, in1=sides[1], op0=ALU.add, op1=ALU.min
             )
 
         def quantise_h(unit):
@@ -280,13 +288,13 @@ def tile_blockresmlp_mixerblock_pb_t_e_kernel(
             chunk, g, n = units[unit]
             if turned(unit):
                 r_turned[unit] = work.tile([P, PACK, MOST * P], F32, name="r_turned")
-                z_rows = z_grouped[unit][:].rearrange("p a r k -> p (a r) k")
+                z_rows = z_grouped[unit][:].rearrange("p (r a k) -> p k a r", a=MOST, k=PACK)
                 for t in range(PACK):
                     nc.vector.scalar_tensor_tensor(
-                        out=r_turned[unit][:, t, : n * P],
-                        in0=r_ps[unit, t][:, : n * P],
+                        out=r_turned[unit][:, t, :].rearrange("p (a r) -> p a r", a=MOST),
+                        in0=r_ps[unit, t][:].rearrange("p (a r) -> p a r", a=MOST),
                         scalar=b2_col[:, t : t + 1],
-                        in1=z_rows[:, : n * P, t],
+                        in1=z_rows[:, t],
                         op0=ALU.add,
                         op1=ALU.add,
                     )
@@ -330,7 +338,6 @@ def tile_blockresmlp_mixerblock_pb_t_e_kernel(
             transpose_x(k + 3)
             if k == -2:
                 nc.vector.tensor_copy(out=b1_col[:], in_=b1_raw[:].rearrange("p g t -> p (g t)"))
-                nc.vector.tensor_copy(out=b2_col[:], in_=b2_raw[:])
                 reorder(w1_codes[:, 0, :], w1_scale_sb[:, 0, :], w1_raw[:, 0, :], w1_scale_raw[:, 0, :])
             quantise_z(k + 2)
             if k == -2:
@@ -346,7 +353,8 @@ def tile_blockresmlp_mixerblock_pb_t_e_kernel(
                     add_b2(pair[0], pair[1])
                     added.append(pair)
             join(k)
-            if k == 0:
+            if k == W2_AT:
+                nc.vector.tensor_copy(out=b2_col[:], in_=b2_raw[:])
                 reorder(w2_turned[:], w2_turned_scale[:], w2_codes[:, TURNED, :], w2_scale_sb[:, TURNED, :])
             finish(k - 1)
             if k >= 0:

@@ -288,11 +288,11 @@ def tile_blockresmlp_mixerblock_pb_t_e_kernel(
             chunk, g, n = units[unit]
             if turned(unit):
                 r_turned[unit] = work.tile([P, PACK, MOST * P], F32, name="r_turned")
-                z_rows = z_grouped[unit][:].rearrange("p (r a k) -> p k a r", a=MOST, k=PACK)
+                z_rows = z_grouped[unit][:].rearrange("p (r a k) -> p k r a", a=MOST, k=PACK)
                 for t in range(PACK):
                     nc.vector.scalar_tensor_tensor(
-                        out=r_turned[unit][:, t, :].rearrange("p (a r) -> p a r", a=MOST),
-                        in0=r_ps[unit, t][:].rearrange("p (a r) -> p a r", a=MOST),
+                        out=r_turned[unit][:, t, :].rearrange("p (a r) -> p r a", a=MOST),
+                        in0=r_ps[unit, t][:].rearrange("p (a r) -> p r a", a=MOST),
                         scalar=b2_col[:, t : t + 1],
                         in1=z_rows[:, t],
                         op0=ALU.add,

@@ -27,8 +27,8 @@ RESULT_BUFS = 16
 W2_AT = 0
 VECTOR_HEAD = 8
 PER_WINDOW = 2
-VG_MOD = 3
-VG_SET = (1,)
+VG_MOD = 1
+VG_SET = ()
 
 FLOPS = 2 * BATCH * WIDTH * WIDTH * BLOCKS * 2
 
@@ -132,27 +132,26 @@ def tile_blockresmlp_mixerblock_pb_t_e_kernel(
         def halves(unit):
             return (units[unit][2] + 1) // 2
 
-        def transpose_x(unit):
-            if not 0 <= unit < len(units):
+        def transpose_x(unit, half):
+            if not 0 <= unit < len(units) or half >= halves(unit):
                 return
             chunk, g, n = units[unit]
-            for half in range(halves(unit)):
-                x_turned[unit, half] = psum_two.tile([P, 2, 2, P], F32, name="x_turned")
-                for a in range(2 * half, min(2 * half + 2, n)):
-                    x_words = x_sb[chunk][:, a, :].bitcast(F32)
-                    for u in range(2):
-                        nc.tensor.transpose(
-                            x_turned[unit, half][:, a % 2, u, :], x_words[:, WORDS * g + u : WORDS * (g + 1) : 2], ident[:]
-                        )
+            x_turned[unit, half] = psum_two.tile([P, 2, 2, P], F32, name="x_turned")
+            for a in range(2 * half, min(2 * half + 2, n)):
+                x_words = x_sb[chunk][:, a, :].bitcast(F32)
+                for u in range(2):
+                    nc.tensor.transpose(
+                        x_turned[unit, half][:, a % 2, u, :], x_words[:, WORDS * g + u : WORDS * (g + 1) : 2], ident[:]
+                    )
 
         def on_vector(unit, half):
-            return half == 1 and unit % VG_MOD in VG_SET
+            return half == 0 and unit >= 3 and unit % VG_MOD in VG_SET
 
         def gather_z(unit, half):
             if not 0 <= unit < len(units) or half >= halves(unit):
                 return
             n = units[unit][2]
-            if half == 0:
+            if unit not in z_grouped:
                 z_grouped[unit] = ahead.tile([P, MOST * P * PACK], BF16, name="z_grouped", align_bytes=64)
             z_words = z_grouped[unit][:].bitcast(F32)
             low, high = 2 * half, min(2 * half + 2, n)
@@ -335,7 +334,6 @@ def tile_blockresmlp_mixerblock_pb_t_e_kernel(
         for k in range(-3, len(units) + 2):
             copy_and_store(k - 2)
             second_product(k - 1)
-            transpose_x(k + 3)
             if k == -2:
                 nc.vector.tensor_copy(out=b1_col[:], in_=b1_raw[:].rearrange("p g t -> p (g t)"))
                 reorder(w1_codes[:, 0, :], w1_scale_sb[:, 0, :], w1_raw[:, 0, :], w1_scale_raw[:, 0, :])
@@ -344,9 +342,10 @@ def tile_blockresmlp_mixerblock_pb_t_e_kernel(
                 reorder(w1_codes[:, 1, :], w1_scale_sb[:, 1, :], w1_raw[:, 1, :], w1_scale_raw[:, 1, :])
             exp_and_relu(k + 1, 0)
             first_product(k + 1, 2)
+            transpose_x(k + 3, 0)
             exp_and_relu(k + 1, 1)
             first_product(k + 1, 3)
-            gather_z(k + 3, 0)
+            transpose_x(k + 3, 1)
             if k == -1:
                 while len(added) < VECTOR_HEAD:
                     pair = to_add[len(added)]
@@ -363,13 +362,14 @@ def tile_blockresmlp_mixerblock_pb_t_e_kernel(
                     pair = to_add[len(added)]
                     add_b2(pair[0], pair[1])
                     added.append(pair)
-            if on_vector(k + 3, 1):
-                gather_z(k + 3, 1)
+            if on_vector(k + 3, 0):
+                gather_z(k + 3, 0)
             quantise_h(k)
             exp_and_relu(k + 1, 2)
             first_product(k + 2, 0)
-            if not on_vector(k + 3, 1):
-                gather_z(k + 3, 1)
+            if not on_vector(k + 3, 0):
+                gather_z(k + 3, 0)
             exp_and_relu(k + 1, 3)
+            gather_z(k + 3, 1)
             turn_back(k - 1)
             first_product(k + 2, 1)

@@ -25,10 +25,10 @@ CHUNK_TILES = [2, 4, 4, 4, 4, 4, 4, 4, 2]
 TURNED = 1
 RESULT_BUFS = 16
 W2_AT = 0
-VECTOR_HEAD = 8
+VECTOR_HEAD = 12
 PER_WINDOW = 2
-VG_MOD = 1
-VG_SET = ()
+VG_MOD = 2
+VG_SET = (0,)
 
 FLOPS = 2 * BATCH * WIDTH * WIDTH * BLOCKS * 2
 
@@ -42,7 +42,7 @@ def tile_blockresmlp_mixerblock_pb_t_e_kernel(
 
     def turned(unit):
         chunk, g, n = units[unit]
-        return g == TURNED and n == MOST
+        return g == TURNED and n == MOST and 1 < chunk < 7
 
     with ExitStack() as ctx:
         ctx.enter_context(tc.manual_schedule())
@@ -337,7 +337,8 @@ def tile_blockresmlp_mixerblock_pb_t_e_kernel(
             if k == -2:
                 nc.vector.tensor_copy(out=b1_col[:], in_=b1_raw[:].rearrange("p g t -> p (g t)"))
                 reorder(w1_codes[:, 0, :], w1_scale_sb[:, 0, :], w1_raw[:, 0, :], w1_scale_raw[:, 0, :])
-            quantise_z(k + 2)
+            if k < 0:
+                quantise_z(k + 2)
             if k == -2:
                 reorder(w1_codes[:, 1, :], w1_scale_sb[:, 1, :], w1_raw[:, 1, :], w1_scale_raw[:, 1, :])
             exp_and_relu(k + 1, 0)
@@ -352,6 +353,8 @@ def tile_blockresmlp_mixerblock_pb_t_e_kernel(
                     add_b2(pair[0], pair[1])
                     added.append(pair)
             join(k)
+            if k >= 0:
+                quantise_z(k + 2)
             if k == W2_AT:
                 nc.vector.tensor_copy(out=b2_col[:], in_=b2_raw[:])
                 reorder(w2_turned[:], w2_turned_scale[:], w2_codes[:, TURNED, :], w2_scale_sb[:, TURNED, :])

@@ -22,13 +22,11 @@ WORDS = WIDTH // 2
 TILES = BATCH // P
 MOST = 4
 CHUNK_TILES = [2, 4, 4, 4, 4, 4, 4, 4, 2]
-TURNED = 1
-RESULT_BUFS = 16
-W2_AT = 0
-VECTOR_HEAD = 12
-PER_WINDOW = 2
-VG_MOD = 2
+PLAIN = 2
+VG_MOD = 1
 VG_SET = (0,)
+VG_FROM = 3
+ADD_LEAD = 3
 
 FLOPS = 2 * BATCH * WIDTH * WIDTH * BLOCKS * 2
 
@@ -37,22 +35,13 @@ def tile_blockresmlp_mixerblock_pb_t_e_kernel(
     tc, x_blocks, w1_words, w1_scales, b1, w2_words, w2_scales, b2, out
 ):
     nc = tc.nc
-    firsts = [sum(CHUNK_TILES[:c]) for c in range(len(CHUNK_TILES))]
     units = [(c, g, n) for c, n in enumerate(CHUNK_TILES) for g in range(BLOCKS)]
-
-    def turned(unit):
-        chunk, g, n = units[unit]
-        return g == TURNED and n == MOST and 1 < chunk < 7
-
+    firsts = [sum(CHUNK_TILES[:c]) for c in range(len(CHUNK_TILES))]
     with ExitStack() as ctx:
         ctx.enter_context(tc.manual_schedule())
         const = ctx.enter_context(tc.tile_pool(name="const", bufs=1))
-        results = ctx.enter_context(tc.tile_pool(name="results", bufs=RESULT_BUFS))
-        ahead = ctx.enter_context(tc.tile_pool(name="ahead", bufs=5))
-        stage = ctx.enter_context(tc.tile_pool(name="stage", bufs=8))
         work = ctx.enter_context(tc.tile_pool(name="work", bufs=2))
-        psum_two = ctx.enter_context(tc.psum_pool(name="psum_two", bufs=2))
-        psum_four = ctx.enter_context(tc.psum_pool(name="psum_four", bufs=4))
+        psum = ctx.enter_context(tc.psum_pool(name="psum", bufs=2))
 
         x_view = x_blocks.rearrange("(p i) c -> p i c", i=TILES)
         out_view = out.rearrange("(p i) c -> p i c", i=TILES)
@@ -61,9 +50,14 @@ def tile_blockresmlp_mixerblock_pb_t_e_kernel(
 
         def load_rows(chunk):
             n = CHUNK_TILES[chunk]
-            first = firsts[chunk]
             x_sb[chunk] = const.tile([P, n, BLOCKS * WIDTH], BF16, name="x_sb%d" % chunk)
-            nc.sync.dma_start(out=x_sb[chunk][:], in_=x_view[:, first : first + n, :])
+            nc.sync.dma_start(out=x_sb[chunk][:], in_=x_view[:, firsts[chunk] : firsts[chunk] + n, :])
+
+        def load_codes(codes, words):
+            for g in range(BLOCKS):
+                nc.sync.dma_start(
+                    out=codes[:, g, :].bitcast(I32), in_=words[g].rearrange("p n t -> p (n t)").bitcast(I32)
+                )
 
         def load_scales(scale_sb, scales):
             nc.vector.memset(scale_sb[:].rearrange("p g n -> p (g n)").bitcast(I32), 0)
@@ -73,20 +67,15 @@ def tile_blockresmlp_mixerblock_pb_t_e_kernel(
                     in_=scales[:, PACK * quadrant : PACK * (quadrant + 1), :].rearrange("g r n -> r g n").bitcast(I32),
                 )
 
-        def load_codes(codes, words):
-            for g in range(BLOCKS):
-                nc.sync.dma_start(
-                    out=codes[:, g, :].bitcast(I32), in_=words[g].rearrange("p n t -> p (n t)").bitcast(I32)
-                )
+        def weight_tiles(label):
+            codes = const.tile([P, BLOCKS, WIDTH], U32, name=label + "_codes", align_bytes=64)
+            scale_sb = const.tile([P, BLOCKS, WIDTH], U8, name=label + "_scale_sb", align_bytes=64)
+            return codes, scale_sb
 
-        w1_raw = const.tile([P, BLOCKS, WIDTH], U32, name="w1_raw", align_bytes=64)
-        w1_scale_raw = const.tile([P, BLOCKS, WIDTH], U8, name="w1_scale_raw", align_bytes=64)
-        w1_codes = const.tile([P, BLOCKS, WIDTH], U32, name="w1_codes", align_bytes=64)
-        w1_scale_sb = const.tile([P, BLOCKS, WIDTH], U8, name="w1_scale_sb", align_bytes=64)
-        w2_codes = const.tile([P, BLOCKS, WIDTH], U32, name="w2_codes", align_bytes=64)
-        w2_scale_sb = const.tile([P, BLOCKS, WIDTH], U8, name="w2_scale_sb", align_bytes=64)
-        w2_turned = const.tile([P, WIDTH], U32, name="w2_turned", align_bytes=64)
-        w2_turned_scale = const.tile([P, WIDTH], U8, name="w2_turned_scale", align_bytes=64)
+        w1_raw, w1_scale_raw = weight_tiles("w1_raw")
+        w1_codes, w1_scale_sb = weight_tiles("w1")
+        w2_codes, w2_scale_sb = weight_tiles("w2")
+        w2_turned, w2_turned_scale = weight_tiles("w2_turned")
 
         load_rows(0)
         load_scales(w1_scale_raw, w1_scales)
@@ -101,7 +90,7 @@ def tile_blockresmlp_mixerblock_pb_t_e_kernel(
         nc.gpsimd.memset(warm[:], 0.0)
         warmed = const.tile([P, 1], F32, name="warmed")
         nc.scalar.activation(out=warmed[:], in_=warm[:], func=ACT.Exp)
-        cue_sb = const.tile([P, 32], BF16, name="cue_sb")
+        cue_sb = const.tile([P, len(units)], BF16, name="cue_sb")
         ident = const.tile([P, P], F32, name="ident")
         make_identity(nc, ident[:])
 
@@ -110,63 +99,60 @@ def tile_blockresmlp_mixerblock_pb_t_e_kernel(
         b1_col = const.tile([P, BLOCKS * PACK], F32, name="b1_col")
         b2_all = const.tile([P, BLOCKS * WIDTH], BF16, name="b2_all")
         nc.scalar.dma_start(out=b2_all[:], in_=b2.rearrange("g o d -> (g o d)").partition_broadcast(P))
-        b2_raw = const.tile([P, PACK], BF16, name="b2_raw")
-        nc.scalar.dma_start(out=b2_raw[:], in_=b2[1].rearrange("o (p t) -> p (o t)", t=PACK))
-        b2_col = const.tile([P, PACK], F32, name="b2_col")
+        b2_raw = const.tile([P, BLOCKS, PACK], BF16, name="b2_raw")
+        nc.scalar.dma_start(out=b2_raw[:], in_=b2.rearrange("g o (p t) -> p (g o) t", t=PACK))
+        b2_col = const.tile([P, BLOCKS * PACK], F32, name="b2_col")
 
         x_turned, z_grouped, z_codes, z_scales = {}, {}, {}, {}
         v_ps, grown, kept = {}, {}, {}
         h_grouped, h_codes, h_scales = {}, {}, {}
-        r_ps, result, r_turned = {}, {}, {}
+        r_ps, result, r_turned, rows_ps = {}, {}, {}, {}
 
-        def reorder(codes_to, scale_to, codes_from, scale_from):
+        def reorder(codes_to, scale_to, codes_from, scale_from, g):
             nc.vector.tensor_copy(
-                out=codes_to.bitcast(I32).rearrange("p (t m) -> p t m", t=PACK),
-                in_=codes_from.bitcast(I32).rearrange("p (m t) -> p t m", t=PACK),
+                out=codes_to[:, g, :].bitcast(I32).rearrange("p (t m) -> p t m", t=PACK),
+                in_=codes_from[:, g, :].bitcast(I32).rearrange("p (m t) -> p t m", t=PACK),
             )
             nc.vector.tensor_copy(
-                out=scale_to.rearrange("p (t m) -> p t m", t=PACK),
-                in_=scale_from.rearrange("p (m t) -> p t m", t=PACK),
+                out=scale_to[:, g, :].rearrange("p (t m) -> p t m", t=PACK),
+                in_=scale_from[:, g, :].rearrange("p (m t) -> p t m", t=PACK),
             )
 
-        def halves(unit):
-            return (units[unit][2] + 1) // 2
+        def known(unit):
+            return 0 <= unit < len(units)
 
         def transpose_x(unit, half):
-            if not 0 <= unit < len(units) or half >= halves(unit):
+            if not known(unit) or 2 * half >= units[unit][2]:
                 return
             chunk, g, n = units[unit]
-            x_turned[unit, half] = psum_two.tile([P, 2, 2, P], F32, name="x_turned")
-            for a in range(2 * half, min(2 * half + 2, n)):
-                x_words = x_sb[chunk][:, a, :].bitcast(F32)
+            x_turned[unit, half] = psum.tile([P, 2, 2, P], F32, name="x_turned")
+            for a in range(2):
+                x_words = x_sb[chunk][:, 2 * half + a, :].bitcast(F32)
                 for u in range(2):
                     nc.tensor.transpose(
-                        x_turned[unit, half][:, a % 2, u, :], x_words[:, WORDS * g + u : WORDS * (g + 1) : 2], ident[:]
+                        x_turned[unit, half][:, a, u, :], x_words[:, WORDS * g + u : WORDS * (g + 1) : 2], ident[:]
                     )
 
-        def on_vector(unit, half):
-            return half == 0 and unit >= 3 and unit % VG_MOD in VG_SET
-
-        def gather_z(unit, half):
-            if not 0 <= unit < len(units) or half >= halves(unit):
+        def gather_z(unit, half, copy):
+            if not known(unit) or 2 * half >= units[unit][2]:
                 return
             n = units[unit][2]
-            if unit not in z_grouped:
-                z_grouped[unit] = ahead.tile([P, MOST * P * PACK], BF16, name="z_grouped", align_bytes=64)
+            if half == 0:
+                z_grouped[unit] = work.tile([P, MOST * P * PACK], BF16, name="z_grouped", bufs=5, align_bytes=64)
             z_words = z_grouped[unit][:].bitcast(F32)
-            low, high = 2 * half, min(2 * half + 2, n)
-            turned_words = x_turned[unit, half][:, : high - low]
             if n == MOST:
-                out_words = z_words.rearrange("p (r a u) -> p r a u", a=MOST, u=2)[:, :, low:high, :]
-                in_words = turned_words.rearrange("p a u r -> p r a u")
+                copy(
+                    out=z_words.rearrange("p (r a u) -> p r a u", a=MOST, u=2)[:, :, 2 * half : 2 * half + 2, :],
+                    in_=x_turned[unit, half][:].rearrange("p a u r -> p r a u"),
+                )
             else:
-                out_words = z_words.rearrange("p (a r u) -> p a r u", r=P, u=2)[:, low:high]
-                in_words = turned_words.rearrange("p a u r -> p a r u")
-            copy = nc.vector.tensor_copy if on_vector(unit, half) else nc.scalar.copy
-            copy(out=out_words, in_=in_words)
+                copy(
+                    out=z_words.rearrange("p (a r u) -> p a r u", r=P, u=2)[:, :n],
+                    in_=x_turned[unit, half][:].rearrange("p a u r -> p a r u"),
+                )
 
         def quantise_z(unit):
-            if not 0 <= unit < len(units):
+            if not known(unit):
                 return
             n = units[unit][2]
             z_codes[unit] = work.tile([P, MOST * P], U32, name="z_codes", align_bytes=64)
@@ -178,10 +164,10 @@ def tile_blockresmlp_mixerblock_pb_t_e_kernel(
             )
 
         def first_product(unit, t):
-            if not 0 <= unit < len(units):
+            if not known(unit):
                 return
             chunk, g, n = units[unit]
-            v_ps[unit, t] = psum_two.tile([P, MOST * P], F32, name="v_ps")
+            v_ps[unit, t] = psum.tile([P, MOST * P], F32, name="v_ps")
             nc.tensor.matmul_mx(
                 out=v_ps[unit, t][:, : n * P],
                 lhsT=w1_codes[:, g, P * t : P * (t + 1)].bitcast(FP8X4),
@@ -198,7 +184,7 @@ def tile_blockresmlp_mixerblock_pb_t_e_kernel(
             return values[:, n * P * t : n * P * (t + 1)]
 
         def exp_and_relu(unit, t):
-            if not 0 <= unit < len(units):
+            if not known(unit):
                 return
             chunk, g, n = units[unit]
             if t == 0:
@@ -212,22 +198,23 @@ def tile_blockresmlp_mixerblock_pb_t_e_kernel(
             nc.scalar.activation(out=quarter(kept[unit], n, t), in_=source, func=ACT.Relu, bias=bias, scale=1.0)
 
         def join(unit):
-            if not 0 <= unit < len(units):
+            if not known(unit):
                 return
             n = units[unit][2]
             h_grouped[unit] = work.tile([P, MOST * P, PACK], BF16, name="h_grouped", align_bytes=64)
             if n == MOST:
-                out_view_h = h_grouped[unit][:].rearrange("p (a r) t -> p (r t) a", a=MOST)
-                sides = [values[:].rearrange("p (r t a) -> p (r t) a", t=PACK, a=MOST) for values in (grown[unit], kept[unit])]
+                h_side = h_grouped[unit][:].rearrange("p (a r) t -> p (r t) a", a=MOST)
+                order = "p (r t a) -> p (r t) a"
+                sides = [values[:].rearrange(order, t=PACK, a=MOST) for values in (grown[unit], kept[unit])]
             else:
-                out_view_h = h_grouped[unit][:, : n * P, :]
+                h_side = h_grouped[unit][:, : n * P, :]
                 sides = [values[:, : n * P * PACK].rearrange("p (t w) -> p w t", t=PACK) for values in (grown[unit], kept[unit])]
             nc.vector.scalar_tensor_tensor(
-                out=out_view_h, in0=sides[0], scalar=-1.0, in1=sides[1], op0=ALU.add, op1=ALU.min
+                out=h_side, in0=sides[0], scalar=-1.0, in1=sides[1], op0=ALU.add, op1=ALU.min
             )
 
         def quantise_h(unit):
-            if not 0 <= unit < len(units):
+            if not known(unit):
                 return
             n = units[unit][2]
             h_codes[unit] = work.tile([P, MOST * P], U32, name="h_codes", align_bytes=64)
@@ -239,24 +226,11 @@ def tile_blockresmlp_mixerblock_pb_t_e_kernel(
             )
 
         def second_product(unit):
-            if not 0 <= unit < len(units):
+            if not known(unit):
                 return
             chunk, g, n = units[unit]
-            if turned(unit):
-                for t in range(PACK):
-                    r_ps[unit, t] = psum_four.tile([P, WIDTH], F32, name="r_ps")
-                    nc.tensor.matmul_mx(
-                        out=r_ps[unit, t][:, : n * P],
-                        lhsT=w2_turned[:, P * t : P * (t + 1)].bitcast(FP8X4),
-                        lhsT_scale=w2_turned_scale[:, P * t : P * (t + 1)],
-                        rhs=h_codes[unit][:, : n * P].bitcast(FP8X4),
-                        rhs_scale=h_scales[unit][:, : n * P],
-                        start=True,
-                        stop=True,
-                    )
-                return
-            for a in range(n):
-                r_ps[unit, a] = psum_four.tile([P, WIDTH], F32, name="r_ps")
+            for a in range(PLAIN):
+                r_ps[unit, a] = psum.tile([P, WIDTH], F32, name="r_ps", bufs=4)
                 nc.tensor.matmul_mx(
                     out=r_ps[unit, a][:],
                     lhsT=h_codes[unit][:, P * a : P * (a + 1)].bitcast(FP8X4),
@@ -266,81 +240,84 @@ def tile_blockresmlp_mixerblock_pb_t_e_kernel(
                     start=True,
                     stop=True,
                 )
-
-        def cue(unit):
-            if not 0 <= unit < len(units):
+            if n == PLAIN:
                 return
-            nc.gpsimd.tensor_copy(out=cue_sb[:, unit : unit + 1], in_=h_grouped[unit][:, 0, :1])
+            for t in range(PACK):
+                if t % 2 == 0:
+                    rows_ps[unit, t // 2] = psum.tile([P, 2, (MOST - PLAIN) * P], F32, name="r_ps", bufs=4)
+                nc.tensor.matmul_mx(
+                    out=rows_ps[unit, t // 2][:, t % 2, :],
+                    lhsT=w2_turned[:, g, P * t : P * (t + 1)].bitcast(FP8X4),
+                    lhsT_scale=w2_turned_scale[:, g, P * t : P * (t + 1)],
+                    rhs=h_codes[unit][:, PLAIN * P : n * P].bitcast(FP8X4),
+                    rhs_scale=h_scales[unit][:, PLAIN * P : n * P],
+                    start=True,
+                    stop=True,
+                )
 
-        def add_b2(unit, a):
+        def add_b2(unit, engine):
+            if not known(unit):
+                return
             chunk, g, n = units[unit]
             columns = slice(WIDTH * g, WIDTH * (g + 1))
-            result[unit, a] = results.tile([P, WIDTH], F32, name="result")
-            engine = nc.vector if len(added) < VECTOR_HEAD else nc.gpsimd
-            engine.tensor_tensor(
-                out=result[unit, a][:], in0=x_sb[chunk][:, a, columns], in1=b2_all[:, columns], op=ALU.add
-            )
+            for a in range(PLAIN):
+                result[unit, a] = work.tile([P, WIDTH], F32, name="result", bufs=14)
+                engine.tensor_tensor(
+                    out=result[unit, a][:], in0=x_sb[chunk][:, a, columns], in1=b2_all[:, columns], op=ALU.add
+                )
 
         def finish(unit):
-            if not 0 <= unit < len(units):
+            if not known(unit):
                 return
             chunk, g, n = units[unit]
-            if turned(unit):
-                r_turned[unit] = work.tile([P, PACK, MOST * P], F32, name="r_turned")
-                z_rows = z_grouped[unit][:].rearrange("p (r a k) -> p k r a", a=MOST, k=PACK)
-                for t in range(PACK):
-                    nc.vector.scalar_tensor_tensor(
-                        out=r_turned[unit][:, t, :].rearrange("p (a r) -> p r a", a=MOST),
-                        in0=r_ps[unit, t][:].rearrange("p (a r) -> p r a", a=MOST),
-                        scalar=b2_col[:, t : t + 1],
-                        in1=z_rows[:, t],
-                        op0=ALU.add,
-                        op1=ALU.add,
-                    )
-                return
-            for a in range(n):
+            for a in range(PLAIN):
                 block = result[unit, a][:]
                 nc.vector.tensor_tensor(out=block, in0=r_ps[unit, a][:], in1=block, op=ALU.add)
                 nc.sync.dma_start(out=out_view[:, firsts[chunk] + a, WIDTH * g : WIDTH * (g + 1)], in_=block)
+            if n == PLAIN:
+                return
+            z_rows = z_grouped[unit][:].rearrange("p (r a k) -> p k r a", a=MOST, k=PACK)
+            r_turned[unit] = work.tile([P, PACK, MOST - PLAIN, P], F32, name="r_turned")
+            for t in range(PACK):
+                nc.vector.scalar_tensor_tensor(
+                    out=r_turned[unit][:, t].rearrange("p a r -> p r a"),
+                    in0=rows_ps[unit, t // 2][:, t % 2, :].rearrange("p (a r) -> p r a", r=P),
+                    scalar=b2_col[:, PACK * g + t : PACK * g + t + 1],
+                    in1=z_rows[:, t, :, PLAIN:],
+                    op0=ALU.add,
+                    op1=ALU.add,
+                )
 
         def turn_back(unit):
-            if not 0 <= unit < len(units) or not turned(unit):
+            if not known(unit):
                 return
-            for a in range(units[unit][2]):
-                r_ps[unit, PACK + a] = psum_four.tile([P, PACK, P], F32, name="r_ps")
+            for a in range(PLAIN, units[unit][2]):
+                r_ps[unit, a] = psum.tile([P, PACK, P], F32, name="r_ps", bufs=4)
                 for t in range(PACK):
-                    nc.tensor.transpose(
-                        r_ps[unit, PACK + a][:, t, :], r_turned[unit][:, t, P * a : P * (a + 1)], ident[:]
-                    )
+                    nc.tensor.transpose(r_ps[unit, a][:, t, :], r_turned[unit][:, t, a - PLAIN, :], ident[:])
 
-        def copy_and_store(unit, low=0, high=MOST):
-            if not 0 <= unit < len(units) or not turned(unit):
+        def copy_and_store(unit):
+            if not known(unit):
                 return
             chunk, g, n = units[unit]
-            for a in range(low, min(high, n)):
-                rows = stage.tile([P, P, PACK], F32, name="rows")
-                nc.scalar.copy(out=rows[:], in_=r_ps[unit, PACK + a][:].rearrange("b t p -> b p t"))
+            for a in range(PLAIN, n):
+                rows = work.tile([P, P, PACK], F32, name="rows", bufs=6)
+                nc.scalar.copy(out=rows[:], in_=r_ps[unit, a][:].rearrange("b t p -> b p t"))
                 nc.sync.dma_start(
                     out=out_view[:, firsts[chunk] + a, WIDTH * g : WIDTH * (g + 1)], in_=rows[:].rearrange("b p t -> b (p t)")
                 )
 
-        to_add = [(u, a) for u in range(len(units)) if not turned(u) for a in range(units[u][2])]
-        added = []
-
-        def adds_due(unit):
-            done = sum(units[u][2] for u in range(min(unit + 1, len(units))))
-            return min(len(to_add), VECTOR_HEAD + max(0, (unit + 1) * PER_WINDOW))
-
+        on_vector = lambda unit: unit >= VG_FROM and unit % VG_MOD in VG_SET
         for k in range(-3, len(units) + 2):
             copy_and_store(k - 2)
             second_product(k - 1)
             if k == -2:
                 nc.vector.tensor_copy(out=b1_col[:], in_=b1_raw[:].rearrange("p g t -> p (g t)"))
-                reorder(w1_codes[:, 0, :], w1_scale_sb[:, 0, :], w1_raw[:, 0, :], w1_scale_raw[:, 0, :])
+                reorder(w1_codes, w1_scale_sb, w1_raw, w1_scale_raw, 0)
             if k < 0:
                 quantise_z(k + 2)
             if k == -2:
-                reorder(w1_codes[:, 1, :], w1_scale_sb[:, 1, :], w1_raw[:, 1, :], w1_scale_raw[:, 1, :])
+                reorder(w1_codes, w1_scale_sb, w1_raw, w1_scale_raw, 1)
             exp_and_relu(k + 1, 0)
             first_product(k + 1, 2)
             transpose_x(k + 3, 0)
@@ -348,31 +325,27 @@ def tile_blockresmlp_mixerblock_pb_t_e_kernel(
             first_product(k + 1, 3)
             transpose_x(k + 3, 1)
             if k == -1:
-                while len(added) < VECTOR_HEAD:
-                    pair = to_add[len(added)]
-                    add_b2(pair[0], pair[1])
-                    added.append(pair)
+                for unit in range(ADD_LEAD):
+                    add_b2(unit, nc.vector)
             join(k)
             if k >= 0:
                 quantise_z(k + 2)
-            if k == W2_AT:
-                nc.vector.tensor_copy(out=b2_col[:], in_=b2_raw[:])
-                reorder(w2_turned[:], w2_turned_scale[:], w2_codes[:, TURNED, :], w2_scale_sb[:, TURNED, :])
+            if k == 0:
+                nc.vector.tensor_copy(out=b2_col[:], in_=b2_raw[:].rearrange("p g t -> p (g t)"))
+            if 0 <= k < BLOCKS:
+                reorder(w2_turned, w2_turned_scale, w2_codes, w2_scale_sb, k)
             finish(k - 1)
-            if k >= 0:
-                cue(k)
-                while len(added) < adds_due(k):
-                    pair = to_add[len(added)]
-                    add_b2(pair[0], pair[1])
-                    added.append(pair)
-            if on_vector(k + 3, 0):
-                gather_z(k + 3, 0)
+            if known(k) and known(k + ADD_LEAD):
+                nc.gpsimd.tensor_copy(out=cue_sb[:, k : k + 1], in_=h_grouped[k][:, 0, :1])
+                add_b2(k + ADD_LEAD, nc.gpsimd)
+            if on_vector(k + 3):
+                gather_z(k + 3, 0, nc.vector.tensor_copy)
             quantise_h(k)
             exp_and_relu(k + 1, 2)
             first_product(k + 2, 0)
-            if not on_vector(k + 3, 0):
-                gather_z(k + 3, 0)
+            if not on_vector(k + 3):
+                gather_z(k + 3, 0, nc.scalar.copy)
             exp_and_relu(k + 1, 3)
-            gather_z(k + 3, 1)
+            gather_z(k + 3, 1, nc.scalar.copy)
             turn_back(k - 1)
             first_product(k + 2, 1)

@@ -20,13 +20,12 @@ BLOCKS = 2
 WIDTH = 512
 WORDS = WIDTH // 2
 TILES = BATCH // P
-MOST = 4
-CHUNK_TILES = [2, 4, 4, 4, 4, 4, 4, 4, 2]
+FULL = 4
+PAIR = 2
 PLAIN = 2
-VG_MOD = 1
-VG_SET = (0,)
-VG_FROM = 3
-ADD_LEAD = 3
+TURNED = FULL - PLAIN
+CHUNK_TILES = [2, 4, 4, 4, 4, 4, 4, 4, 2]
+EARLY_ADDS = 3 * PLAIN
 
 FLOPS = 2 * BATCH * WIDTH * WIDTH * BLOCKS * 2
 
@@ -35,8 +34,10 @@ def tile_blockresmlp_mixerblock_pb_t_e_kernel(
     tc, x_blocks, w1_words, w1_scales, b1, w2_words, w2_scales, b2, out
 ):
     nc = tc.nc
-    units = [(c, g, n) for c, n in enumerate(CHUNK_TILES) for g in range(BLOCKS)]
-    firsts = [sum(CHUNK_TILES[:c]) for c in range(len(CHUNK_TILES))]
+    units = [(chunk, block) for chunk in range(len(CHUNK_TILES)) for block in range(BLOCKS)]
+    plain_tiles = [(unit, a) for unit in range(len(units)) for a in range(PLAIN)]
+    first_tile = [sum(CHUNK_TILES[:chunk]) for chunk in range(len(CHUNK_TILES))]
+
     with ExitStack() as ctx:
         ctx.enter_context(tc.manual_schedule())
         const = ctx.enter_context(tc.tile_pool(name="const", bufs=1))
@@ -51,12 +52,17 @@ def tile_blockresmlp_mixerblock_pb_t_e_kernel(
         def load_rows(chunk):
             n = CHUNK_TILES[chunk]
             x_sb[chunk] = const.tile([P, n, BLOCKS * WIDTH], BF16, name="x_sb%d" % chunk)
-            nc.sync.dma_start(out=x_sb[chunk][:], in_=x_view[:, firsts[chunk] : firsts[chunk] + n, :])
+            nc.sync.dma_start(out=x_sb[chunk][:], in_=x_view[:, first_tile[chunk] : first_tile[chunk] + n, :])
+
+        def weight_tiles(label):
+            codes = const.tile([P, BLOCKS, WIDTH], U32, name=label + "_codes", align_bytes=64)
+            scale_sb = const.tile([P, BLOCKS, WIDTH], U8, name=label + "_scale_sb", align_bytes=64)
+            return codes, scale_sb
 
         def load_codes(codes, words):
-            for g in range(BLOCKS):
+            for block in range(BLOCKS):
                 nc.sync.dma_start(
-                    out=codes[:, g, :].bitcast(I32), in_=words[g].rearrange("p n t -> p (n t)").bitcast(I32)
+                    out=codes[:, block, :].bitcast(I32), in_=words[block].rearrange("p n t -> p (n t)").bitcast(I32)
                 )
 
         def load_scales(scale_sb, scales):
@@ -67,15 +73,10 @@ def tile_blockresmlp_mixerblock_pb_t_e_kernel(
                     in_=scales[:, PACK * quadrant : PACK * (quadrant + 1), :].rearrange("g r n -> r g n").bitcast(I32),
                 )
 
-        def weight_tiles(label):
-            codes = const.tile([P, BLOCKS, WIDTH], U32, name=label + "_codes", align_bytes=64)
-            scale_sb = const.tile([P, BLOCKS, WIDTH], U8, name=label + "_scale_sb", align_bytes=64)
-            return codes, scale_sb
-
         w1_raw, w1_scale_raw = weight_tiles("w1_raw")
         w1_codes, w1_scale_sb = weight_tiles("w1")
         w2_codes, w2_scale_sb = weight_tiles("w2")
-        w2_turned, w2_turned_scale = weight_tiles("w2_turned")
+        w2_turned, w2_scale_turned = weight_tiles("w2_turned")
 
         load_rows(0)
         load_scales(w1_scale_raw, w1_scales)
@@ -90,9 +91,9 @@ def tile_blockresmlp_mixerblock_pb_t_e_kernel(
         nc.gpsimd.memset(warm[:], 0.0)
         warmed = const.tile([P, 1], F32, name="warmed")
         nc.scalar.activation(out=warmed[:], in_=warm[:], func=ACT.Exp)
-        cue_sb = const.tile([P, len(units)], BF16, name="cue_sb")
         ident = const.tile([P, P], F32, name="ident")
         make_identity(nc, ident[:])
+        cue_sb = const.tile([P, len(units)], BF16, name="cue_sb")
 
         b1_raw = const.tile([P, BLOCKS, PACK], BF16, name="b1_raw")
         nc.scalar.dma_start(out=b1_raw[:], in_=b1.rearrange("g o (p t) -> p (g o) t", t=PACK))
@@ -103,187 +104,195 @@ def tile_blockresmlp_mixerblock_pb_t_e_kernel(
         nc.scalar.dma_start(out=b2_raw[:], in_=b2.rearrange("g o (p t) -> p (g o) t", t=PACK))
         b2_col = const.tile([P, BLOCKS * PACK], F32, name="b2_col")
 
-        x_turned, z_grouped, z_codes, z_scales = {}, {}, {}, {}
+        x_ps, z_grouped, z_codes, z_scales = {}, {}, {}, {}
         v_ps, grown, kept = {}, {}, {}
         h_grouped, h_codes, h_scales = {}, {}, {}
-        r_ps, result, r_turned, rows_ps = {}, {}, {}, {}
-
-        def reorder(codes_to, scale_to, codes_from, scale_from, g):
-            nc.vector.tensor_copy(
-                out=codes_to[:, g, :].bitcast(I32).rearrange("p (t m) -> p t m", t=PACK),
-                in_=codes_from[:, g, :].bitcast(I32).rearrange("p (m t) -> p t m", t=PACK),
-            )
-            nc.vector.tensor_copy(
-                out=scale_to[:, g, :].rearrange("p (t m) -> p t m", t=PACK),
-                in_=scale_from[:, g, :].rearrange("p (m t) -> p t m", t=PACK),
-            )
+        plain_ps, turned_ps, turned_sum, rows_ps, result = {}, {}, {}, {}, {}
 
         def known(unit):
             return 0 <= unit < len(units)
 
+        def tiles_of(unit):
+            return CHUNK_TILES[units[unit][0]]
+
+        def store(unit, a, rows):
+            chunk, block = units[unit]
+            nc.sync.dma_start(out=out_view[:, first_tile[chunk] + a, WIDTH * block : WIDTH * (block + 1)], in_=rows)
+
+        def bias_column(columns, block, t):
+            return columns[:, PACK * block + t : PACK * block + t + 1]
+
+        def reorder(codes_to, scale_to, codes_from, scale_from, block):
+            nc.vector.tensor_copy(
+                out=codes_to[:, block, :].bitcast(I32).rearrange("p (t m) -> p t m", t=PACK),
+                in_=codes_from[:, block, :].bitcast(I32).rearrange("p (m t) -> p t m", t=PACK),
+            )
+            nc.vector.tensor_copy(
+                out=scale_to[:, block, :].rearrange("p (t m) -> p t m", t=PACK),
+                in_=scale_from[:, block, :].rearrange("p (m t) -> p t m", t=PACK),
+            )
+
         def transpose_x(unit, half):
-            if not known(unit) or 2 * half >= units[unit][2]:
+            if not known(unit) or PAIR * half >= tiles_of(unit):
                 return
-            chunk, g, n = units[unit]
-            x_turned[unit, half] = psum.tile([P, 2, 2, P], F32, name="x_turned")
-            for a in range(2):
-                x_words = x_sb[chunk][:, 2 * half + a, :].bitcast(F32)
+            chunk, block = units[unit]
+            x_ps[unit, half] = psum.tile([P, PAIR, 2, P], F32, name="x_ps")
+            for a in range(PAIR):
+                x_words = x_sb[chunk][:, PAIR * half + a, :].bitcast(F32)
                 for u in range(2):
                     nc.tensor.transpose(
-                        x_turned[unit, half][:, a, u, :], x_words[:, WORDS * g + u : WORDS * (g + 1) : 2], ident[:]
+                        x_ps[unit, half][:, a, u, :], x_words[:, WORDS * block + u : WORDS * (block + 1) : 2], ident[:]
                     )
 
         def gather_z(unit, half, copy):
-            if not known(unit) or 2 * half >= units[unit][2]:
+            if not known(unit) or PAIR * half >= tiles_of(unit):
                 return
-            n = units[unit][2]
             if half == 0:
-                z_grouped[unit] = work.tile([P, MOST * P * PACK], BF16, name="z_grouped", bufs=5, align_bytes=64)
+                z_grouped[unit] = work.tile([P, FULL * P * PACK], BF16, name="z_grouped", bufs=5, align_bytes=64)
             z_words = z_grouped[unit][:].bitcast(F32)
-            if n == MOST:
+            if tiles_of(unit) == FULL:
                 copy(
-                    out=z_words.rearrange("p (r a u) -> p r a u", a=MOST, u=2)[:, :, 2 * half : 2 * half + 2, :],
-                    in_=x_turned[unit, half][:].rearrange("p a u r -> p r a u"),
+                    out=z_words.rearrange("p (r a u) -> p r a u", a=FULL, u=2)[:, :, PAIR * half : PAIR * (half + 1), :],
+                    in_=x_ps[unit, half][:].rearrange("p a u r -> p r a u"),
                 )
             else:
                 copy(
-                    out=z_words.rearrange("p (a r u) -> p a r u", r=P, u=2)[:, :n],
-                    in_=x_turned[unit, half][:].rearrange("p a u r -> p a r u"),
+                    out=z_words.rearrange("p (a r u) -> p a r u", r=P, u=2)[:, :PAIR],
+                    in_=x_ps[unit, half][:].rearrange("p a u r -> p a r u"),
                 )
 
         def quantise_z(unit):
             if not known(unit):
                 return
-            n = units[unit][2]
-            z_codes[unit] = work.tile([P, MOST * P], U32, name="z_codes", align_bytes=64)
-            z_scales[unit] = work.tile([P, MOST * P], U8, name="z_scales", align_bytes=64)
+            columns = P * tiles_of(unit)
+            z_codes[unit] = work.tile([P, FULL * P], U32, name="z_codes", align_bytes=64)
+            z_scales[unit] = work.tile([P, FULL * P], U8, name="z_scales", align_bytes=64)
             nc.vector.quantize_mx(
-                out=z_codes[unit][:, : n * P].bitcast(FP8X4),
-                scales=z_scales[unit][:, : n * P],
-                in_=z_grouped[unit][:, : n * P * PACK],
+                out=z_codes[unit][:, :columns].bitcast(FP8X4),
+                scales=z_scales[unit][:, :columns],
+                in_=z_grouped[unit][:, : columns * PACK],
             )
 
         def first_product(unit, t):
             if not known(unit):
                 return
-            chunk, g, n = units[unit]
-            v_ps[unit, t] = psum.tile([P, MOST * P], F32, name="v_ps")
+            chunk, block = units[unit]
+            columns = P * tiles_of(unit)
+            v_ps[unit, t] = psum.tile([P, FULL * P], F32, name="v_ps")
             nc.tensor.matmul_mx(
-                out=v_ps[unit, t][:, : n * P],
-                lhsT=w1_codes[:, g, P * t : P * (t + 1)].bitcast(FP8X4),
-                lhsT_scale=w1_scale_sb[:, g, P * t : P * (t + 1)],
-                rhs=z_codes[unit][:, : n * P].bitcast(FP8X4),
-                rhs_scale=z_scales[unit][:, : n * P],
+                out=v_ps[unit, t][:, :columns],
+                lhsT=w1_codes[:, block, P * t : P * (t + 1)].bitcast(FP8X4),
+                lhsT_scale=w1_scale_sb[:, block, P * t : P * (t + 1)],
+                rhs=z_codes[unit][:, :columns].bitcast(FP8X4),
+                rhs_scale=z_scales[unit][:, :columns],
                 start=True,
                 stop=True,
             )
 
-        def quarter(values, n, t):
-            if n == MOST:
-                return values[:].rearrange("p (r t a) -> p r t a", t=PACK, a=MOST)[:, :, t, :]
-            return values[:, n * P * t : n * P * (t + 1)]
-
         def exp_and_relu(unit, t):
             if not known(unit):
                 return
-            chunk, g, n = units[unit]
+            chunk, block = units[unit]
+            columns = P * tiles_of(unit)
             if t == 0:
-                grown[unit] = work.tile([P, PACK * MOST * P], F32, name="grown")
-                kept[unit] = work.tile([P, PACK * MOST * P], F32, name="kept")
-            bias = b1_col[:, PACK * g + t : PACK * g + t + 1]
-            source = v_ps[unit, t][:, : n * P]
-            if n == MOST:
-                source = source.rearrange("p (r a) -> p r a", a=MOST)
-            nc.scalar.activation(out=quarter(grown[unit], n, t), in_=source, func=ACT.Exp, bias=bias, scale=1.0)
-            nc.scalar.activation(out=quarter(kept[unit], n, t), in_=source, func=ACT.Relu, bias=bias, scale=1.0)
+                grown[unit] = work.tile([P, PACK * FULL * P], F32, name="grown")
+                kept[unit] = work.tile([P, PACK * FULL * P], F32, name="kept")
+            source = v_ps[unit, t][:, :columns]
+            if columns == FULL * P:
+                source = source.rearrange("p (r a) -> p r a", a=FULL)
+            for values, func in ((grown[unit], ACT.Exp), (kept[unit], ACT.Relu)):
+                if columns == FULL * P:
+                    quarter = values[:].rearrange("p (r t a) -> p r t a", t=PACK, a=FULL)[:, :, t, :]
+                else:
+                    quarter = values[:, columns * t : columns * (t + 1)]
+                nc.scalar.activation(
+                    out=quarter, in_=source, func=func, bias=bias_column(b1_col, block, t), scale=1.0
+                )
 
         def join(unit):
             if not known(unit):
                 return
-            n = units[unit][2]
-            h_grouped[unit] = work.tile([P, MOST * P, PACK], BF16, name="h_grouped", align_bytes=64)
-            if n == MOST:
-                h_side = h_grouped[unit][:].rearrange("p (a r) t -> p (r t) a", a=MOST)
-                order = "p (r t a) -> p (r t) a"
-                sides = [values[:].rearrange(order, t=PACK, a=MOST) for values in (grown[unit], kept[unit])]
+            columns = P * tiles_of(unit)
+            h_grouped[unit] = work.tile([P, FULL * P, PACK], BF16, name="h_grouped", align_bytes=64)
+            if columns == FULL * P:
+                joined = h_grouped[unit][:].rearrange("p (a r) t -> p (r t) a", a=FULL)
+                sides = [v[:].rearrange("p (r t a) -> p (r t) a", t=PACK, a=FULL) for v in (grown[unit], kept[unit])]
             else:
-                h_side = h_grouped[unit][:, : n * P, :]
-                sides = [values[:, : n * P * PACK].rearrange("p (t w) -> p w t", t=PACK) for values in (grown[unit], kept[unit])]
+                joined = h_grouped[unit][:, :columns, :]
+                sides = [v[:, : columns * PACK].rearrange("p (t w) -> p w t", t=PACK) for v in (grown[unit], kept[unit])]
             nc.vector.scalar_tensor_tensor(
-                out=h_side, in0=sides[0], scalar=-1.0, in1=sides[1], op0=ALU.add, op1=ALU.min
+                out=joined, in0=sides[0], scalar=-1.0, in1=sides[1], op0=ALU.add, op1=ALU.min
             )
 
         def quantise_h(unit):
             if not known(unit):
                 return
-            n = units[unit][2]
-            h_codes[unit] = work.tile([P, MOST * P], U32, name="h_codes", align_bytes=64)
-            h_scales[unit] = work.tile([P, MOST * P], U8, name="h_scales", align_bytes=64)
+            columns = P * tiles_of(unit)
+            h_codes[unit] = work.tile([P, FULL * P], U32, name="h_codes", align_bytes=64)
+            h_scales[unit] = work.tile([P, FULL * P], U8, name="h_scales", align_bytes=64)
             nc.vector.quantize_mx(
-                out=h_codes[unit][:, : n * P].bitcast(FP8X4),
-                scales=h_scales[unit][:, : n * P],
-                in_=h_grouped[unit][:, : n * P, :].rearrange("p w t -> p (w t)"),
+                out=h_codes[unit][:, :columns].bitcast(FP8X4),
+                scales=h_scales[unit][:, :columns],
+                in_=h_grouped[unit][:, :columns, :].rearrange("p w t -> p (w t)"),
             )
 
         def second_product(unit):
             if not known(unit):
                 return
-            chunk, g, n = units[unit]
+            chunk, block = units[unit]
             for a in range(PLAIN):
-                r_ps[unit, a] = psum.tile([P, WIDTH], F32, name="r_ps", bufs=4)
+                plain_ps[unit, a] = psum.tile([P, WIDTH], F32, name="r_ps", bufs=4)
                 nc.tensor.matmul_mx(
-                    out=r_ps[unit, a][:],
+                    out=plain_ps[unit, a][:],
                     lhsT=h_codes[unit][:, P * a : P * (a + 1)].bitcast(FP8X4),
                     lhsT_scale=h_scales[unit][:, P * a : P * (a + 1)],
-                    rhs=w2_codes[:, g, :].bitcast(FP8X4),
-                    rhs_scale=w2_scale_sb[:, g, :],
+                    rhs=w2_codes[:, block, :].bitcast(FP8X4),
+                    rhs_scale=w2_scale_sb[:, block, :],
                     start=True,
                     stop=True,
                 )
-            if n == PLAIN:
+            if tiles_of(unit) < FULL:
                 return
             for t in range(PACK):
                 if t % 2 == 0:
-                    rows_ps[unit, t // 2] = psum.tile([P, 2, (MOST - PLAIN) * P], F32, name="r_ps", bufs=4)
+                    turned_ps[unit, t // 2] = psum.tile([P, 2, TURNED * P], F32, name="r_ps", bufs=4)
                 nc.tensor.matmul_mx(
-                    out=rows_ps[unit, t // 2][:, t % 2, :],
-                    lhsT=w2_turned[:, g, P * t : P * (t + 1)].bitcast(FP8X4),
-                    lhsT_scale=w2_turned_scale[:, g, P * t : P * (t + 1)],
-                    rhs=h_codes[unit][:, PLAIN * P : n * P].bitcast(FP8X4),
-                    rhs_scale=h_scales[unit][:, PLAIN * P : n * P],
+                    out=turned_ps[unit, t // 2][:, t % 2, :],
+                    lhsT=w2_turned[:, block, P * t : P * (t + 1)].bitcast(FP8X4),
+                    lhsT_scale=w2_scale_turned[:, block, P * t : P * (t + 1)],
+                    rhs=h_codes[unit][:, PLAIN * P : FULL * P].bitcast(FP8X4),
+                    rhs_scale=h_scales[unit][:, PLAIN * P : FULL * P],
                     start=True,
                     stop=True,
                 )
 
-        def add_b2(unit, engine):
-            if not known(unit):
-                return
-            chunk, g, n = units[unit]
-            columns = slice(WIDTH * g, WIDTH * (g + 1))
-            for a in range(PLAIN):
-                result[unit, a] = work.tile([P, WIDTH], F32, name="result", bufs=14)
-                engine.tensor_tensor(
-                    out=result[unit, a][:], in0=x_sb[chunk][:, a, columns], in1=b2_all[:, columns], op=ALU.add
-                )
+        def add_b2(item, engine):
+            unit, a = plain_tiles[item]
+            chunk, block = units[unit]
+            columns = slice(WIDTH * block, WIDTH * (block + 1))
+            result[unit, a] = work.tile([P, WIDTH], F32, name="result", bufs=7 * PLAIN)
+            engine.tensor_tensor(
+                out=result[unit, a][:], in0=x_sb[chunk][:, a, columns], in1=b2_all[:, columns], op=ALU.add
+            )
 
         def finish(unit):
             if not known(unit):
                 return
-            chunk, g, n = units[unit]
+            chunk, block = units[unit]
             for a in range(PLAIN):
-                block = result[unit, a][:]
-                nc.vector.tensor_tensor(out=block, in0=r_ps[unit, a][:], in1=block, op=ALU.add)
-                nc.sync.dma_start(out=out_view[:, firsts[chunk] + a, WIDTH * g : WIDTH * (g + 1)], in_=block)
-            if n == PLAIN:
+                rows = result[unit, a][:]
+                nc.vector.tensor_tensor(out=rows, in0=plain_ps[unit, a][:], in1=rows, op=ALU.add)
+                store(unit, a, rows)
+            if tiles_of(unit) < FULL:
                 return
-            z_rows = z_grouped[unit][:].rearrange("p (r a k) -> p k r a", a=MOST, k=PACK)
-            r_turned[unit] = work.tile([P, PACK, MOST - PLAIN, P], F32, name="r_turned")
+            z_values = z_grouped[unit][:].rearrange("p (r a k) -> p k r a", a=FULL, k=PACK)
+            turned_sum[unit] = work.tile([P, PACK, TURNED, P], F32, name="turned_sum")
             for t in range(PACK):
                 nc.vector.scalar_tensor_tensor(
-                    out=r_turned[unit][:, t].rearrange("p a r -> p r a"),
-                    in0=rows_ps[unit, t // 2][:, t % 2, :].rearrange("p (a r) -> p r a", r=P),
-                    scalar=b2_col[:, PACK * g + t : PACK * g + t + 1],
-                    in1=z_rows[:, t, :, PLAIN:],
+                    out=turned_sum[unit][:, t].rearrange("p a r -> p r a"),
+                    in0=turned_ps[unit, t // 2][:, t % 2, :].rearrange("p (a r) -> p r a", r=P),
+                    scalar=bias_column(b2_col, block, t),
+                    in1=z_values[:, t, :, PLAIN:],
                     op0=ALU.add,
                     op1=ALU.add,
                 )
@@ -291,23 +300,20 @@ def tile_blockresmlp_mixerblock_pb_t_e_kernel(
         def turn_back(unit):
             if not known(unit):
                 return
-            for a in range(PLAIN, units[unit][2]):
-                r_ps[unit, a] = psum.tile([P, PACK, P], F32, name="r_ps", bufs=4)
+            for a in range(PLAIN, tiles_of(unit)):
+                rows_ps[unit, a] = psum.tile([P, PACK, P], F32, name="r_ps", bufs=4)
                 for t in range(PACK):
-                    nc.tensor.transpose(r_ps[unit, a][:, t, :], r_turned[unit][:, t, a - PLAIN, :], ident[:])
+                    nc.tensor.transpose(rows_ps[unit, a][:, t, :], turned_sum[unit][:, t, a - PLAIN, :], ident[:])
 
         def copy_and_store(unit):
             if not known(unit):
                 return
-            chunk, g, n = units[unit]
-            for a in range(PLAIN, n):
-                rows = work.tile([P, P, PACK], F32, name="rows", bufs=6)
-                nc.scalar.copy(out=rows[:], in_=r_ps[unit, a][:].rearrange("b t p -> b p t"))
-                nc.sync.dma_start(
-                    out=out_view[:, firsts[chunk] + a, WIDTH * g : WIDTH * (g + 1)], in_=rows[:].rearrange("b p t -> b (p t)")
-                )
+            for a in range(PLAIN, tiles_of(unit)):
+                rows = work.tile([P, P, PACK], F32, name="rows", bufs=3 * TURNED)
+                nc.scalar.copy(out=rows[:], in_=rows_ps[unit, a][:].rearrange("b t p -> b p t"))
+                store(unit, a, rows[:].rearrange("b p t -> b (p t)"))
 
-        on_vector = lambda unit: unit >= VG_FROM and unit % VG_MOD in VG_SET
+        added = EARLY_ADDS
         for k in range(-3, len(units) + 2):
             copy_and_store(k - 2)
             second_product(k - 1)
@@ -318,32 +324,38 @@ def tile_blockresmlp_mixerblock_pb_t_e_kernel(
                 quantise_z(k + 2)
             if k == -2:
                 reorder(w1_codes, w1_scale_sb, w1_raw, w1_scale_raw, 1)
+
             exp_and_relu(k + 1, 0)
             first_product(k + 1, 2)
             transpose_x(k + 3, 0)
             exp_and_relu(k + 1, 1)
             first_product(k + 1, 3)
             transpose_x(k + 3, 1)
+
             if k == -1:
-                for unit in range(ADD_LEAD):
-                    add_b2(unit, nc.vector)
+                for item in range(EARLY_ADDS):
+                    add_b2(item, nc.vector)
             join(k)
             if k >= 0:
                 quantise_z(k + 2)
             if k == 0:
                 nc.vector.tensor_copy(out=b2_col[:], in_=b2_raw[:].rearrange("p g t -> p (g t)"))
             if 0 <= k < BLOCKS:
-                reorder(w2_turned, w2_turned_scale, w2_codes, w2_scale_sb, k)
+                reorder(w2_turned, w2_scale_turned, w2_codes, w2_scale_sb, k)
             finish(k - 1)
-            if known(k) and known(k + ADD_LEAD):
+            if known(k) and added < len(plain_tiles):
                 nc.gpsimd.tensor_copy(out=cue_sb[:, k : k + 1], in_=h_grouped[k][:, 0, :1])
-                add_b2(k + ADD_LEAD, nc.gpsimd)
-            if on_vector(k + 3):
+                due = min(added + (1 if k <= BLOCKS else 2), len(plain_tiles))
+                for item in range(added, due):
+                    add_b2(item, nc.gpsimd)
+                added = due
+            if k >= 0:
                 gather_z(k + 3, 0, nc.vector.tensor_copy)
             quantise_h(k)
+
             exp_and_relu(k + 1, 2)
             first_product(k + 2, 0)
-            if not on_vector(k + 3):
+            if k < 0:
                 gather_z(k + 3, 0, nc.scalar.copy)
             exp_and_relu(k + 1, 3)
             gather_z(k + 3, 1, nc.scalar.copy)

@@ -22,10 +22,8 @@ WORDS = WIDTH // 2
 TILES = BATCH // P
 FULL = 4
 PAIR = 2
-PLAIN = 2
-TURNED = FULL - PLAIN
-CHUNK_TILES = [2, 4, 4, 4, 4, 4, 4, 4, 2]
-EARLY_ADDS = 3 * PLAIN
+UNIT_TILES = [2, 4, 4, 4, 4, 4, 4, 4, 2]
+UNIT_COUNT = BLOCKS * len(UNIT_TILES)
 
 FLOPS = 2 * BATCH * WIDTH * WIDTH * BLOCKS * 2
 
@@ -34,9 +32,17 @@ def tile_blockresmlp_mixerblock_pb_t_e_kernel(
     tc, x_blocks, w1_words, w1_scales, b1, w2_words, w2_scales, b2, out
 ):
     nc = tc.nc
-    units = [(chunk, block) for chunk in range(len(CHUNK_TILES)) for block in range(BLOCKS)]
-    plain_tiles = [(unit, a) for unit in range(len(units)) for a in range(PLAIN)]
-    first_tile = [sum(CHUNK_TILES[:chunk]) for chunk in range(len(CHUNK_TILES))]
+    block_of = [u % BLOCKS for u in range(UNIT_COUNT)]
+    tiles_of = [UNIT_TILES[u // BLOCKS] for u in range(UNIT_COUNT)]
+    first_tile = [sum(UNIT_TILES[: u // BLOCKS]) for u in range(UNIT_COUNT)]
+
+    base_by = {}
+    for u in range(UNIT_COUNT):
+        scalar_tiles = 1 if u % 3 == 2 else 2
+        for a in range(tiles_of[u]):
+            base_by[u, a] = "vector" if u < 3 else "scalar" if a < scalar_tiles else "gpsimd"
+    vector_bases = [item for item in base_by if base_by[item] == "vector"]
+    gpsimd_bases = [item for item in base_by if base_by[item] == "gpsimd"]
 
     with ExitStack() as ctx:
         ctx.enter_context(tc.manual_schedule())
@@ -47,23 +53,23 @@ def tile_blockresmlp_mixerblock_pb_t_e_kernel(
         x_view = x_blocks.rearrange("(p i) c -> p i c", i=TILES)
         out_view = out.rearrange("(p i) c -> p i c", i=TILES)
 
-        x_sb = {}
+        x_sb = const.tile([P, TILES, BLOCKS * WIDTH], BF16, name="x_sb")
 
-        def load_rows(chunk):
-            n = CHUNK_TILES[chunk]
-            x_sb[chunk] = const.tile([P, n, BLOCKS * WIDTH], BF16, name="x_sb%d" % chunk)
-            nc.sync.dma_start(out=x_sb[chunk][:], in_=x_view[:, first_tile[chunk] : first_tile[chunk] + n, :])
+        def columns_of(block):
+            return slice(WIDTH * block, WIDTH * (block + 1))
+
+        def load_x(start, stop, columns):
+            nc.sync.dma_start(out=x_sb[:, start:stop, columns], in_=x_view[:, start:stop, columns])
 
         def weight_tiles(label):
             codes = const.tile([P, BLOCKS, WIDTH], U32, name=label + "_codes", align_bytes=64)
             scale_sb = const.tile([P, BLOCKS, WIDTH], U8, name=label + "_scale_sb", align_bytes=64)
             return codes, scale_sb
 
-        def load_codes(codes, words):
-            for block in range(BLOCKS):
-                nc.sync.dma_start(
-                    out=codes[:, block, :].bitcast(I32), in_=words[block].rearrange("p n t -> p (n t)").bitcast(I32)
-                )
+        def load_codes(codes, words, block):
+            nc.sync.dma_start(
+                out=codes[:, block, :].bitcast(I32), in_=words[block].rearrange("p n t -> p (n t)").bitcast(I32)
+            )
 
         def load_scales(scale_sb, scales):
             nc.vector.memset(scale_sb[:].rearrange("p g n -> p (g n)").bitcast(I32), 0)
@@ -76,16 +82,25 @@ def tile_blockresmlp_mixerblock_pb_t_e_kernel(
         w1_raw, w1_scale_raw = weight_tiles("w1_raw")
         w1_codes, w1_scale_sb = weight_tiles("w1")
         w2_codes, w2_scale_sb = weight_tiles("w2")
-        w2_turned, w2_scale_turned = weight_tiles("w2_turned")
 
-        load_rows(0)
+        b1_raw = const.tile([P, BLOCKS, PACK], BF16, name="b1_raw")
+        nc.scalar.dma_start(out=b1_raw[:], in_=b1.rearrange("g o (p t) -> p (g o) t", t=PACK))
+        b1_col = const.tile([P, BLOCKS * PACK], F32, name="b1_col")
+        b2_all = const.tile([P, BLOCKS * WIDTH], BF16, name="b2_all")
+        nc.scalar.dma_start(out=b2_all[:], in_=b2.rearrange("g o d -> (g o d)").partition_broadcast(P))
+
+        load_x(0, 2, columns_of(0))
+        load_codes(w1_raw, w1_words, 0)
         load_scales(w1_scale_raw, w1_scales)
-        load_codes(w1_raw, w1_words)
-        load_rows(1)
-        load_codes(w2_codes, w2_words)
+        load_x(0, 2, columns_of(1))
+        load_codes(w1_raw, w1_words, 1)
+        load_x(2, 6, columns_of(0))
+        load_x(2, 6, columns_of(1))
+        for block in range(BLOCKS):
+            load_codes(w2_codes, w2_words, block)
         load_scales(w2_scale_sb, w2_scales)
-        for chunk in range(2, len(CHUNK_TILES)):
-            load_rows(chunk)
+        for start in range(6, TILES, FULL):
+            load_x(start, min(start + FULL, TILES), slice(0, BLOCKS * WIDTH))
 
         warm = const.tile([P, 1], F32, name="warm")
         nc.gpsimd.memset(warm[:], 0.0)
@@ -93,31 +108,22 @@ def tile_blockresmlp_mixerblock_pb_t_e_kernel(
         nc.scalar.activation(out=warmed[:], in_=warm[:], func=ACT.Exp)
         ident = const.tile([P, P], F32, name="ident")
         make_identity(nc, ident[:])
-        cue_sb = const.tile([P, len(units)], BF16, name="cue_sb")
+        ident_bf = const.tile([P, P], BF16, name="ident_bf")
+        make_identity(nc, ident_bf[:])
+        first_row = const.tile([P, P], BF16, name="first_row")
+        nc.gpsimd.memset(first_row[:], 0.0)
+        nc.gpsimd.memset(first_row[:1, :], 1.0)
+        cue_sb = const.tile([P, UNIT_COUNT], U32, name="cue_sb")
 
-        b1_raw = const.tile([P, BLOCKS, PACK], BF16, name="b1_raw")
-        nc.scalar.dma_start(out=b1_raw[:], in_=b1.rearrange("g o (p t) -> p (g o) t", t=PACK))
-        b1_col = const.tile([P, BLOCKS * PACK], F32, name="b1_col")
-        b2_all = const.tile([P, BLOCKS * WIDTH], BF16, name="b2_all")
-        nc.scalar.dma_start(out=b2_all[:], in_=b2.rearrange("g o d -> (g o d)").partition_broadcast(P))
-        b2_raw = const.tile([P, BLOCKS, PACK], BF16, name="b2_raw")
-        nc.scalar.dma_start(out=b2_raw[:], in_=b2.rearrange("g o (p t) -> p (g o) t", t=PACK))
-        b2_col = const.tile([P, BLOCKS * PACK], F32, name="b2_col")
-
-        x_ps, z_grouped, z_codes, z_scales = {}, {}, {}, {}
+        x_ps, grouped, codes, scales = {}, {}, {}, {}
         v_ps, grown, kept = {}, {}, {}
-        h_grouped, h_codes, h_scales = {}, {}, {}
-        plain_ps, turned_ps, turned_sum, rows_ps, result = {}, {}, {}, {}, {}
+        base_ps, r_ps, result = {}, {}, {}
 
         def known(unit):
-            return 0 <= unit < len(units)
+            return 0 <= unit < UNIT_COUNT
 
-        def tiles_of(unit):
-            return CHUNK_TILES[units[unit][0]]
-
-        def store(unit, a, rows):
-            chunk, block = units[unit]
-            nc.sync.dma_start(out=out_view[:, first_tile[chunk] + a, WIDTH * block : WIDTH * (block + 1)], in_=rows)
+        def new_grouped(unit):
+            grouped[unit] = work.tile([P, 2, FULL * P * PACK], BF16, name="grouped", bufs=3, align_bytes=64)
 
         def bias_column(columns, block, t):
             return columns[:, PACK * block + t : PACK * block + t + 1]
@@ -133,24 +139,24 @@ def tile_blockresmlp_mixerblock_pb_t_e_kernel(
             )
 
         def transpose_x(unit, half):
-            if not known(unit) or PAIR * half >= tiles_of(unit):
+            if not known(unit) or PAIR * half >= tiles_of[unit]:
                 return
-            chunk, block = units[unit]
+            block = block_of[unit]
             x_ps[unit, half] = psum.tile([P, PAIR, 2, P], F32, name="x_ps")
             for a in range(PAIR):
-                x_words = x_sb[chunk][:, PAIR * half + a, :].bitcast(F32)
+                x_words = x_sb[:, first_tile[unit] + PAIR * half + a, :].bitcast(F32)
                 for u in range(2):
                     nc.tensor.transpose(
                         x_ps[unit, half][:, a, u, :], x_words[:, WORDS * block + u : WORDS * (block + 1) : 2], ident[:]
                     )
 
         def gather_z(unit, half, copy):
-            if not known(unit) or PAIR * half >= tiles_of(unit):
+            if not known(unit) or PAIR * half >= tiles_of[unit]:
                 return
             if half == 0:
-                z_grouped[unit] = work.tile([P, FULL * P * PACK], BF16, name="z_grouped", bufs=5, align_bytes=64)
-            z_words = z_grouped[unit][:].bitcast(F32)
-            if tiles_of(unit) == FULL:
+                new_grouped(unit)
+            z_words = grouped[unit][:, 0, :].bitcast(F32)
+            if tiles_of[unit] == FULL:
                 copy(
                     out=z_words.rearrange("p (r a u) -> p r a u", a=FULL, u=2)[:, :, PAIR * half : PAIR * (half + 1), :],
                     in_=x_ps[unit, half][:].rearrange("p a u r -> p r a u"),
@@ -161,30 +167,40 @@ def tile_blockresmlp_mixerblock_pb_t_e_kernel(
                     in_=x_ps[unit, half][:].rearrange("p a u r -> p a r u"),
                 )
 
-        def quantise_z(unit):
-            if not known(unit):
+        def quantise(k):
+            if not known(k) and not known(k + 2):
                 return
-            columns = P * tiles_of(unit)
-            z_codes[unit] = work.tile([P, FULL * P], U32, name="z_codes", align_bytes=64)
-            z_scales[unit] = work.tile([P, FULL * P], U8, name="z_scales", align_bytes=64)
-            nc.vector.quantize_mx(
-                out=z_codes[unit][:, :columns].bitcast(FP8X4),
-                scales=z_scales[unit][:, :columns],
-                in_=z_grouped[unit][:, : columns * PACK],
-            )
+            unit = k + 2
+            codes[unit] = work.tile([P, 2, FULL * P], U32, name="codes", bufs=4, align_bytes=64)
+            scales[unit] = work.tile([P, 2, FULL * P], U8, name="scales", bufs=4, align_bytes=64)
+            widths = [P * tiles_of[u] if known(u) else 0 for u in (unit, k)]
+            if widths == [FULL * P, FULL * P]:
+                nc.vector.quantize_mx(
+                    out=codes[unit][:].rearrange("p s c -> p (s c)").bitcast(FP8X4),
+                    scales=scales[unit][:].rearrange("p s c -> p (s c)"),
+                    in_=grouped[unit][:].rearrange("p s c -> p (s c)"),
+                )
+                return
+            for side in range(2):
+                if widths[side]:
+                    nc.vector.quantize_mx(
+                        out=codes[unit][:, side, : widths[side]].bitcast(FP8X4),
+                        scales=scales[unit][:, side, : widths[side]],
+                        in_=grouped[unit][:, side, : widths[side] * PACK],
+                    )
 
         def first_product(unit, t):
             if not known(unit):
                 return
-            chunk, block = units[unit]
-            columns = P * tiles_of(unit)
+            block = block_of[unit]
+            columns = P * tiles_of[unit]
             v_ps[unit, t] = psum.tile([P, FULL * P], F32, name="v_ps")
             nc.tensor.matmul_mx(
                 out=v_ps[unit, t][:, :columns],
                 lhsT=w1_codes[:, block, P * t : P * (t + 1)].bitcast(FP8X4),
                 lhsT_scale=w1_scale_sb[:, block, P * t : P * (t + 1)],
-                rhs=z_codes[unit][:, :columns].bitcast(FP8X4),
-                rhs_scale=z_scales[unit][:, :columns],
+                rhs=codes[unit][:, 0, :columns].bitcast(FP8X4),
+                rhs_scale=scales[unit][:, 0, :columns],
                 start=True,
                 stop=True,
             )
@@ -192,8 +208,8 @@ def tile_blockresmlp_mixerblock_pb_t_e_kernel(
         def exp_and_relu(unit, t):
             if not known(unit):
                 return
-            chunk, block = units[unit]
-            columns = P * tiles_of(unit)
+            block = block_of[unit]
+            columns = P * tiles_of[unit]
             if t == 0:
                 grown[unit] = work.tile([P, PACK * FULL * P], F32, name="grown")
                 kept[unit] = work.tile([P, PACK * FULL * P], F32, name="kept")
@@ -212,152 +228,121 @@ def tile_blockresmlp_mixerblock_pb_t_e_kernel(
         def join(unit):
             if not known(unit):
                 return
-            columns = P * tiles_of(unit)
-            h_grouped[unit] = work.tile([P, FULL * P, PACK], BF16, name="h_grouped", align_bytes=64)
+            columns = P * tiles_of[unit]
+            if not known(unit + 2):
+                new_grouped(unit + 2)
+            h_grouped = grouped[unit + 2][:, 1, :].rearrange("p (w t) -> p w t", t=PACK)
             if columns == FULL * P:
-                joined = h_grouped[unit][:].rearrange("p (a r) t -> p (r t) a", a=FULL)
+                joined = h_grouped.rearrange("p (a r) t -> p (r t) a", a=FULL)
                 sides = [v[:].rearrange("p (r t a) -> p (r t) a", t=PACK, a=FULL) for v in (grown[unit], kept[unit])]
             else:
-                joined = h_grouped[unit][:, :columns, :]
+                joined = h_grouped[:, :columns, :]
                 sides = [v[:, : columns * PACK].rearrange("p (t w) -> p w t", t=PACK) for v in (grown[unit], kept[unit])]
             nc.vector.scalar_tensor_tensor(
                 out=joined, in0=sides[0], scalar=-1.0, in1=sides[1], op0=ALU.add, op1=ALU.min
             )
 
-        def quantise_h(unit):
-            if not known(unit):
+        def second_product(unit, a):
+            if not known(unit) or a >= tiles_of[unit]:
                 return
-            columns = P * tiles_of(unit)
-            h_codes[unit] = work.tile([P, FULL * P], U32, name="h_codes", align_bytes=64)
-            h_scales[unit] = work.tile([P, FULL * P], U8, name="h_scales", align_bytes=64)
-            nc.vector.quantize_mx(
-                out=h_codes[unit][:, :columns].bitcast(FP8X4),
-                scales=h_scales[unit][:, :columns],
-                in_=h_grouped[unit][:, :columns, :].rearrange("p w t -> p (w t)"),
+            block = block_of[unit]
+            r_ps[unit, a] = psum.tile([P, WIDTH], F32, name="r_ps", bufs=3)
+            nc.tensor.matmul_mx(
+                out=r_ps[unit, a][:],
+                lhsT=codes[unit + 2][:, 1, P * a : P * (a + 1)].bitcast(FP8X4),
+                lhsT_scale=scales[unit + 2][:, 1, P * a : P * (a + 1)],
+                rhs=w2_codes[:, block, :].bitcast(FP8X4),
+                rhs_scale=w2_scale_sb[:, block, :],
+                start=True,
+                stop=True,
             )
 
-        def second_product(unit):
-            if not known(unit):
-                return
-            chunk, block = units[unit]
-            for a in range(PLAIN):
-                plain_ps[unit, a] = psum.tile([P, WIDTH], F32, name="r_ps", bufs=4)
-                nc.tensor.matmul_mx(
-                    out=plain_ps[unit, a][:],
-                    lhsT=h_codes[unit][:, P * a : P * (a + 1)].bitcast(FP8X4),
-                    lhsT_scale=h_scales[unit][:, P * a : P * (a + 1)],
-                    rhs=w2_codes[:, block, :].bitcast(FP8X4),
-                    rhs_scale=w2_scale_sb[:, block, :],
-                    start=True,
-                    stop=True,
-                )
-            if tiles_of(unit) < FULL:
-                return
-            for t in range(PACK):
-                if t % 2 == 0:
-                    turned_ps[unit, t // 2] = psum.tile([P, 2, TURNED * P], F32, name="r_ps", bufs=4)
-                nc.tensor.matmul_mx(
-                    out=turned_ps[unit, t // 2][:, t % 2, :],
-                    lhsT=w2_turned[:, block, P * t : P * (t + 1)].bitcast(FP8X4),
-                    lhsT_scale=w2_scale_turned[:, block, P * t : P * (t + 1)],
-                    rhs=h_codes[unit][:, PLAIN * P : FULL * P].bitcast(FP8X4),
-                    rhs_scale=h_scales[unit][:, PLAIN * P : FULL * P],
-                    start=True,
-                    stop=True,
-                )
+        def new_result(unit, a):
+            result[unit, a] = work.tile([P, WIDTH], F32, name="result", bufs=20)
+            return result[unit, a][:]
 
-        def add_b2(item, engine):
-            unit, a = plain_tiles[item]
-            chunk, block = units[unit]
-            columns = slice(WIDTH * block, WIDTH * (block + 1))
-            result[unit, a] = work.tile([P, WIDTH], F32, name="result", bufs=7 * PLAIN)
+        def add_base(item, engine):
+            unit, a = item
+            columns = columns_of(block_of[unit])
             engine.tensor_tensor(
-                out=result[unit, a][:], in0=x_sb[chunk][:, a, columns], in1=b2_all[:, columns], op=ALU.add
+                out=new_result(unit, a), in0=x_sb[:, first_tile[unit] + a, columns], in1=b2_all[:, columns], op=ALU.add
             )
 
-        def finish(unit):
-            if not known(unit):
+        def base_product(unit, a):
+            if base_by.get((unit, a)) != "scalar":
                 return
-            chunk, block = units[unit]
-            for a in range(PLAIN):
-                rows = result[unit, a][:]
-                nc.vector.tensor_tensor(out=rows, in0=plain_ps[unit, a][:], in1=rows, op=ALU.add)
-                store(unit, a, rows)
-            if tiles_of(unit) < FULL:
-                return
-            z_values = z_grouped[unit][:].rearrange("p (r a k) -> p k r a", a=FULL, k=PACK)
-            turned_sum[unit] = work.tile([P, PACK, TURNED, P], F32, name="turned_sum")
-            for t in range(PACK):
-                nc.vector.scalar_tensor_tensor(
-                    out=turned_sum[unit][:, t].rearrange("p a r -> p r a"),
-                    in0=turned_ps[unit, t // 2][:, t % 2, :].rearrange("p (a r) -> p r a", r=P),
-                    scalar=bias_column(b2_col, block, t),
-                    in1=z_values[:, t, :, PLAIN:],
-                    op0=ALU.add,
-                    op1=ALU.add,
-                )
+            columns = columns_of(block_of[unit])
+            base_ps[unit, a] = psum.tile([P, WIDTH], F32, name="base_ps", bufs=1)
+            nc.tensor.matmul(out=base_ps[unit, a][:], lhsT=first_row[:], rhs=b2_all[:, columns], start=True, stop=False)
+            nc.tensor.matmul(
+                out=base_ps[unit, a][:],
+                lhsT=ident_bf[:],
+                rhs=x_sb[:, first_tile[unit] + a, columns],
+                start=False,
+                stop=True,
+            )
 
-        def turn_back(unit):
-            if not known(unit):
-                return
-            for a in range(PLAIN, tiles_of(unit)):
-                rows_ps[unit, a] = psum.tile([P, PACK, P], F32, name="r_ps", bufs=4)
-                for t in range(PACK):
-                    nc.tensor.transpose(rows_ps[unit, a][:, t, :], turned_sum[unit][:, t, a - PLAIN, :], ident[:])
+        def copy_base(unit, a):
+            if base_by.get((unit, a)) == "scalar":
+                nc.scalar.copy(out=new_result(unit, a), in_=base_ps[unit, a][:])
 
-        def copy_and_store(unit):
-            if not known(unit):
+        def finish(unit, a):
+            if not known(unit) or a >= tiles_of[unit]:
                 return
-            for a in range(PLAIN, tiles_of(unit)):
-                rows = work.tile([P, P, PACK], F32, name="rows", bufs=3 * TURNED)
-                nc.scalar.copy(out=rows[:], in_=rows_ps[unit, a][:].rearrange("b t p -> b p t"))
-                store(unit, a, rows[:].rearrange("b p t -> b (p t)"))
+            rows = result[unit, a][:]
+            nc.vector.tensor_tensor(out=rows, in0=r_ps[unit, a][:], in1=rows, op=ALU.add)
+            nc.sync.dma_start(out=out_view[:, first_tile[unit] + a, columns_of(block_of[unit])], in_=rows)
 
-        added = EARLY_ADDS
-        for k in range(-3, len(units) + 2):
-            copy_and_store(k - 2)
-            second_product(k - 1)
+        added = 0
+        for k in range(-3, UNIT_COUNT + 1):
             if k == -2:
                 nc.vector.tensor_copy(out=b1_col[:], in_=b1_raw[:].rearrange("p g t -> p (g t)"))
-                reorder(w1_codes, w1_scale_sb, w1_raw, w1_scale_raw, 0)
-            if k < 0:
-                quantise_z(k + 2)
-            if k == -2:
-                reorder(w1_codes, w1_scale_sb, w1_raw, w1_scale_raw, 1)
+            if -2 <= k < 0:
+                reorder(w1_codes, w1_scale_sb, w1_raw, w1_scale_raw, k + 2)
+            if k == -1:
+                early = vector_bases[:4]
+            elif k == 0:
+                early = vector_bases[4:6]
+            elif k == 1:
+                early = vector_bases[6:]
+            else:
+                early = []
+            for item in early:
+                add_base(item, nc.vector)
 
+            base_product(k, 0)
+            second_product(k - 1, 0)
+            transpose_x(k + 3, 0)
             exp_and_relu(k + 1, 0)
             first_product(k + 1, 2)
-            transpose_x(k + 3, 0)
+            second_product(k - 1, 1)
             exp_and_relu(k + 1, 1)
             first_product(k + 1, 3)
+            second_product(k - 1, 2)
+            copy_base(k, 0)
+            base_product(k, 1)
             transpose_x(k + 3, 1)
 
-            if k == -1:
-                for item in range(EARLY_ADDS):
-                    add_b2(item, nc.vector)
             join(k)
             if k >= 0:
-                quantise_z(k + 2)
-            if k == 0:
-                nc.vector.tensor_copy(out=b2_col[:], in_=b2_raw[:].rearrange("p g t -> p (g t)"))
-            if 0 <= k < BLOCKS:
-                reorder(w2_turned, w2_scale_turned, w2_codes, w2_scale_sb, k)
-            finish(k - 1)
-            if known(k) and added < len(plain_tiles):
-                nc.gpsimd.tensor_copy(out=cue_sb[:, k : k + 1], in_=h_grouped[k][:, 0, :1])
-                due = min(added + (1 if k <= BLOCKS else 2), len(plain_tiles))
-                for item in range(added, due):
-                    add_b2(item, nc.gpsimd)
-                added = due
-            if k >= 0:
                 gather_z(k + 3, 0, nc.vector.tensor_copy)
-            quantise_h(k)
+            quantise(k)
+            if known(k):
+                nc.gpsimd.tensor_copy(out=cue_sb[:, k : k + 1], in_=codes[k + 2][:, 1, :1])
+                due = min(added + (1 if k < 3 else 2), len(gpsimd_bases))
+                for item in gpsimd_bases[added:due]:
+                    add_base(item, nc.gpsimd)
+                added = due
+            finish(k - 1, 0)
+            second_product(k - 1, 3)
+            for a in range(1, FULL):
+                finish(k - 1, a)
 
             exp_and_relu(k + 1, 2)
             first_product(k + 2, 0)
+            exp_and_relu(k + 1, 3)
+            first_product(k + 2, 1)
+            copy_base(k, 1)
             if k < 0:
                 gather_z(k + 3, 0, nc.scalar.copy)
-            exp_and_relu(k + 1, 3)
             gather_z(k + 3, 1, nc.scalar.copy)
-            turn_back(k - 1)
-            first_product(k + 2, 1)

@@ -36,13 +36,12 @@ def tile_blockresmlp_mixerblock_pb_t_e_kernel(
     tiles_of = [UNIT_TILES[u // BLOCKS] for u in range(UNIT_COUNT)]
     first_tile = [sum(UNIT_TILES[: u // BLOCKS]) for u in range(UNIT_COUNT)]
 
-    base_by = {}
-    for u in range(UNIT_COUNT):
-        scalar_tiles = 1 if u % 3 == 2 else 2
-        for a in range(tiles_of[u]):
-            base_by[u, a] = "vector" if u < 3 else "scalar" if a < scalar_tiles else "gpsimd"
-    vector_bases = [item for item in base_by if base_by[item] == "vector"]
-    gpsimd_bases = [item for item in base_by if base_by[item] == "gpsimd"]
+    base_by = ["VV", "SSVV", "SSGG", "SSGG", "SSGG", "SSGG", "GGGG", "SSGG", "GG"]
+
+    def chunk_tiles(letter):
+        return [(chunk, a) for chunk, by in enumerate(base_by) for a in range(len(by)) if by[a] == letter]
+
+    vector_bases, gpsimd_bases = chunk_tiles("V"), chunk_tiles("G")
 
     with ExitStack() as ctx:
         ctx.enter_context(tc.manual_schedule())
@@ -113,17 +112,15 @@ def tile_blockresmlp_mixerblock_pb_t_e_kernel(
         first_row = const.tile([P, P], BF16, name="first_row")
         nc.gpsimd.memset(first_row[:], 0.0)
         nc.gpsimd.memset(first_row[:1, :], 1.0)
-        cue_sb = const.tile([P, UNIT_COUNT], U32, name="cue_sb")
+        cue_sb = const.tile([P, UNIT_COUNT], BF16, name="cue_sb")
 
-        x_ps, grouped, codes, scales = {}, {}, {}, {}
+        x_ps, z_grouped, z_codes, z_scales = {}, {}, {}, {}
         v_ps, grown, kept = {}, {}, {}
+        h_grouped, h_codes, h_scales = {}, {}, {}
         base_ps, r_ps, result = {}, {}, {}
 
         def known(unit):
             return 0 <= unit < UNIT_COUNT
-
-        def new_grouped(unit):
-            grouped[unit] = work.tile([P, 2, FULL * P * PACK], BF16, name="grouped", bufs=3, align_bytes=64)
 
         def bias_column(columns, block, t):
             return columns[:, PACK * block + t : PACK * block + t + 1]
@@ -154,8 +151,8 @@ def tile_blockresmlp_mixerblock_pb_t_e_kernel(
             if not known(unit) or PAIR * half >= tiles_of[unit]:
                 return
             if half == 0:
-                new_grouped(unit)
-            z_words = grouped[unit][:, 0, :].bitcast(F32)
+                z_grouped[unit] = work.tile([P, FULL * P * PACK], BF16, name="z_grouped", bufs=3, align_bytes=64)
+            z_words = z_grouped[unit][:].bitcast(F32)
             if tiles_of[unit] == FULL:
                 copy(
                     out=z_words.rearrange("p (r a u) -> p r a u", a=FULL, u=2)[:, :, PAIR * half : PAIR * (half + 1), :],
@@ -167,27 +164,23 @@ def tile_blockresmlp_mixerblock_pb_t_e_kernel(
                     in_=x_ps[unit, half][:].rearrange("p a u r -> p a r u"),
                 )
 
-        def quantise(k):
-            if not known(k) and not known(k + 2):
-                return
-            unit = k + 2
-            codes[unit] = work.tile([P, 2, FULL * P], U32, name="codes", bufs=4, align_bytes=64)
-            scales[unit] = work.tile([P, 2, FULL * P], U8, name="scales", bufs=4, align_bytes=64)
-            widths = [P * tiles_of[u] if known(u) else 0 for u in (unit, k)]
-            if widths == [FULL * P, FULL * P]:
-                nc.vector.quantize_mx(
-                    out=codes[unit][:].rearrange("p s c -> p (s c)").bitcast(FP8X4),
-                    scales=scales[unit][:].rearrange("p s c -> p (s c)"),
-                    in_=grouped[unit][:].rearrange("p s c -> p (s c)"),
-                )
-                return
-            for side in range(2):
-                if widths[side]:
-                    nc.vector.quantize_mx(
-                        out=codes[unit][:, side, : widths[side]].bitcast(FP8X4),
-                        scales=scales[unit][:, side, : widths[side]],
-                        in_=grouped[unit][:, side, : widths[side] * PACK],
-                    )
+        def quantise(unit, codes, scales, grouped, label):
+            columns = P * tiles_of[unit]
+            codes[unit] = work.tile([P, FULL * P], U32, name=label + "_codes", bufs=3, align_bytes=64)
+            scales[unit] = work.tile([P, FULL * P], U8, name=label + "_scales", bufs=3, align_bytes=64)
+            nc.vector.quantize_mx(
+                out=codes[unit][:, :columns].bitcast(FP8X4),
+                scales=scales[unit][:, :columns],
+                in_=grouped[unit][:, : columns * PACK],
+            )
+
+        def quantise_z(unit):
+            if known(unit):
+                quantise(unit, z_codes, z_scales, z_grouped, "z")
+
+        def quantise_h(unit):
+            if known(unit):
+                quantise(unit, h_codes, h_scales, h_grouped, "h")
 
         def first_product(unit, t):
             if not known(unit):
@@ -199,8 +192,8 @@ def tile_blockresmlp_mixerblock_pb_t_e_kernel(
                 out=v_ps[unit, t][:, :columns],
                 lhsT=w1_codes[:, block, P * t : P * (t + 1)].bitcast(FP8X4),
                 lhsT_scale=w1_scale_sb[:, block, P * t : P * (t + 1)],
-                rhs=codes[unit][:, 0, :columns].bitcast(FP8X4),
-                rhs_scale=scales[unit][:, 0, :columns],
+                rhs=z_codes[unit][:, :columns].bitcast(FP8X4),
+                rhs_scale=z_scales[unit][:, :columns],
                 start=True,
                 stop=True,
             )
@@ -229,14 +222,12 @@ def tile_blockresmlp_mixerblock_pb_t_e_kernel(
             if not known(unit):
                 return
             columns = P * tiles_of[unit]
-            if not known(unit + 2):
-                new_grouped(unit + 2)
-            h_grouped = grouped[unit + 2][:, 1, :].rearrange("p (w t) -> p w t", t=PACK)
+            h_grouped[unit] = work.tile([P, FULL * P * PACK], BF16, name="h_grouped", align_bytes=64)
             if columns == FULL * P:
-                joined = h_grouped.rearrange("p (a r) t -> p (r t) a", a=FULL)
+                joined = h_grouped[unit][:].rearrange("p (a r t) -> p (r t) a", a=FULL, t=PACK)
                 sides = [v[:].rearrange("p (r t a) -> p (r t) a", t=PACK, a=FULL) for v in (grown[unit], kept[unit])]
             else:
-                joined = h_grouped[:, :columns, :]
+                joined = h_grouped[unit][:, : columns * PACK].rearrange("p (w t) -> p w t", t=PACK)
                 sides = [v[:, : columns * PACK].rearrange("p (t w) -> p w t", t=PACK) for v in (grown[unit], kept[unit])]
             nc.vector.scalar_tensor_tensor(
                 out=joined, in0=sides[0], scalar=-1.0, in1=sides[1], op0=ALU.add, op1=ALU.min
@@ -249,27 +240,28 @@ def tile_blockresmlp_mixerblock_pb_t_e_kernel(
             r_ps[unit, a] = psum.tile([P, WIDTH], F32, name="r_ps", bufs=3)
             nc.tensor.matmul_mx(
                 out=r_ps[unit, a][:],
-                lhsT=codes[unit + 2][:, 1, P * a : P * (a + 1)].bitcast(FP8X4),
-                lhsT_scale=scales[unit + 2][:, 1, P * a : P * (a + 1)],
+                lhsT=h_codes[unit][:, P * a : P * (a + 1)].bitcast(FP8X4),
+                lhsT_scale=h_scales[unit][:, P * a : P * (a + 1)],
                 rhs=w2_codes[:, block, :].bitcast(FP8X4),
                 rhs_scale=w2_scale_sb[:, block, :],
                 start=True,
                 stop=True,
             )
 
-        def new_result(unit, a):
-            result[unit, a] = work.tile([P, WIDTH], F32, name="result", bufs=20)
-            return result[unit, a][:]
-
         def add_base(item, engine):
-            unit, a = item
-            columns = columns_of(block_of[unit])
+            chunk, a = item
+            both = work.tile([P, BLOCKS * WIDTH], F32, name="both", bufs=9)
             engine.tensor_tensor(
-                out=new_result(unit, a), in0=x_sb[:, first_tile[unit] + a, columns], in1=b2_all[:, columns], op=ALU.add
+                out=both[:], in0=x_sb[:, first_tile[BLOCKS * chunk] + a, :], in1=b2_all[:], op=ALU.add
             )
+            for block in range(BLOCKS):
+                result[BLOCKS * chunk + block, a] = both[:, columns_of(block)]
+
+        def scalar_base(unit, a):
+            return known(unit) and base_by[unit // BLOCKS][a] == "S"
 
         def base_product(unit, a):
-            if base_by.get((unit, a)) != "scalar":
+            if not scalar_base(unit, a):
                 return
             columns = columns_of(block_of[unit])
             base_ps[unit, a] = psum.tile([P, WIDTH], F32, name="base_ps", bufs=1)
@@ -283,60 +275,55 @@ def tile_blockresmlp_mixerblock_pb_t_e_kernel(
             )
 
         def copy_base(unit, a):
-            if base_by.get((unit, a)) == "scalar":
-                nc.scalar.copy(out=new_result(unit, a), in_=base_ps[unit, a][:])
+            if scalar_base(unit, a):
+                rows = work.tile([P, WIDTH], F32, name="rows", bufs=10)
+                nc.scalar.copy(out=rows[:], in_=base_ps[unit, a][:])
+                result[unit, a] = rows[:]
 
         def finish(unit, a):
             if not known(unit) or a >= tiles_of[unit]:
                 return
-            rows = result[unit, a][:]
+            rows = result[unit, a]
             nc.vector.tensor_tensor(out=rows, in0=r_ps[unit, a][:], in1=rows, op=ALU.add)
             nc.sync.dma_start(out=out_view[:, first_tile[unit] + a, columns_of(block_of[unit])], in_=rows)
 
-        added = 0
         for k in range(-3, UNIT_COUNT + 1):
-            if k == -2:
-                nc.vector.tensor_copy(out=b1_col[:], in_=b1_raw[:].rearrange("p g t -> p (g t)"))
             if -2 <= k < 0:
                 reorder(w1_codes, w1_scale_sb, w1_raw, w1_scale_raw, k + 2)
-            if k == -1:
-                early = vector_bases[:4]
-            elif k == 0:
-                early = vector_bases[4:6]
-            elif k == 1:
-                early = vector_bases[6:]
-            else:
-                early = []
-            for item in early:
+            if k == -2:
+                nc.vector.tensor_copy(out=b1_col[:], in_=b1_raw[:].rearrange("p g t -> p (g t)"))
+            if k < 0:
+                quantise_z(k + 2)
+            for item in {-1: vector_bases[:2], 0: vector_bases[2:3], 1: vector_bases[3:]}.get(k, []):
                 add_base(item, nc.vector)
 
             base_product(k, 0)
             second_product(k - 1, 0)
             transpose_x(k + 3, 0)
+            second_product(k - 1, 1)
             exp_and_relu(k + 1, 0)
             first_product(k + 1, 2)
-            second_product(k - 1, 1)
+            second_product(k - 1, 2)
             exp_and_relu(k + 1, 1)
             first_product(k + 1, 3)
-            second_product(k - 1, 2)
             copy_base(k, 0)
             base_product(k, 1)
-            transpose_x(k + 3, 1)
 
             join(k)
             if k >= 0:
-                gather_z(k + 3, 0, nc.vector.tensor_copy)
-            quantise(k)
-            if known(k):
-                nc.gpsimd.tensor_copy(out=cue_sb[:, k : k + 1], in_=codes[k + 2][:, 1, :1])
-                due = min(added + (1 if k < 3 else 2), len(gpsimd_bases))
-                for item in gpsimd_bases[added:due]:
-                    add_base(item, nc.gpsimd)
-                added = due
+                quantise_z(k + 2)
+            if 1 <= k <= len(gpsimd_bases):
+                nc.gpsimd.tensor_copy(out=cue_sb[:, k : k + 1], in_=h_grouped[k][:, :1])
+                add_base(gpsimd_bases[k - 1], nc.gpsimd)
             finish(k - 1, 0)
             second_product(k - 1, 3)
-            for a in range(1, FULL):
-                finish(k - 1, a)
+            transpose_x(k + 3, 1)
+            finish(k - 1, 1)
+            if k >= 0:
+                gather_z(k + 3, 0, nc.vector.tensor_copy)
+            finish(k - 1, 2)
+            finish(k - 1, 3)
+            quantise_h(k)
 
             exp_and_relu(k + 1, 2)
             first_product(k + 2, 0)

@@ -36,7 +36,7 @@ def tile_blockresmlp_mixerblock_pb_t_e_kernel(
     tiles_of = [UNIT_TILES[u // BLOCKS] for u in range(UNIT_COUNT)]
     first_tile = [sum(UNIT_TILES[: u // BLOCKS]) for u in range(UNIT_COUNT)]
 
-    base_by = ["VV", "SSVV", "SSGG", "SSGG", "SSGG", "SSGG", "GGGG", "SSGG", "GG"]
+    base_by = ["VV", "SSVV", "SSGG", "SSGG", "SSGG", "SSGG", "SGGG", "SSGG", "SS"]
 
     def chunk_tiles(letter):
         return [(chunk, a) for chunk, by in enumerate(base_by) for a in range(len(by)) if by[a] == letter]
@@ -109,10 +109,8 @@ def tile_blockresmlp_mixerblock_pb_t_e_kernel(
         make_identity(nc, ident[:])
         ident_bf = const.tile([P, P], BF16, name="ident_bf")
         make_identity(nc, ident_bf[:])
-        first_row = const.tile([P, P], BF16, name="first_row")
-        nc.gpsimd.memset(first_row[:], 0.0)
-        nc.gpsimd.memset(first_row[:1, :], 1.0)
-        cue_sb = const.tile([P, UNIT_COUNT], BF16, name="cue_sb")
+        b2_turned = const.tile([P, BLOCKS, PACK, P], F32, name="b2_turned")
+        cue_sb = const.tile([P, UNIT_COUNT], U32, name="cue_sb")
 
         x_ps, z_grouped, z_codes, z_scales = {}, {}, {}, {}
         v_ps, grown, kept = {}, {}, {}
@@ -147,11 +145,12 @@ def tile_blockresmlp_mixerblock_pb_t_e_kernel(
                         x_ps[unit, half][:, a, u, :], x_words[:, WORDS * block + u : WORDS * (block + 1) : 2], ident[:]
                     )
 
-        def gather_z(unit, half, copy):
+        def gather_z(unit, half):
             if not known(unit) or PAIR * half >= tiles_of[unit]:
                 return
             if half == 0:
                 z_grouped[unit] = work.tile([P, FULL * P * PACK], BF16, name="z_grouped", bufs=3, align_bytes=64)
+            copy = nc.vector.tensor_copy if half == 0 and tiles_of[unit] == FULL else nc.scalar.copy
             z_words = z_grouped[unit][:].bitcast(F32)
             if tiles_of[unit] == FULL:
                 copy(
@@ -265,14 +264,29 @@ def tile_blockresmlp_mixerblock_pb_t_e_kernel(
                 return
             columns = columns_of(block_of[unit])
             base_ps[unit, a] = psum.tile([P, WIDTH], F32, name="base_ps", bufs=1)
-            nc.tensor.matmul(out=base_ps[unit, a][:], lhsT=first_row[:], rhs=b2_all[:, columns], start=True, stop=False)
             nc.tensor.matmul(
                 out=base_ps[unit, a][:],
                 lhsT=ident_bf[:],
                 rhs=x_sb[:, first_tile[unit] + a, columns],
-                start=False,
-                stop=True,
+                start=True,
+                stop=False,
             )
+            for t in range(PACK):
+                nc.tensor.matmul(
+                    out=base_ps[unit, a][:, P * t : P * (t + 1)],
+                    lhsT=b2_turned[:, block_of[unit], t, :],
+                    rhs=ident[:],
+                    is_transpose=True,
+                    start=False,
+                    stop=t == PACK - 1,
+                )
+
+        def turn_b2(block):
+            turned_ps = psum.tile([P, PACK, P], BF16, name="base_ps", bufs=1)
+            for t in range(PACK):
+                start = WIDTH * block + P * t
+                nc.tensor.transpose(turned_ps[:, t, :], b2_all[:, start : start + P], ident_bf[:])
+            nc.scalar.copy(out=b2_turned[:, block, :, :], in_=turned_ps[:])
 
         def copy_base(unit, a):
             if scalar_base(unit, a):
@@ -288,48 +302,44 @@ def tile_blockresmlp_mixerblock_pb_t_e_kernel(
             nc.sync.dma_start(out=out_view[:, first_tile[unit] + a, columns_of(block_of[unit])], in_=rows)
 
         for k in range(-3, UNIT_COUNT + 1):
+            for item in {-1: vector_bases[:2], 1: vector_bases[2:]}.get(k, []):
+                add_base(item, nc.vector)
             if -2 <= k < 0:
                 reorder(w1_codes, w1_scale_sb, w1_raw, w1_scale_raw, k + 2)
             if k == -2:
                 nc.vector.tensor_copy(out=b1_col[:], in_=b1_raw[:].rearrange("p g t -> p (g t)"))
-            if k < 0:
-                quantise_z(k + 2)
-            for item in {-1: vector_bases[:2], 0: vector_bases[2:3], 1: vector_bases[3:]}.get(k, []):
-                add_base(item, nc.vector)
 
-            base_product(k, 0)
             second_product(k - 1, 0)
+            base_product(k, 0)
             transpose_x(k + 3, 0)
-            second_product(k - 1, 1)
             exp_and_relu(k + 1, 0)
             first_product(k + 1, 2)
+            second_product(k - 1, 1)
             second_product(k - 1, 2)
             exp_and_relu(k + 1, 1)
             first_product(k + 1, 3)
             copy_base(k, 0)
             base_product(k, 1)
+            transpose_x(k + 3, 1)
 
             join(k)
-            if k >= 0:
-                quantise_z(k + 2)
-            if 1 <= k <= len(gpsimd_bases):
-                nc.gpsimd.tensor_copy(out=cue_sb[:, k : k + 1], in_=h_grouped[k][:, :1])
-                add_base(gpsimd_bases[k - 1], nc.gpsimd)
-            finish(k - 1, 0)
-            second_product(k - 1, 3)
-            transpose_x(k + 3, 1)
-            finish(k - 1, 1)
-            if k >= 0:
-                gather_z(k + 3, 0, nc.vector.tensor_copy)
-            finish(k - 1, 2)
-            finish(k - 1, 3)
+            quantise_z(k + 2)
             quantise_h(k)
-
+            if 2 <= k < 2 + len(gpsimd_bases):
+                nc.gpsimd.tensor_copy(out=cue_sb[:, k : k + 1], in_=h_codes[k][:, :1])
+                add_base(gpsimd_bases[k - 2], nc.gpsimd)
+            finish(k - 1, 0)
+            finish(k - 1, 1)
+            gather_z(k + 3, 0)
             exp_and_relu(k + 1, 2)
             first_product(k + 2, 0)
+            second_product(k - 1, 3)
+            finish(k - 1, 2)
+            finish(k - 1, 3)
             exp_and_relu(k + 1, 3)
             first_product(k + 2, 1)
             copy_base(k, 1)
-            if k < 0:
-                gather_z(k + 3, 0, nc.scalar.copy)
-            gather_z(k + 3, 1, nc.scalar.copy)
+            gather_z(k + 3, 1)
+            if k == -3:
+                for block in range(BLOCKS):
+                    turn_b2(block)

from contextlib import ExitStack

import concourse.mybir as mybir
from concourse.masks import make_identity

F32 = mybir.dt.float32
BF16 = mybir.dt.bfloat16
I32 = mybir.dt.int32
U32 = mybir.dt.uint32
U8 = mybir.dt.uint8
FP8X4 = mybir.dt.float8_e4m3fn_x4
ALU = mybir.AluOpType
ACT = mybir.ActivationFunctionType

P = 128
QUADRANT = 32
PACK = 4
BATCH = 4096
BLOCKS = 2
WIDTH = 512
WORDS = WIDTH // 2
TILES = BATCH // P
FULL = 4
PAIR = 2
UNIT_TILES = [2, 4, 4, 4, 4, 4, 4, 4, 2]
UNIT_COUNT = BLOCKS * len(UNIT_TILES)

FLOPS = 2 * BATCH * WIDTH * WIDTH * BLOCKS * 2


def tile_blockresmlp_mixerblock_pb_t_e_kernel(
    tc, x_blocks, w1_words, w1_scales, b1, w2_words, w2_scales, b2, out
):
    nc = tc.nc
    block_of = [u % BLOCKS for u in range(UNIT_COUNT)]
    tiles_of = [UNIT_TILES[u // BLOCKS] for u in range(UNIT_COUNT)]
    first_tile = [sum(UNIT_TILES[: u // BLOCKS]) for u in range(UNIT_COUNT)]

    base_by = ["VV", "SSVV", "SSGG", "SSGG", "SSGG", "SSGG", "SGGG", "SSGG", "SS"]

    def chunk_tiles(letter):
        return [(chunk, a) for chunk, by in enumerate(base_by) for a in range(len(by)) if by[a] == letter]

    vector_bases, gpsimd_bases = chunk_tiles("V"), chunk_tiles("G")

    with ExitStack() as ctx:
        ctx.enter_context(tc.manual_schedule())
        const = ctx.enter_context(tc.tile_pool(name="const", bufs=1))
        work = ctx.enter_context(tc.tile_pool(name="work", bufs=2))
        psum = ctx.enter_context(tc.psum_pool(name="psum", bufs=2))

        x_view = x_blocks.rearrange("(p i) c -> p i c", i=TILES)
        out_view = out.rearrange("(p i) c -> p i c", i=TILES)

        x_sb = const.tile([P, TILES, BLOCKS * WIDTH], BF16, name="x_sb")

        def columns_of(block):
            return slice(WIDTH * block, WIDTH * (block + 1))

        def load_x(start, stop, columns):
            nc.sync.dma_start(out=x_sb[:, start:stop, columns], in_=x_view[:, start:stop, columns])

        def weight_tiles(label):
            codes = const.tile([P, BLOCKS, WIDTH], U32, name=label + "_codes", align_bytes=64)
            scale_sb = const.tile([P, BLOCKS, WIDTH], U8, name=label + "_scale_sb", align_bytes=64)
            return codes, scale_sb

        def load_codes(codes, words, block):
            nc.sync.dma_start(
                out=codes[:, block, :].bitcast(I32), in_=words[block].rearrange("p n t -> p (n t)").bitcast(I32)
            )

        def load_scales(scale_sb, scales):
            nc.vector.memset(scale_sb[:].rearrange("p g n -> p (g n)").bitcast(I32), 0)
            for quadrant in range(P // QUADRANT):
                nc.sync.dma_start(
                    out=scale_sb[QUADRANT * quadrant : QUADRANT * quadrant + PACK].bitcast(I32),
                    in_=scales[:, PACK * quadrant : PACK * (quadrant + 1), :].rearrange("g r n -> r g n").bitcast(I32),
                )

        w1_raw, w1_scale_raw = weight_tiles("w1_raw")
        w1_codes, w1_scale_sb = weight_tiles("w1")
        w2_codes, w2_scale_sb = weight_tiles("w2")

        b1_raw = const.tile([P, BLOCKS, PACK], BF16, name="b1_raw")
        nc.scalar.dma_start(out=b1_raw[:], in_=b1.rearrange("g o (p t) -> p (g o) t", t=PACK))
        b1_col = const.tile([P, BLOCKS * PACK], F32, name="b1_col")
        b2_all = const.tile([P, BLOCKS * WIDTH], BF16, name="b2_all")
        nc.scalar.dma_start(out=b2_all[:], in_=b2.rearrange("g o d -> (g o d)").partition_broadcast(P))

        load_x(0, 2, columns_of(0))
        load_codes(w1_raw, w1_words, 0)
        load_scales(w1_scale_raw, w1_scales)
        load_x(0, 2, columns_of(1))
        load_codes(w1_raw, w1_words, 1)
        load_x(2, 6, columns_of(0))
        load_x(2, 6, columns_of(1))
        for block in range(BLOCKS):
            load_codes(w2_codes, w2_words, block)
        load_scales(w2_scale_sb, w2_scales)
        for start in range(6, TILES, FULL):
            load_x(start, min(start + FULL, TILES), slice(0, BLOCKS * WIDTH))

        warm = const.tile([P, 1], F32, name="warm")
        nc.gpsimd.memset(warm[:], 0.0)
        warmed = const.tile([P, 1], F32, name="warmed")
        nc.scalar.activation(out=warmed[:], in_=warm[:], func=ACT.Exp)
        ident = const.tile([P, P], F32, name="ident")
        make_identity(nc, ident[:])
        ident_bf = const.tile([P, P], BF16, name="ident_bf")
        make_identity(nc, ident_bf[:])
        b2_turned = const.tile([P, BLOCKS, PACK, P], F32, name="b2_turned")
        cue_sb = const.tile([P, UNIT_COUNT], U32, name="cue_sb")

        x_ps, z_grouped, z_codes, z_scales = {}, {}, {}, {}
        v_ps, grown, kept = {}, {}, {}
        h_grouped, h_codes, h_scales = {}, {}, {}
        base_ps, r_ps, result = {}, {}, {}

        def known(unit):
            return 0 <= unit < UNIT_COUNT

        def bias_column(columns, block, t):
            return columns[:, PACK * block + t : PACK * block + t + 1]

        def reorder(codes_to, scale_to, codes_from, scale_from, block):
            nc.vector.tensor_copy(
                out=codes_to[:, block, :].bitcast(I32).rearrange("p (t m) -> p t m", t=PACK),
                in_=codes_from[:, block, :].bitcast(I32).rearrange("p (m t) -> p t m", t=PACK),
            )
            nc.vector.tensor_copy(
                out=scale_to[:, block, :].rearrange("p (t m) -> p t m", t=PACK),
                in_=scale_from[:, block, :].rearrange("p (m t) -> p t m", t=PACK),
            )

        def transpose_x(unit, half):
            if not known(unit) or PAIR * half >= tiles_of[unit]:
                return
            block = block_of[unit]
            x_ps[unit, half] = psum.tile([P, PAIR, 2, P], F32, name="x_ps")
            for a in range(PAIR):
                x_words = x_sb[:, first_tile[unit] + PAIR * half + a, :].bitcast(F32)
                for u in range(2):
                    nc.tensor.transpose(
                        x_ps[unit, half][:, a, u, :], x_words[:, WORDS * block + u : WORDS * (block + 1) : 2], ident[:]
                    )

        def gather_z(unit, half):
            if not known(unit) or PAIR * half >= tiles_of[unit]:
                return
            if half == 0:
                z_grouped[unit] = work.tile([P, FULL * P * PACK], BF16, name="z_grouped", bufs=3, align_bytes=64)
            copy = nc.vector.tensor_copy if half == 0 and tiles_of[unit] == FULL else nc.scalar.copy
            z_words = z_grouped[unit][:].bitcast(F32)
            if tiles_of[unit] == FULL:
                copy(
                    out=z_words.rearrange("p (r a u) -> p r a u", a=FULL, u=2)[:, :, PAIR * half : PAIR * (half + 1), :],
                    in_=x_ps[unit, half][:].rearrange("p a u r -> p r a u"),
                )
            else:
                copy(
                    out=z_words.rearrange("p (a r u) -> p a r u", r=P, u=2)[:, :PAIR],
                    in_=x_ps[unit, half][:].rearrange("p a u r -> p a r u"),
                )

        def quantise(unit, codes, scales, grouped, label):
            columns = P * tiles_of[unit]
            codes[unit] = work.tile([P, FULL * P], U32, name=label + "_codes", bufs=3, align_bytes=64)
            scales[unit] = work.tile([P, FULL * P], U8, name=label + "_scales", bufs=3, align_bytes=64)
            nc.vector.quantize_mx(
                out=codes[unit][:, :columns].bitcast(FP8X4),
                scales=scales[unit][:, :columns],
                in_=grouped[unit][:, : columns * PACK],
            )

        def quantise_z(unit):
            if known(unit):
                quantise(unit, z_codes, z_scales, z_grouped, "z")

        def quantise_h(unit):
            if known(unit):
                quantise(unit, h_codes, h_scales, h_grouped, "h")

        def first_product(unit, t):
            if not known(unit):
                return
            block = block_of[unit]
            columns = P * tiles_of[unit]
            v_ps[unit, t] = psum.tile([P, FULL * P], F32, name="v_ps")
            nc.tensor.matmul_mx(
                out=v_ps[unit, t][:, :columns],
                lhsT=w1_codes[:, block, P * t : P * (t + 1)].bitcast(FP8X4),
                lhsT_scale=w1_scale_sb[:, block, P * t : P * (t + 1)],
                rhs=z_codes[unit][:, :columns].bitcast(FP8X4),
                rhs_scale=z_scales[unit][:, :columns],
                start=True,
                stop=True,
            )

        def exp_and_relu(unit, t):
            if not known(unit):
                return
            block = block_of[unit]
            columns = P * tiles_of[unit]
            if t == 0:
                grown[unit] = work.tile([P, PACK * FULL * P], F32, name="grown")
                kept[unit] = work.tile([P, PACK * FULL * P], F32, name="kept")
            source = v_ps[unit, t][:, :columns]
            if columns == FULL * P:
                source = source.rearrange("p (r a) -> p r a", a=FULL)
            for values, func in ((grown[unit], ACT.Exp), (kept[unit], ACT.Relu)):
                if columns == FULL * P:
                    quarter = values[:].rearrange("p (r t a) -> p r t a", t=PACK, a=FULL)[:, :, t, :]
                else:
                    quarter = values[:, columns * t : columns * (t + 1)]
                nc.scalar.activation(
                    out=quarter, in_=source, func=func, bias=bias_column(b1_col, block, t), scale=1.0
                )

        def join(unit):
            if not known(unit):
                return
            columns = P * tiles_of[unit]
            h_grouped[unit] = work.tile([P, FULL * P * PACK], BF16, name="h_grouped", align_bytes=64)
            if columns == FULL * P:
                joined = h_grouped[unit][:].rearrange("p (a r t) -> p (r t) a", a=FULL, t=PACK)
                sides = [v[:].rearrange("p (r t a) -> p (r t) a", t=PACK, a=FULL) for v in (grown[unit], kept[unit])]
            else:
                joined = h_grouped[unit][:, : columns * PACK].rearrange("p (w t) -> p w t", t=PACK)
                sides = [v[:, : columns * PACK].rearrange("p (t w) -> p w t", t=PACK) for v in (grown[unit], kept[unit])]
            nc.vector.scalar_tensor_tensor(
                out=joined, in0=sides[0], scalar=-1.0, in1=sides[1], op0=ALU.add, op1=ALU.min
            )

        def second_product(unit, a):
            if not known(unit) or a >= tiles_of[unit]:
                return
            block = block_of[unit]
            r_ps[unit, a] = psum.tile([P, WIDTH], F32, name="r_ps", bufs=3)
            nc.tensor.matmul_mx(
                out=r_ps[unit, a][:],
                lhsT=h_codes[unit][:, P * a : P * (a + 1)].bitcast(FP8X4),
                lhsT_scale=h_scales[unit][:, P * a : P * (a + 1)],
                rhs=w2_codes[:, block, :].bitcast(FP8X4),
                rhs_scale=w2_scale_sb[:, block, :],
                start=True,
                stop=True,
            )

        def add_base(item, engine):
            chunk, a = item
            both = work.tile([P, BLOCKS * WIDTH], F32, name="both", bufs=9)
            engine.tensor_tensor(
                out=both[:], in0=x_sb[:, first_tile[BLOCKS * chunk] + a, :], in1=b2_all[:], op=ALU.add
            )
            for block in range(BLOCKS):
                result[BLOCKS * chunk + block, a] = both[:, columns_of(block)]

        def scalar_base(unit, a):
            return known(unit) and base_by[unit // BLOCKS][a] == "S"

        def base_product(unit, a):
            if not scalar_base(unit, a):
                return
            columns = columns_of(block_of[unit])
            base_ps[unit, a] = psum.tile([P, WIDTH], F32, name="base_ps", bufs=1)
            nc.tensor.matmul(
                out=base_ps[unit, a][:],
                lhsT=ident_bf[:],
                rhs=x_sb[:, first_tile[unit] + a, columns],
                start=True,
                stop=False,
            )
            for t in range(PACK):
                nc.tensor.matmul(
                    out=base_ps[unit, a][:, P * t : P * (t + 1)],
                    lhsT=b2_turned[:, block_of[unit], t, :],
                    rhs=ident[:],
                    is_transpose=True,
                    start=False,
                    stop=t == PACK - 1,
                )

        def turn_b2(block):
            turned_ps = psum.tile([P, PACK, P], BF16, name="base_ps", bufs=1)
            for t in range(PACK):
                start = WIDTH * block + P * t
                nc.tensor.transpose(turned_ps[:, t, :], b2_all[:, start : start + P], ident_bf[:])
            nc.scalar.copy(out=b2_turned[:, block, :, :], in_=turned_ps[:])

        def copy_base(unit, a):
            if scalar_base(unit, a):
                rows = work.tile([P, WIDTH], F32, name="rows", bufs=10)
                nc.scalar.copy(out=rows[:], in_=base_ps[unit, a][:])
                result[unit, a] = rows[:]

        def finish(unit, a):
            if not known(unit) or a >= tiles_of[unit]:
                return
            rows = result[unit, a]
            nc.vector.tensor_tensor(out=rows, in0=r_ps[unit, a][:], in1=rows, op=ALU.add)
            nc.sync.dma_start(out=out_view[:, first_tile[unit] + a, columns_of(block_of[unit])], in_=rows)

        for k in range(-3, UNIT_COUNT + 1):
            for item in {-1: vector_bases[:2], 1: vector_bases[2:]}.get(k, []):
                add_base(item, nc.vector)
            if -2 <= k < 0:
                reorder(w1_codes, w1_scale_sb, w1_raw, w1_scale_raw, k + 2)
            if k == -2:
                nc.vector.tensor_copy(out=b1_col[:], in_=b1_raw[:].rearrange("p g t -> p (g t)"))

            second_product(k - 1, 0)
            base_product(k, 0)
            transpose_x(k + 3, 0)
            exp_and_relu(k + 1, 0)
            first_product(k + 1, 2)
            second_product(k - 1, 1)
            second_product(k - 1, 2)
            exp_and_relu(k + 1, 1)
            first_product(k + 1, 3)
            copy_base(k, 0)
            base_product(k, 1)
            transpose_x(k + 3, 1)

            join(k)
            quantise_z(k + 2)
            quantise_h(k)
            if 2 <= k < 2 + len(gpsimd_bases):
                nc.gpsimd.tensor_copy(out=cue_sb[:, k : k + 1], in_=h_codes[k][:, :1])
                add_base(gpsimd_bases[k - 2], nc.gpsimd)
            finish(k - 1, 0)
            finish(k - 1, 1)
            gather_z(k + 3, 0)
            exp_and_relu(k + 1, 2)
            first_product(k + 2, 0)
            second_product(k - 1, 3)
            finish(k - 1, 2)
            finish(k - 1, 3)
            exp_and_relu(k + 1, 3)
            first_product(k + 2, 1)
            copy_base(k, 1)
            gather_z(k + 3, 1)
            if k == -3:
                for block in range(BLOCKS):
                    turn_b2(block)
